import numpy as np
import ml_dtypes


def mxq(x, axis, fmt="e4m3"):
    dtype, down = {"e4m3": (ml_dtypes.float8_e4m3fn, 7), "e5m2": (ml_dtypes.float8_e5m2, 14)}[fmt]
    v = np.moveaxis(np.asarray(x, np.float32).astype(ml_dtypes.bfloat16).astype(np.float64), axis, -1)
    blocks = v.reshape(v.shape[:-1] + (-1, 32))
    amax = np.abs(blocks).max(-1, keepdims=True)
    byte = np.maximum(np.where(amax > 0, np.frexp(amax)[1] - 1 + 127, 0) - down, 1)
    scale = np.exp2(byte - 127.0)
    codes = (blocks / scale).astype(np.float32).astype(dtype).astype(np.float64)
    return np.moveaxis((codes * scale).reshape(v.shape), -1, axis)


WIDE = False


def mx_kscale(k):
    if not WIDE:
        return np.ones(k)
    levels = np.array([10, -10, 5, -5, 0])
    a = np.random.permutation(np.resize(levels, k // 512 * 4)).reshape(k // 512, 4)
    idx = np.arange(k)
    return np.exp2(a[idx // 512, idx % 128 // 32])


BF16 = ml_dtypes.bfloat16


def bf(x):
    return np.asarray(x, np.float32).astype(BF16)


def f64(x):
    return np.asarray(x).astype(np.float64)


B, S, DIM, H, NOPE, ROPE_SP, V_SP, KV_RANK = 4, 1024, 1024, 2, 64, 128, 64, 512
C = 1.0
EPS = 1e-6


def lift(sp):
    return np.concatenate([np.sqrt((sp * sp).sum(-1, keepdims=True) + C), sp], -1)


def rope(u, cos, sin):
    u1, u2 = u[..., 0::2], u[..., 1::2]
    cos, sin = cos[None, :, None, :], sin[None, :, None, :]
    return np.stack([u1 * cos - u2 * sin, u1 * sin + u2 * cos], -1).reshape(u.shape)


def setup_inputs():
    s = mx_kscale(DIM)
    inv = 1.0 / (10000.0 ** (np.arange(0, ROPE_SP, 2) / ROPE_SP))
    ang = np.arange(S)[:, None] * inv[None, :]
    return {"x": bf(np.random.standard_normal((B, S, DIM)) * s),
            "freqs_cos": bf(np.cos(ang)),
            "freqs_sin": bf(np.sin(ang)),
            "wkv_a_w": bf(np.random.standard_normal((KV_RANK + ROPE_SP, DIM)) * 0.25 / np.sqrt(DIM) / s[None, :]),
            "wkv_a_b": bf(np.random.standard_normal(KV_RANK + ROPE_SP) * 0.1),
            "kv_norm_w": bf(np.sqrt(8.0 / KV_RANK) * (1.0 + 0.1 * np.random.standard_normal(KV_RANK))),
            "wkv_b_w": bf(np.random.standard_normal((H * (NOPE + V_SP), KV_RANK + 1)) * 0.06),
            "wkv_b_b": bf(np.random.standard_normal(H * (NOPE + V_SP)) * 0.1)}


def reference(x, freqs_cos, freqs_sin, wkv_a_w, wkv_a_b, kv_norm_w, wkv_b_w, wkv_b_b):
    kv_full = (mxq(f64(x), 2, "e4m3") @ mxq(f64(wkv_a_w), 1, "e4m3").T) + f64(wkv_a_b)
    kv, k_pe = kv_full[..., :KV_RANK], kv_full[..., KV_RANK:]
    k_pe = rope(k_pe[:, :, None, :], f64(freqs_cos), f64(freqs_sin))
    sp = kv / np.sqrt((kv * kv).mean(-1, keepdims=True) + EPS) * f64(kv_norm_w)
    t = np.sqrt((sp * sp).sum(-1, keepdims=True) + C)
    wb = f64(wkv_b_w)
    kv2 = (mxq(sp, 2, "e4m3") @ mxq(wb[:, 1:], 1, "e4m3").T) + t * wb[:, 0] + f64(wkv_b_b)
    kv2 = kv2.reshape(B, S, H, NOPE + V_SP)
    k = np.concatenate([kv2[..., :NOPE], np.broadcast_to(k_pe, (B, S, H, ROPE_SP))], -1)
    return lift(k), lift(kv2[..., NOPE:])

@@ -1,0 +1,453 @@
+from contextlib import ExitStack
+
+import concourse.mybir as mybir
+from concourse.masks import make_identity
+
+F32 = mybir.dt.float32
+BF16 = mybir.dt.bfloat16
+U32 = mybir.dt.uint32
+U8 = mybir.dt.uint8
+FP8X4 = mybir.dt.float8_e4m3fn_x4
+ALU = mybir.AluOpType
+ACT = mybir.ActivationFunctionType
+AXIS = mybir.AxisListType
+
+P = 128
+TOKENS = 4 * 1024
+DIM = 1024
+PASSES = DIM // (4 * P)
+KV_RANK = 512
+ROPE = 128
+HEADS = 2
+NOPE = 64
+V_DIM = 64
+KV2 = HEADS * (NOPE + V_DIM)
+K_ROW = 1 + NOPE + ROPE
+V_ROW = 1 + V_DIM
+SUB = 4
+GROUP = P * SUB
+GROUPS = TOKENS // GROUP
+TABLE_HALVES = 1024 // GROUP
+EPS = 1e-6
+
+FLOPS = 2 * TOKENS * DIM * (KV_RANK + ROPE) + 2 * TOKENS * KV_RANK * KV2
+
+
+def tile_lorentzmla_pa_t_kernel(
+    tc, x, freqs_cos, freqs_sin, wkv_a_w, wkv_a_b, kv_norm_w, wkv_b_w, wkv_b_b, out_0, out_1
+):
+    nc = tc.nc
+    x_groups = x.flatten_outer_dims().rearrange("(g p n) k -> g p n k", p=P, n=SUB)
+    ksl_groups = out_0.rearrange("b s h f -> (b s) (h f)").rearrange("(g p n) f -> g p (n f)", p=P, n=SUB)
+    vs_groups = out_1.rearrange("b s h f -> (b s) (h f)").rearrange("(g p n) f -> g p (n f)", p=P, n=SUB)
+
+    with ExitStack() as ctx:
+        consts = ctx.enter_context(tc.tile_pool(name="consts", bufs=1))
+        rows_in = ctx.enter_context(tc.tile_pool(name="rows_in", bufs=6))
+        work = ctx.enter_context(tc.tile_pool(name="work", bufs=2))
+        outs = ctx.enter_context(tc.tile_pool(name="outs", bufs=3))
+        psum = ctx.enter_context(tc.psum_pool(name="psum", bufs=1))
+        ctx.enter_context(tc.manual_schedule())
+
+        wa_kv_sb = rows_in.tile([P, SUB, DIM], BF16, tag="rows")
+        nc.sync.dma_start(out=wa_kv_sb[:], in_=wkv_a_w[0:KV_RANK, :].rearrange("(p t) k -> p t k", t=SUB))
+        wa_pe_sb = rows_in.tile([P, SUB, DIM], BF16, tag="rows")
+        wa_pe_rows = wkv_a_w[KV_RANK : KV_RANK + ROPE, :].rearrange("(j e) k -> e j k", e=2)
+        for e in range(2):
+            nc.sync.dma_start(out=wa_pe_sb[e * 64 : (e + 1) * 64, 0, :], in_=wa_pe_rows[e])
+
+        x_sb = {}
+
+        def load_x(g):
+            x_tile = rows_in.tile([P, SUB, DIM], BF16, tag="rows")
+            nc.sync.dma_start(out=x_tile[:], in_=x_groups[g])
+            x_sb[g] = x_tile
+
+        for g in range(4):
+            load_x(g)
+
+        b_bf = consts.tile([P, SUB], BF16)
+        nc.scalar.dma_start(out=b_bf[:], in_=wkv_a_b[0:KV_RANK].rearrange("(p t) -> p t", t=SUB))
+        w_bf = consts.tile([P, SUB], BF16)
+        nc.scalar.dma_start(out=w_bf[:], in_=kv_norm_w.rearrange("(p t) -> p t", t=SUB))
+        wb_full = consts.tile([P, 2, KV_RANK + 1], BF16)
+        nc.scalar.dma_start(out=wb_full[:], in_=wkv_b_w.rearrange("(o p) k -> p o k", p=P))
+        vec_rows = consts.tile([P, 512], BF16)
+        nc.vector.memset(vec_rows[:], 0.0)
+        nc.scalar.dma_start(out=vec_rows[0:1, 0:KV2], in_=wkv_b_b.unsqueeze(0))
+        nc.scalar.dma_start(out=vec_rows[0:1, KV2 : KV2 + ROPE], in_=wkv_a_b[KV_RANK : KV_RANK + ROPE].unsqueeze(0))
+        cos_t = consts.tile([P, TABLE_HALVES, SUB, ROPE // 2], BF16)
+        nc.scalar.dma_start(out=cos_t[:], in_=freqs_cos.rearrange("(a p n) j -> p a n j", p=P, n=SUB))
+        sin_t = consts.tile([P, TABLE_HALVES, SUB, ROPE // 2], BF16)
+        nc.scalar.dma_start(out=sin_t[:], in_=freqs_sin.rearrange("(a p n) j -> p a n j", p=P, n=SUB))
+
+        ident = consts.tile([P, P], F32)
+        make_identity(nc, ident[:])
+        ones_bf = consts.tile([P, P], BF16)
+        nc.vector.memset(ones_bf[:], 1.0)
+
+        def transpose_and_group(rows_words, grouped_words):
+            flipped = psum.tile([P, 4, P], F32, tag="flip", bufs=2)
+            for c in range(4):
+                nc.tensor.transpose(flipped[:, c, :], rows_words[:, c * P : (c + 1) * P], ident[:])
+            nc.scalar.copy(out=grouped_words, in_=flipped[:].rearrange("q (a u) r -> q a r u", u=2))
+
+        def new_grouped():
+            grouped = work.tile([P, PASSES, SUB, P, 4], BF16, tag="grouped", align_bytes=64)
+            return grouped
+
+        def flip_place(rows_sb, grouped, n):
+            transpose_and_group(rows_sb[:].bitcast(F32)[:, n, :], grouped[:].bitcast(F32)[:, :, n, :, :])
+
+        def quantise_passes(grouped, codes, scales):
+            for a in range(PASSES):
+                nc.vector.quantize_mx(
+                    out=codes[:, a, :].bitcast(FP8X4),
+                    scales=scales[:, a, :],
+                    in_=grouped[:, a, :, :, :].rearrange("q n r t -> q (n r t)"),
+                )
+
+        wa_kv_codes = consts.tile([P, PASSES, KV_RANK], U32, align_bytes=64)
+        wa_kv_scales = consts.tile([P, PASSES, KV_RANK], U8, align_bytes=64)
+        wa_grouped = new_grouped()
+        for t in range(SUB):
+            flip_place(wa_kv_sb, wa_grouped, t)
+        quantise_passes(wa_grouped, wa_kv_codes, wa_kv_scales)
+
+        wa_pe_codes = consts.tile([P, PASSES, ROPE], U32, align_bytes=64)
+        wa_pe_scales = consts.tile([P, PASSES, ROPE], U8, align_bytes=64)
+        pe_grouped = new_grouped()
+        flip_place(wa_pe_sb, pe_grouped, 0)
+        for a in range(PASSES):
+            nc.vector.quantize_mx(
+                out=wa_pe_codes[:, a, :].bitcast(FP8X4),
+                scales=wa_pe_scales[:, a, :],
+                in_=pe_grouped[:, a, 0, :, :].rearrange("q r t -> q (r t)"),
+            )
+
+        x_codes = {}
+        x_scales = {}
+
+        x_grouped = {}
+
+        def flip_x(g, places):
+            if places[0] == 0:
+                x_grouped[g] = new_grouped()
+            for n in places:
+                flip_place(x_sb[g], x_grouped[g], n)
+
+        def quantise_x(g):
+            codes = work.tile([P, PASSES, GROUP], U32, tag="x_codes", align_bytes=64)
+            scales = work.tile([P, PASSES, GROUP], U8, tag="x_scales", align_bytes=64)
+            quantise_passes(x_grouped[g], codes, scales)
+            x_codes[g] = codes
+            x_scales[g] = scales
+
+        flip_x(0, (0, 1, 2, 3))
+        quantise_x(0)
+
+        b32 = consts.tile([P, SUB], F32)
+        nc.vector.tensor_copy(out=b32[:], in_=b_bf[:])
+        w32 = consts.tile([P, SUB], F32)
+        nc.vector.tensor_copy(out=w32[:], in_=w_bf[:])
+        bw32 = consts.tile([P, SUB], F32)
+        nc.vector.tensor_tensor(out=bw32[:], in0=b32[:], in1=w32[:], op=ALU.mult)
+        sum_cols = consts.tile([P, SUB, 2], F32)
+        nc.vector.memset(sum_cols[:], 1.0)
+        nc.vector.tensor_tensor(out=sum_cols[:, :, 1], in0=w32[:], in1=w32[:], op=ALU.mult)
+        nsin_t = consts.tile([P, TABLE_HALVES, SUB, ROPE // 2], BF16)
+        nc.vector.tensor_scalar(out=nsin_t[:], in0=sin_t[:], scalar1=-1.0, scalar2=None, op0=ALU.mult)
+
+        wb_even = consts.tile([P, 2, KV_RANK], BF16)
+        nc.vector.tensor_copy(out=wb_even[:], in_=wb_full[:, :, 1 : KV_RANK + 1])
+        wb_words = wb_even[:].bitcast(F32).rearrange("r o (q u) -> r o u q", u=2)
+        wb_flipped = psum.tile([P, 4, P], F32, tag="flip", bufs=2)
+        for o in range(2):
+            for u in range(2):
+                nc.tensor.transpose(wb_flipped[:, 2 * o + u, :], wb_words[:, o, u, :], ident[:])
+        wb_grouped = consts.tile([P, KV2, 4], BF16, align_bytes=64)
+        nc.scalar.copy(
+            out=wb_grouped[:].bitcast(F32).rearrange("q (o r) u -> q o r u", o=2),
+            in_=wb_flipped[:].rearrange("q (o u) r -> q o r u", u=2),
+        )
+        wb_codes = consts.tile([P, KV2], U32, align_bytes=64)
+        wb_scales = consts.tile([P, KV2], U8, align_bytes=64)
+        nc.vector.quantize_mx(
+            out=wb_codes[:].bitcast(FP8X4),
+            scales=wb_scales[:],
+            in_=wb_grouped[:].rearrange("q c t -> q (c t)"),
+        )
+
+        wb0_col = consts.tile([P, 2], F32)
+        nc.vector.tensor_copy(out=wb0_col[:], in_=wb_full[:, :, 0])
+        wb0_bank = psum.tile([P, 512], F32, tag="y", bufs=3)
+        for o in range(2):
+            nc.tensor.transpose(
+                wb0_bank[:, o * P : (o + 1) * P], wb0_col[:, o : o + 1].to_broadcast([P, P]), ident[:]
+            )
+        wb0_all = consts.tile([P, KV2], F32)
+        nc.scalar.copy(out=wb0_all[:], in_=wb0_bank[:, 0:KV2])
+        vec_bank = psum.tile([P, 512], F32, tag="y", bufs=3)
+        nc.tensor.matmul(out=vec_bank[:], lhsT=ones_bf[:], rhs=vec_rows[:], start=True, stop=True)
+        bb_all = consts.tile([P, KV2], F32)
+        nc.scalar.copy(out=bb_all[:], in_=vec_bank[:, 0:KV2])
+        bpe_all = consts.tile([P, 2, ROPE // 2], F32)
+        nc.scalar.copy(out=bpe_all[:], in_=vec_bank[:, KV2 : KV2 + ROPE].rearrange("p (j e) -> p e j", e=2))
+
+        squares = {}
+        kv_w = {}
+        rope_in = {}
+        rstd = {}
+        time_sp = {}
+        sp_codes = {}
+        sp_scales = {}
+        ksl_sb = {}
+        vs_sb = {}
+        lift_sq = {}
+
+        def kv_banks(g):
+            sq = work.tile([P, SUB, GROUP], F32, tag="sq")
+            kw = work.tile([P, SUB, GROUP], F32, tag="kw", bufs=3)
+            for t in range(SUB):
+                y = psum.tile([P, GROUP], F32, tag="y", bufs=3)
+                for a in range(PASSES):
+                    nc.tensor.matmul_mx(
+                        out=y[:],
+                        lhsT=wa_kv_codes[:, a, t * P : (t + 1) * P].bitcast(FP8X4),
+                        lhsT_scale=wa_kv_scales[:, a, t * P : (t + 1) * P],
+                        rhs=x_codes[g][:, a, :].bitcast(FP8X4),
+                        rhs_scale=x_scales[g][:, a, :],
+                        start=(a == 0),
+                        stop=(a == PASSES - 1),
+                    )
+                nc.scalar.activation(out=sq[:, t, :], in_=y[:], func=ACT.Square, bias=b32[:, t : t + 1], scale=1.0)
+                nc.scalar.activation(
+                    out=kw[:, t, :], in_=y[:], func=ACT.Identity, bias=bw32[:, t : t + 1], scale=w32[:, t : t + 1]
+                )
+            squares[g] = sq
+            kv_w[g] = kw
+
+        def rope_columns(g):
+            pe = psum.tile([P, SUB, ROPE], F32, tag="small", bufs=2)
+            for n in range(SUB):
+                for a in range(PASSES):
+                    nc.tensor.matmul_mx(
+                        out=pe[:, n, :],
+                        lhsT=x_codes[g][:, a, n * P : (n + 1) * P].bitcast(FP8X4),
+                        lhsT_scale=x_scales[g][:, a, n * P : (n + 1) * P],
+                        rhs=wa_pe_codes[:, a, :].bitcast(FP8X4),
+                        rhs_scale=wa_pe_scales[:, a, :],
+                        start=(a == 0),
+                        stop=(a == PASSES - 1),
+                    )
+            pb = outs.tile([P, SUB, 2, ROPE // 2], F32, tag="pb")
+            nc.vector.tensor_tensor(
+                out=pb[:],
+                in0=pe[:].rearrange("p n (e j) -> p n e j", e=2),
+                in1=bpe_all[:].unsqueeze(1).to_broadcast([P, SUB, 2, ROPE // 2]),
+                op=ALU.add,
+            )
+            rope_in[g] = pb
+
+        norm_sums = {}
+        inv_mean_sq = {}
+        sp_square_sum = {}
+
+        def feature_sums(g):
+            sums = psum.tile([P, SUB, 2], F32, tag="norm", bufs=1)
+            for n in range(SUB):
+                for t in range(SUB):
+                    nc.tensor.matmul(
+                        out=sums[:, n, :],
+                        lhsT=squares[g][:, t, n * P : (n + 1) * P],
+                        rhs=sum_cols[:, t, :],
+                        start=(t == 0),
+                        stop=(t == SUB - 1),
+                    )
+            norm_sums[g] = sums
+
+        def norm_scalars_vector(g):
+            sums = norm_sums[g]
+            mean_sq = outs.tile([P, SUB], F32, tag="mean_sq")
+            nc.vector.tensor_scalar(
+                out=mean_sq[:], in0=sums[:, :, 0], scalar1=1.0 / KV_RANK, scalar2=EPS, op0=ALU.mult, op1=ALU.add
+            )
+            inv_ms = outs.tile([P, SUB], F32, tag="inv_ms")
+            nc.vector.reciprocal(out=inv_ms[:], in_=mean_sq[:])
+            sp_sq = outs.tile([P, SUB], F32, tag="sp_sq")
+            nc.vector.tensor_tensor(out=sp_sq[:], in0=sums[:, :, 1], in1=inv_ms[:], op=ALU.mult)
+            inv_mean_sq[g] = inv_ms
+            sp_square_sum[g] = sp_sq
+
+        def norm_scalars_scalar(g):
+            inv_ms = inv_mean_sq[g]
+            sp_sq = sp_square_sum[g]
+            rs = outs.tile([P, SUB], F32, tag="rs")
+            nc.scalar.activation(out=rs[:], in_=inv_ms[:], func=ACT.Sqrt)
+            tm = outs.tile([P, SUB], F32, tag="tm")
+            nc.scalar.activation(out=tm[:], in_=sp_sq[:], func=ACT.Sqrt, bias=1.0, scale=1.0)
+            rstd[g] = rs
+            time_sp[g] = tm
+
+        def norm(g):
+            spread = psum.tile([P, GROUP], F32, tag="norm", bufs=1)
+            for n in range(SUB):
+                nc.tensor.transpose(
+                    spread[:, n * P : (n + 1) * P], rstd[g][:, n : n + 1].to_broadcast([P, P]), ident[:]
+                )
+            sp_grouped = work.tile([P, GROUP, SUB], BF16, tag="sp_grouped", align_bytes=64)
+            nc.vector.tensor_tensor(
+                out=sp_grouped[:],
+                in0=kv_w[g][:].rearrange("p t c -> p c t"),
+                in1=spread[:].unsqueeze(2).to_broadcast([P, GROUP, SUB]),
+                op=ALU.mult,
+            )
+            codes = work.tile([P, GROUP], U32, tag="sp_codes", align_bytes=64)
+            scales = work.tile([P, GROUP], U8, tag="sp_scales", align_bytes=64)
+            nc.vector.quantize_mx(
+                out=codes[:].bitcast(FP8X4), scales=scales[:], in_=sp_grouped[:].rearrange("p c t -> p (c t)")
+            )
+            sp_codes[g] = codes
+            sp_scales[g] = scales
+
+        kv2_sb = {}
+
+        def rope_rotate(g):
+            ksl = outs.tile([P, SUB, HEADS, K_ROW], F32, tag="ksl", bufs=4)
+            ksl_sb[g] = ksl
+            half = g % TABLE_HALVES
+            pb = rope_in[g]
+            by_cos = work.tile([P, SUB, 2, ROPE // 2], F32, tag="by_cos")
+            nc.gpsimd.tensor_tensor(
+                out=by_cos[:],
+                in0=pb[:],
+                in1=cos_t[:, half, :, :].unsqueeze(2).to_broadcast([P, SUB, 2, ROPE // 2]),
+                op=ALU.mult,
+            )
+            by_sin = work.tile([P, SUB, 2, ROPE // 2], F32, tag="by_sin")
+            nc.gpsimd.tensor_tensor(out=by_sin[:, :, 0, :], in0=pb[:, :, 1, :], in1=nsin_t[:, half, :, :], op=ALU.mult)
+            nc.gpsimd.tensor_tensor(out=by_sin[:, :, 1, :], in0=pb[:, :, 0, :], in1=sin_t[:, half, :, :], op=ALU.mult)
+            nc.gpsimd.tensor_tensor(
+                out=ksl[:, :, 0, 1 + NOPE : K_ROW].rearrange("p n (j e) -> p n j e", e=2),
+                in0=by_cos[:].rearrange("p n e j -> p n j e"),
+                in1=by_sin[:].rearrange("p n e j -> p n j e"),
+                op=ALU.add,
+            )
+            nc.gpsimd.tensor_scalar(
+                out=ksl[:, :, 1, 1 + NOPE : K_ROW],
+                in0=ksl[:, :, 0, 1 + NOPE : K_ROW],
+                scalar1=1.0,
+                scalar2=0.0,
+                op0=ALU.mult,
+                op1=ALU.add,
+            )
+
+        def second_product(g):
+            kv2 = work.tile([P, SUB, HEADS, NOPE + V_DIM], F32, tag="kv2")
+            for pair in range(SUB // 2):
+                bank = psum.tile([P, 2, KV2], F32, tag="small", bufs=2)
+                for i in range(2):
+                    n = 2 * pair + i
+                    nc.tensor.matmul_mx(
+                        out=bank[:, i, :],
+                        lhsT=sp_codes[g][:, n * P : (n + 1) * P].bitcast(FP8X4),
+                        lhsT_scale=sp_scales[g][:, n * P : (n + 1) * P],
+                        rhs=wb_codes[:].bitcast(FP8X4),
+                        rhs_scale=wb_scales[:],
+                        start=True,
+                        stop=True,
+                    )
+                    nc.vector.scalar_tensor_tensor(
+                        out=kv2[:, n, :, :].rearrange("p h c -> p (h c)"),
+                        in0=wb0_all[:],
+                        scalar=time_sp[g][:, n : n + 1],
+                        in1=bank[:, i, :],
+                        op0=ALU.mult,
+                        op1=ALU.add,
+                    )
+            kv2_sb[g] = kv2
+
+        def add_second_bias(g):
+            kv2 = kv2_sb[g]
+            ksl = ksl_sb[g]
+            vs = outs.tile([P, SUB, HEADS, V_ROW], F32, tag="vs", bufs=4)
+            vs_sb[g] = vs
+            bb4 = bb_all[:].rearrange("p (h c) -> p h c", h=HEADS).unsqueeze(1).to_broadcast([P, SUB, HEADS, NOPE + V_DIM])
+            nc.gpsimd.tensor_tensor(
+                out=ksl[:, :, :, 1 : 1 + NOPE], in0=kv2[:, :, :, 0:NOPE], in1=bb4[:, :, :, 0:NOPE], op=ALU.add
+            )
+            nc.gpsimd.tensor_tensor(
+                out=vs[:, :, :, 1:V_ROW], in0=kv2[:, :, :, NOPE : NOPE + V_DIM], in1=bb4[:, :, :, NOPE : NOPE + V_DIM], op=ALU.add
+            )
+
+        def lift_squares(g):
+            ksl = ksl_sb[g]
+            vs = vs_sb[g]
+            lsq = work.tile([P, SUB, 6, 64], F32, tag="lsq")
+            nc.scalar.activation(out=lsq[:, :, 0:2, :], in_=ksl[:, :, :, 1 : 1 + NOPE], func=ACT.Square)
+            nc.scalar.activation(
+                out=lsq[:, :, 2:4, :].rearrange("p n b c -> p n (b c)"), in_=ksl[:, :, 1, 1 + NOPE : K_ROW], func=ACT.Square
+            )
+            nc.scalar.activation(out=lsq[:, :, 4:6, :], in_=vs[:, :, :, 1:V_ROW], func=ACT.Square)
+            lift_sq[g] = lsq
+
+        lift_k = {}
+        lift_all = {}
+
+        def lift_sums(g):
+            sums = outs.tile([P, SUB, 6], F32, tag="lift_sums")
+            nc.vector.tensor_reduce(
+                out=sums[:].rearrange("p n b -> p (n b)"),
+                in_=lift_sq[g][:].rearrange("p n b c -> p (n b) c"),
+                axis=AXIS.X,
+                op=ALU.add,
+            )
+            rope_sum = outs.tile([P, SUB], F32, tag="rope_sum")
+            nc.vector.tensor_tensor(out=rope_sum[:], in0=sums[:, :, 2], in1=sums[:, :, 3], op=ALU.add)
+            k_sum = outs.tile([P, SUB, HEADS], F32, tag="k_sum")
+            nc.vector.tensor_tensor(
+                out=k_sum[:], in0=sums[:, :, 0:2], in1=rope_sum[:].unsqueeze(2).to_broadcast([P, SUB, HEADS]), op=ALU.add
+            )
+            lift_k[g] = k_sum
+            lift_all[g] = sums
+
+        def lift_roots_and_store(g):
+            nc.scalar.activation(out=ksl_sb[g][:, :, :, 0], in_=lift_k[g][:], func=ACT.Sqrt, bias=1.0, scale=1.0)
+            nc.scalar.activation(out=vs_sb[g][:, :, :, 0], in_=lift_all[g][:, :, 4:6], func=ACT.Sqrt, bias=1.0, scale=1.0)
+            nc.sync.dma_start(out=ksl_groups[g], in_=ksl_sb[g][:].rearrange("p n h f -> p (n h f)"))
+            nc.sync.dma_start(out=vs_groups[g], in_=vs_sb[g][:].rearrange("p n h f -> p (n h f)"))
+
+        def live(g):
+            return 0 <= g < GROUPS
+
+        for i in range(GROUPS + 4):
+            if live(i):
+                kv_banks(i)
+            if live(i - 2):
+                rope_rotate(i - 2)
+                second_product(i - 2)
+                add_second_bias(i - 2)
+            if live(i):
+                rope_columns(i)
+            if live(i + 4):
+                load_x(i + 4)
+            if live(i + 1):
+                flip_x(i + 1, (0, 1))
+            if live(i - 1):
+                feature_sums(i - 1)
+            if live(i - 4):
+                lift_sums(i - 4)
+            if live(i - 1):
+                norm_scalars_vector(i - 1)
+            if live(i + 1):
+                flip_x(i + 1, (2, 3))
+            if live(i - 1):
+                norm_scalars_scalar(i - 1)
+            if live(i + 1):
+                quantise_x(i + 1)
+            if live(i - 1):
+                norm(i - 1)
+            if live(i - 3):
+                lift_squares(i - 3)
+            if live(i - 4):
+                lift_roots_and_store(i - 4)

@@ -18,6 +18,7 @@ DIM = 1024
 PASSES = DIM // (4 * P)
 KV_RANK = 512
 ROPE = 128
+HALF = ROPE // 2
 HEADS = 2
 NOPE = 64
 V_DIM = 64
@@ -42,193 +43,207 @@ def tile_lorentzmla_pa_t_kernel(
     vs_groups = out_1.rearrange("b s h f -> (b s) (h f)").rearrange("(g p n) f -> g p (n f)", p=P, n=SUB)
 
     with ExitStack() as ctx:
-        consts = ctx.enter_context(tc.tile_pool(name="consts", bufs=1))
-        rows_in = ctx.enter_context(tc.tile_pool(name="rows_in", bufs=6))
-        work = ctx.enter_context(tc.tile_pool(name="work", bufs=2))
-        outs = ctx.enter_context(tc.tile_pool(name="outs", bufs=3))
-        psum = ctx.enter_context(tc.psum_pool(name="psum", bufs=1))
+        once = ctx.enter_context(tc.tile_pool(name="once", bufs=1))
+        twice = ctx.enter_context(tc.tile_pool(name="twice", bufs=2))
+        four = ctx.enter_context(tc.tile_pool(name="four", bufs=4))
+        five = ctx.enter_context(tc.tile_pool(name="five", bufs=5))
+        psum_flip = ctx.enter_context(tc.psum_pool(name="psum_flip", bufs=2))
+        psum_y = ctx.enter_context(tc.psum_pool(name="psum_y", bufs=2))
+        psum_small = ctx.enter_context(tc.psum_pool(name="psum_small", bufs=2))
+        psum_norm = ctx.enter_context(tc.psum_pool(name="psum_norm", bufs=2))
         ctx.enter_context(tc.manual_schedule())
-
-        wa_kv_sb = rows_in.tile([P, SUB, DIM], BF16, tag="rows")
-        nc.sync.dma_start(out=wa_kv_sb[:], in_=wkv_a_w[0:KV_RANK, :].rearrange("(p t) k -> p t k", t=SUB))
-        wa_pe_sb = rows_in.tile([P, SUB, DIM], BF16, tag="rows")
-        wa_pe_rows = wkv_a_w[KV_RANK : KV_RANK + ROPE, :].rearrange("(j e) k -> e j k", e=2)
-        for e in range(2):
-            nc.sync.dma_start(out=wa_pe_sb[e * 64 : (e + 1) * 64, 0, :], in_=wa_pe_rows[e])
 
         x_sb = {}
 
         def load_x(g):
-            x_tile = rows_in.tile([P, SUB, DIM], BF16, tag="rows")
+            x_tile = five.tile([P, SUB, DIM], BF16, tag="rows")
             nc.sync.dma_start(out=x_tile[:], in_=x_groups[g])
             x_sb[g] = x_tile
 
-        for g in range(4):
+        load_x(0)
+        wa_kv_sb = five.tile([P, SUB, DIM], BF16, tag="rows")
+        wa_kv_rows = wkv_a_w[0:KV_RANK, :].rearrange("(p t) k -> p t k", t=SUB)
+        for t in range(SUB):
+            nc.sync.dma_start(out=wa_kv_sb[:, t, :], in_=wa_kv_rows[:, t, :])
+        wa_pe_sb = once.tile([P, 1, DIM], BF16)
+        wa_pe_rows = wkv_a_w[KV_RANK : KV_RANK + ROPE, :].rearrange("(j e) k -> e j k", e=2)
+        for e in range(2):
+            nc.sync.dma_start(out=wa_pe_sb[e * HALF : (e + 1) * HALF, 0, :], in_=wa_pe_rows[e])
+        for g in range(1, 4):
             load_x(g)
 
-        b_bf = consts.tile([P, SUB], BF16)
+        b_bf = once.tile([P, SUB], BF16)
         nc.scalar.dma_start(out=b_bf[:], in_=wkv_a_b[0:KV_RANK].rearrange("(p t) -> p t", t=SUB))
-        w_bf = consts.tile([P, SUB], BF16)
+        w_bf = once.tile([P, SUB], BF16)
         nc.scalar.dma_start(out=w_bf[:], in_=kv_norm_w.rearrange("(p t) -> p t", t=SUB))
-        wb_full = consts.tile([P, 2, KV_RANK + 1], BF16)
+        wb_full = once.tile([P, 2, KV_RANK + 1], BF16)
         nc.scalar.dma_start(out=wb_full[:], in_=wkv_b_w.rearrange("(o p) k -> p o k", p=P))
-        vec_rows = consts.tile([P, 512], BF16)
+        vec_rows = once.tile([P, 512], BF16)
         nc.vector.memset(vec_rows[:], 0.0)
         nc.scalar.dma_start(out=vec_rows[0:1, 0:KV2], in_=wkv_b_b.unsqueeze(0))
         nc.scalar.dma_start(out=vec_rows[0:1, KV2 : KV2 + ROPE], in_=wkv_a_b[KV_RANK : KV_RANK + ROPE].unsqueeze(0))
-        cos_t = consts.tile([P, TABLE_HALVES, SUB, ROPE // 2], BF16)
+        cos_t = once.tile([P, TABLE_HALVES, SUB, HALF], BF16)
         nc.scalar.dma_start(out=cos_t[:], in_=freqs_cos.rearrange("(a p n) j -> p a n j", p=P, n=SUB))
-        sin_t = consts.tile([P, TABLE_HALVES, SUB, ROPE // 2], BF16)
+        sin_t = once.tile([P, TABLE_HALVES, SUB, HALF], BF16)
         nc.scalar.dma_start(out=sin_t[:], in_=freqs_sin.rearrange("(a p n) j -> p a n j", p=P, n=SUB))
 
-        ident = consts.tile([P, P], F32)
+        ident = once.tile([P, P], F32)
         make_identity(nc, ident[:])
-        ones_bf = consts.tile([P, P], BF16)
+        ones_bf = once.tile([P, P], BF16)
         nc.vector.memset(ones_bf[:], 1.0)
 
-        def transpose_and_group(rows_words, grouped_words):
-            flipped = psum.tile([P, 4, P], F32, tag="flip", bufs=2)
-            for c in range(4):
-                nc.tensor.transpose(flipped[:, c, :], rows_words[:, c * P : (c + 1) * P], ident[:])
-            nc.scalar.copy(out=grouped_words, in_=flipped[:].rearrange("q (a u) r -> q a r u", u=2))
-
-        def new_grouped():
-            grouped = work.tile([P, PASSES, SUB, P, 4], BF16, tag="grouped", align_bytes=64)
-            return grouped
+        b32 = once.tile([P, SUB], F32)
+        nc.vector.tensor_copy(out=b32[:], in_=b_bf[:])
+        w32 = once.tile([P, SUB], F32)
+        nc.vector.tensor_copy(out=w32[:], in_=w_bf[:])
+        bw32 = once.tile([P, SUB], F32)
+        nc.vector.tensor_tensor(out=bw32[:], in0=b32[:], in1=w32[:], op=ALU.mult)
+        w_sq = once.tile([P, SUB], F32)
+        nc.vector.tensor_tensor(out=w_sq[:], in0=w32[:], in1=w32[:], op=ALU.mult)
+        sum_cols = once.tile([P, SUB, 4], BF16)
+        nc.vector.memset(sum_cols[:], 0.0)
+        nc.vector.memset(sum_cols[:, :, 0], 1.0)
+        nc.vector.tensor_copy(out=sum_cols[:, :, 1], in_=w_sq[:])
+        nc.vector.tensor_tensor(out=sum_cols[:, :, 2], in0=w_sq[:], in1=sum_cols[:, :, 1], op=ALU.subtract)
+        nsin_t = once.tile([P, TABLE_HALVES, SUB, HALF], BF16)
+        nc.vector.tensor_scalar(out=nsin_t[:], in0=sin_t[:], scalar1=-1.0, scalar2=None, op0=ALU.mult)
 
         def flip_place(rows_sb, grouped, n):
-            transpose_and_group(rows_sb[:].bitcast(F32)[:, n, :], grouped[:].bitcast(F32)[:, :, n, :, :])
-
-        def quantise_passes(grouped, codes, scales):
-            for a in range(PASSES):
-                nc.vector.quantize_mx(
-                    out=codes[:, a, :].bitcast(FP8X4),
-                    scales=scales[:, a, :],
-                    in_=grouped[:, a, :, :, :].rearrange("q n r t -> q (n r t)"),
-                )
-
-        wa_kv_codes = consts.tile([P, PASSES, KV_RANK], U32, align_bytes=64)
-        wa_kv_scales = consts.tile([P, PASSES, KV_RANK], U8, align_bytes=64)
-        wa_grouped = new_grouped()
-        for t in range(SUB):
-            flip_place(wa_kv_sb, wa_grouped, t)
-        quantise_passes(wa_grouped, wa_kv_codes, wa_kv_scales)
-
-        wa_pe_codes = consts.tile([P, PASSES, ROPE], U32, align_bytes=64)
-        wa_pe_scales = consts.tile([P, PASSES, ROPE], U8, align_bytes=64)
-        pe_grouped = new_grouped()
-        flip_place(wa_pe_sb, pe_grouped, 0)
-        for a in range(PASSES):
-            nc.vector.quantize_mx(
-                out=wa_pe_codes[:, a, :].bitcast(FP8X4),
-                scales=wa_pe_scales[:, a, :],
-                in_=pe_grouped[:, a, 0, :, :].rearrange("q r t -> q (r t)"),
+            rows_words = rows_sb[:].bitcast(F32)[:, n, :]
+            flipped = psum_flip.tile([P, 4, P], F32, tag="flip")
+            for c in range(4):
+                nc.tensor.transpose(flipped[:, c, :], rows_words[:, c * P : (c + 1) * P], ident[:])
+            nc.scalar.copy(
+                out=grouped[:].bitcast(F32)[:, :, n, :, :], in_=flipped[:].rearrange("q (a u) r -> q a r u", u=2)
             )
 
+        wa_kv_codes = once.tile([P, PASSES, KV_RANK], U32, align_bytes=64)
+        wa_kv_scales = once.tile([P, PASSES, KV_RANK], U8, align_bytes=64)
+        wa_grouped = once.tile([P, PASSES, SUB, P, 4], BF16, align_bytes=64)
+
+        def prepare_wa_tile(t):
+            flip_place(wa_kv_sb, wa_grouped, t)
+            for a in range(PASSES):
+                nc.vector.quantize_mx(
+                    out=wa_kv_codes[:, a, t * P : (t + 1) * P].bitcast(FP8X4),
+                    scales=wa_kv_scales[:, a, t * P : (t + 1) * P],
+                    in_=wa_grouped[:, a, t, :, :].rearrange("q r j -> q (r j)"),
+                )
+
+        wa_pe_codes = once.tile([P, PASSES, ROPE], U32, align_bytes=64)
+        wa_pe_scales = once.tile([P, PASSES, ROPE], U8, align_bytes=64)
+        pe_grouped = once.tile([P, PASSES, 1, P, 4], BF16, align_bytes=64)
+
+        def prepare_wa_rope():
+            flip_place(wa_pe_sb, pe_grouped, 0)
+            for a in range(PASSES):
+                nc.vector.quantize_mx(
+                    out=wa_pe_codes[:, a, :].bitcast(FP8X4),
+                    scales=wa_pe_scales[:, a, :],
+                    in_=pe_grouped[:, a, 0, :, :].rearrange("q r j -> q (r j)"),
+                )
+
+        x_grouped = {}
         x_codes = {}
         x_scales = {}
 
-        x_grouped = {}
-
         def flip_x(g, places):
             if places[0] == 0:
-                x_grouped[g] = new_grouped()
+                grouped = twice.tile([P, PASSES, SUB, P, 4], BF16, tag="grouped", align_bytes=64)
+                x_grouped[g] = grouped
             for n in places:
                 flip_place(x_sb[g], x_grouped[g], n)
 
         def quantise_x(g):
-            codes = work.tile([P, PASSES, GROUP], U32, tag="x_codes", align_bytes=64)
-            scales = work.tile([P, PASSES, GROUP], U8, tag="x_scales", align_bytes=64)
-            quantise_passes(x_grouped[g], codes, scales)
+            codes = twice.tile([P, PASSES, GROUP], U32, tag="x_codes", align_bytes=64)
+            scales = twice.tile([P, PASSES, GROUP], U8, tag="x_scales", align_bytes=64)
+            for a in range(PASSES):
+                nc.vector.quantize_mx(
+                    out=codes[:, a, :].bitcast(FP8X4),
+                    scales=scales[:, a, :],
+                    in_=x_grouped[g][:, a, :, :, :].rearrange("q n r j -> q (n r j)"),
+                )
             x_codes[g] = codes
             x_scales[g] = scales
 
-        flip_x(0, (0, 1, 2, 3))
-        quantise_x(0)
+        bb_all = once.tile([P, KV2], F32)
+        bpe_all = once.tile([P, 2, HALF], F32)
+        wb_codes = once.tile([P, KV2], U32, align_bytes=64)
+        wb_scales = once.tile([P, KV2], U8, align_bytes=64)
+        wb0_all = once.tile([P, KV2], F32)
 
-        b32 = consts.tile([P, SUB], F32)
-        nc.vector.tensor_copy(out=b32[:], in_=b_bf[:])
-        w32 = consts.tile([P, SUB], F32)
-        nc.vector.tensor_copy(out=w32[:], in_=w_bf[:])
-        bw32 = consts.tile([P, SUB], F32)
-        nc.vector.tensor_tensor(out=bw32[:], in0=b32[:], in1=w32[:], op=ALU.mult)
-        sum_cols = consts.tile([P, SUB, 2], F32)
-        nc.vector.memset(sum_cols[:], 1.0)
-        nc.vector.tensor_tensor(out=sum_cols[:, :, 1], in0=w32[:], in1=w32[:], op=ALU.mult)
-        nsin_t = consts.tile([P, TABLE_HALVES, SUB, ROPE // 2], BF16)
-        nc.vector.tensor_scalar(out=nsin_t[:], in0=sin_t[:], scalar1=-1.0, scalar2=None, op0=ALU.mult)
+        def prepare_vectors():
+            vec_bank = psum_small.tile([P, 512], F32, tag="small")
+            nc.tensor.matmul(out=vec_bank[:], lhsT=ones_bf[:], rhs=vec_rows[:], start=True, stop=True)
+            nc.scalar.copy(out=bb_all[:], in_=vec_bank[:, 0:KV2])
+            nc.scalar.copy(out=bpe_all[:], in_=vec_bank[:, KV2 : KV2 + ROPE].rearrange("p (j e) -> p e j", e=2))
 
-        wb_even = consts.tile([P, 2, KV_RANK], BF16)
-        nc.vector.tensor_copy(out=wb_even[:], in_=wb_full[:, :, 1 : KV_RANK + 1])
-        wb_words = wb_even[:].bitcast(F32).rearrange("r o (q u) -> r o u q", u=2)
-        wb_flipped = psum.tile([P, 4, P], F32, tag="flip", bufs=2)
-        for o in range(2):
-            for u in range(2):
-                nc.tensor.transpose(wb_flipped[:, 2 * o + u, :], wb_words[:, o, u, :], ident[:])
-        wb_grouped = consts.tile([P, KV2, 4], BF16, align_bytes=64)
-        nc.scalar.copy(
-            out=wb_grouped[:].bitcast(F32).rearrange("q (o r) u -> q o r u", o=2),
-            in_=wb_flipped[:].rearrange("q (o u) r -> q o r u", u=2),
-        )
-        wb_codes = consts.tile([P, KV2], U32, align_bytes=64)
-        wb_scales = consts.tile([P, KV2], U8, align_bytes=64)
-        nc.vector.quantize_mx(
-            out=wb_codes[:].bitcast(FP8X4),
-            scales=wb_scales[:],
-            in_=wb_grouped[:].rearrange("q c t -> q (c t)"),
-        )
-
-        wb0_col = consts.tile([P, 2], F32)
-        nc.vector.tensor_copy(out=wb0_col[:], in_=wb_full[:, :, 0])
-        wb0_bank = psum.tile([P, 512], F32, tag="y", bufs=3)
-        for o in range(2):
-            nc.tensor.transpose(
-                wb0_bank[:, o * P : (o + 1) * P], wb0_col[:, o : o + 1].to_broadcast([P, P]), ident[:]
+        def prepare_wkv_b():
+            wb_even = once.tile([P, 2, KV_RANK], BF16)
+            nc.vector.tensor_copy(out=wb_even[:], in_=wb_full[:, :, 1 : KV_RANK + 1])
+            wb_words = wb_even[:].bitcast(F32).rearrange("r o (q u) -> r o u q", u=2)
+            wb_flipped = psum_flip.tile([P, 4, P], F32, tag="flip")
+            for o in range(2):
+                for u in range(2):
+                    nc.tensor.transpose(wb_flipped[:, 2 * o + u, :], wb_words[:, o, u, :], ident[:])
+            wb_grouped = once.tile([P, KV2, 4], BF16, align_bytes=64)
+            nc.scalar.copy(
+                out=wb_grouped[:].bitcast(F32).rearrange("q (o r) u -> q o r u", o=2),
+                in_=wb_flipped[:].rearrange("q (o u) r -> q o r u", u=2),
             )
-        wb0_all = consts.tile([P, KV2], F32)
-        nc.scalar.copy(out=wb0_all[:], in_=wb0_bank[:, 0:KV2])
-        vec_bank = psum.tile([P, 512], F32, tag="y", bufs=3)
-        nc.tensor.matmul(out=vec_bank[:], lhsT=ones_bf[:], rhs=vec_rows[:], start=True, stop=True)
-        bb_all = consts.tile([P, KV2], F32)
-        nc.scalar.copy(out=bb_all[:], in_=vec_bank[:, 0:KV2])
-        bpe_all = consts.tile([P, 2, ROPE // 2], F32)
-        nc.scalar.copy(out=bpe_all[:], in_=vec_bank[:, KV2 : KV2 + ROPE].rearrange("p (j e) -> p e j", e=2))
+            nc.vector.quantize_mx(
+                out=wb_codes[:].bitcast(FP8X4), scales=wb_scales[:], in_=wb_grouped[:].rearrange("q c j -> q (c j)")
+            )
+            wb0_col = once.tile([P, 2], F32)
+            nc.vector.tensor_copy(out=wb0_col[:], in_=wb_full[:, :, 0])
+            wb0_bank = psum_small.tile([P, 512], F32, tag="small")
+            for o in range(2):
+                nc.tensor.transpose(
+                    wb0_bank[:, o * P : (o + 1) * P], wb0_col[:, o : o + 1].to_broadcast([P, P]), ident[:]
+                )
+            nc.scalar.copy(out=wb0_all[:], in_=wb0_bank[:, 0:KV2])
 
         squares = {}
+        squares_rest = {}
         kv_w = {}
-        rope_in = {}
-        rstd = {}
-        time_sp = {}
-        sp_codes = {}
-        sp_scales = {}
-        ksl_sb = {}
-        vs_sb = {}
-        lift_sq = {}
 
-        def kv_banks(g):
-            sq = work.tile([P, SUB, GROUP], F32, tag="sq")
-            kw = work.tile([P, SUB, GROUP], F32, tag="kw", bufs=3)
-            for t in range(SUB):
-                y = psum.tile([P, GROUP], F32, tag="y", bufs=3)
-                for a in range(PASSES):
-                    nc.tensor.matmul_mx(
-                        out=y[:],
-                        lhsT=wa_kv_codes[:, a, t * P : (t + 1) * P].bitcast(FP8X4),
-                        lhsT_scale=wa_kv_scales[:, a, t * P : (t + 1) * P],
-                        rhs=x_codes[g][:, a, :].bitcast(FP8X4),
-                        rhs_scale=x_scales[g][:, a, :],
-                        start=(a == 0),
-                        stop=(a == PASSES - 1),
-                    )
-                nc.scalar.activation(out=sq[:, t, :], in_=y[:], func=ACT.Square, bias=b32[:, t : t + 1], scale=1.0)
-                nc.scalar.activation(
-                    out=kw[:, t, :], in_=y[:], func=ACT.Identity, bias=bw32[:, t : t + 1], scale=w32[:, t : t + 1]
+        def kv_bank(g, t):
+            if g == 0:
+                prepare_wa_tile(t)
+            if t == 0:
+                sq_new = twice.tile([P, SUB, GROUP], F32, tag="sq")
+                rest_new = twice.tile([P, SUB, GROUP], BF16, tag="sq_rest")
+                kw_new = four.tile([P, SUB, GROUP], F32, tag="kw")
+                squares[g] = sq_new
+                squares_rest[g] = rest_new
+                kv_w[g] = kw_new
+            sq = squares[g]
+            y = psum_y.tile([P, GROUP], F32, tag="y")
+            for a in range(PASSES):
+                nc.tensor.matmul_mx(
+                    out=y[:],
+                    lhsT=wa_kv_codes[:, a, t * P : (t + 1) * P].bitcast(FP8X4),
+                    lhsT_scale=wa_kv_scales[:, a, t * P : (t + 1) * P],
+                    rhs=x_codes[g][:, a, :].bitcast(FP8X4),
+                    rhs_scale=x_scales[g][:, a, :],
+                    start=(a == 0),
+                    stop=(a == PASSES - 1),
                 )
-            squares[g] = sq
-            kv_w[g] = kw
+            nc.scalar.activation(out=sq[:, t, :], in_=y[:], func=ACT.Square, bias=b32[:, t : t + 1], scale=1.0)
+            nc.scalar.activation(
+                out=kv_w[g][:, t, :], in_=y[:], func=ACT.Identity, bias=bw32[:, t : t + 1], scale=w32[:, t : t + 1]
+            )
+            nc.vector.tensor_tensor(
+                out=squares_rest[g][:, t, :], in0=sq[:, t, :], in1=upper_halves(sq)[:, t, :], op=ALU.subtract
+            )
+
+        def upper_halves(tile_f32):
+            return tile_f32[:].bitcast(BF16).rearrange("p t (c h) -> p t c h", h=2)[:, :, :, 1]
+
+        rope_in = {}
 
         def rope_columns(g):
-            pe = psum.tile([P, SUB, ROPE], F32, tag="small", bufs=2)
+            pe = psum_small.tile([P, SUB, ROPE], F32, tag="small")
             for n in range(SUB):
                 for a in range(PASSES):
                     nc.tensor.matmul_mx(
@@ -240,70 +255,81 @@ def tile_lorentzmla_pa_t_kernel(
                         start=(a == 0),
                         stop=(a == PASSES - 1),
                     )
-            pb = outs.tile([P, SUB, 2, ROPE // 2], F32, tag="pb")
+            pb = five.tile([P, SUB, 2, HALF], F32, tag="pb")
             nc.vector.tensor_tensor(
                 out=pb[:],
                 in0=pe[:].rearrange("p n (e j) -> p n e j", e=2),
-                in1=bpe_all[:].unsqueeze(1).to_broadcast([P, SUB, 2, ROPE // 2]),
+                in1=bpe_all[:].unsqueeze(1).to_broadcast([P, SUB, 2, HALF]),
                 op=ALU.add,
             )
             rope_in[g] = pb
 
         norm_sums = {}
-        inv_mean_sq = {}
-        sp_square_sum = {}
+        rstd = {}
+        time_sp = {}
 
-        def feature_sums(g):
-            sums = psum.tile([P, SUB, 2], F32, tag="norm", bufs=1)
-            for n in range(SUB):
+        def feature_sums(g, places):
+            if places[0] == 0:
+                sums_new = psum_norm.tile([P, SUB, 4], F32, tag="norm")
+                norm_sums[g] = sums_new
+            upper = upper_halves(squares[g])
+            for n in places:
                 for t in range(SUB):
                     nc.tensor.matmul(
-                        out=sums[:, n, :],
-                        lhsT=squares[g][:, t, n * P : (n + 1) * P],
+                        out=norm_sums[g][:, n, :],
+                        lhsT=upper[:, t, n * P : (n + 1) * P],
                         rhs=sum_cols[:, t, :],
                         start=(t == 0),
+                        stop=False,
+                    )
+                    nc.tensor.matmul(
+                        out=norm_sums[g][:, n, :],
+                        lhsT=squares_rest[g][:, t, n * P : (n + 1) * P],
+                        rhs=sum_cols[:, t, :],
+                        start=False,
                         stop=(t == SUB - 1),
                     )
-            norm_sums[g] = sums
 
-        def norm_scalars_vector(g):
+        def norm_scalars(g):
             sums = norm_sums[g]
-            mean_sq = outs.tile([P, SUB], F32, tag="mean_sq")
+            mean_sq = four.tile([P, SUB], F32, tag="mean_sq")
             nc.vector.tensor_scalar(
                 out=mean_sq[:], in0=sums[:, :, 0], scalar1=1.0 / KV_RANK, scalar2=EPS, op0=ALU.mult, op1=ALU.add
             )
-            inv_ms = outs.tile([P, SUB], F32, tag="inv_ms")
+            inv_ms = four.tile([P, SUB], F32, tag="inv_ms")
             nc.vector.reciprocal(out=inv_ms[:], in_=mean_sq[:])
-            sp_sq = outs.tile([P, SUB], F32, tag="sp_sq")
-            nc.vector.tensor_tensor(out=sp_sq[:], in0=sums[:, :, 1], in1=inv_ms[:], op=ALU.mult)
-            inv_mean_sq[g] = inv_ms
-            sp_square_sum[g] = sp_sq
-
-        def norm_scalars_scalar(g):
-            inv_ms = inv_mean_sq[g]
-            sp_sq = sp_square_sum[g]
-            rs = outs.tile([P, SUB], F32, tag="rs")
+            kw_sq = four.tile([P, SUB], F32, tag="kw_sq")
+            nc.vector.tensor_reduce(out=kw_sq[:], in_=sums[:, :, 1:3], axis=AXIS.X, op=ALU.add)
+            sp_sq = four.tile([P, SUB], F32, tag="sp_sq")
+            nc.vector.tensor_tensor(out=sp_sq[:], in0=kw_sq[:], in1=inv_ms[:], op=ALU.mult)
+            rs = four.tile([P, SUB], F32, tag="rs")
             nc.scalar.activation(out=rs[:], in_=inv_ms[:], func=ACT.Sqrt)
-            tm = outs.tile([P, SUB], F32, tag="tm")
+            tm = four.tile([P, SUB], F32, tag="tm")
             nc.scalar.activation(out=tm[:], in_=sp_sq[:], func=ACT.Sqrt, bias=1.0, scale=1.0)
             rstd[g] = rs
             time_sp[g] = tm
 
+        sp_codes = {}
+        sp_scales = {}
+        ksl_sb = {}
+        vs_sb = {}
+        lift_sq = {}
+
         def norm(g):
-            spread = psum.tile([P, GROUP], F32, tag="norm", bufs=1)
+            spread = psum_norm.tile([P, GROUP], F32, tag="norm")
             for n in range(SUB):
                 nc.tensor.transpose(
                     spread[:, n * P : (n + 1) * P], rstd[g][:, n : n + 1].to_broadcast([P, P]), ident[:]
                 )
-            sp_grouped = work.tile([P, GROUP, SUB], BF16, tag="sp_grouped", align_bytes=64)
+            sp_grouped = once.tile([P, GROUP, SUB], BF16, tag="sp_grouped", align_bytes=64)
             nc.vector.tensor_tensor(
                 out=sp_grouped[:],
                 in0=kv_w[g][:].rearrange("p t c -> p c t"),
                 in1=spread[:].unsqueeze(2).to_broadcast([P, GROUP, SUB]),
                 op=ALU.mult,
             )
-            codes = work.tile([P, GROUP], U32, tag="sp_codes", align_bytes=64)
-            scales = work.tile([P, GROUP], U8, tag="sp_scales", align_bytes=64)
+            codes = twice.tile([P, GROUP], U32, tag="sp_codes", align_bytes=64)
+            scales = twice.tile([P, GROUP], U8, tag="sp_scales", align_bytes=64)
             nc.vector.quantize_mx(
                 out=codes[:].bitcast(FP8X4), scales=scales[:], in_=sp_grouped[:].rearrange("p c t -> p (c t)")
             )
@@ -313,18 +339,18 @@ def tile_lorentzmla_pa_t_kernel(
         kv2_sb = {}
 
         def rope_rotate(g):
-            ksl = outs.tile([P, SUB, HEADS, K_ROW], F32, tag="ksl", bufs=4)
+            ksl = four.tile([P, SUB, HEADS, K_ROW], F32, tag="ksl")
             ksl_sb[g] = ksl
             half = g % TABLE_HALVES
             pb = rope_in[g]
-            by_cos = work.tile([P, SUB, 2, ROPE // 2], F32, tag="by_cos")
+            by_cos = once.tile([P, SUB, 2, HALF], F32, tag="by_cos")
             nc.gpsimd.tensor_tensor(
                 out=by_cos[:],
                 in0=pb[:],
-                in1=cos_t[:, half, :, :].unsqueeze(2).to_broadcast([P, SUB, 2, ROPE // 2]),
+                in1=cos_t[:, half, :, :].unsqueeze(2).to_broadcast([P, SUB, 2, HALF]),
                 op=ALU.mult,
             )
-            by_sin = work.tile([P, SUB, 2, ROPE // 2], F32, tag="by_sin")
+            by_sin = once.tile([P, SUB, 2, HALF], F32, tag="by_sin")
             nc.gpsimd.tensor_tensor(out=by_sin[:, :, 0, :], in0=pb[:, :, 1, :], in1=nsin_t[:, half, :, :], op=ALU.mult)
             nc.gpsimd.tensor_tensor(out=by_sin[:, :, 1, :], in0=pb[:, :, 0, :], in1=sin_t[:, half, :, :], op=ALU.mult)
             nc.gpsimd.tensor_tensor(
@@ -343,9 +369,9 @@ def tile_lorentzmla_pa_t_kernel(
             )
 
         def second_product(g):
-            kv2 = work.tile([P, SUB, HEADS, NOPE + V_DIM], F32, tag="kv2")
+            kv2 = twice.tile([P, SUB, HEADS, NOPE + V_DIM], F32, tag="kv2")
             for pair in range(SUB // 2):
-                bank = psum.tile([P, 2, KV2], F32, tag="small", bufs=2)
+                bank = psum_small.tile([P, 2, KV2], F32, tag="small")
                 for i in range(2):
                     n = 2 * pair + i
                     nc.tensor.matmul_mx(
@@ -370,7 +396,7 @@ def tile_lorentzmla_pa_t_kernel(
         def add_second_bias(g):
             kv2 = kv2_sb[g]
             ksl = ksl_sb[g]
-            vs = outs.tile([P, SUB, HEADS, V_ROW], F32, tag="vs", bufs=4)
+            vs = four.tile([P, SUB, HEADS, V_ROW], F32, tag="vs")
             vs_sb[g] = vs
             bb4 = bb_all[:].rearrange("p (h c) -> p h c", h=HEADS).unsqueeze(1).to_broadcast([P, SUB, HEADS, NOPE + V_DIM])
             nc.gpsimd.tensor_tensor(
@@ -383,7 +409,7 @@ def tile_lorentzmla_pa_t_kernel(
         def lift_squares(g):
             ksl = ksl_sb[g]
             vs = vs_sb[g]
-            lsq = work.tile([P, SUB, 6, 64], F32, tag="lsq")
+            lsq = twice.tile([P, SUB, 6, 64], F32, tag="lsq")
             nc.scalar.activation(out=lsq[:, :, 0:2, :], in_=ksl[:, :, :, 1 : 1 + NOPE], func=ACT.Square)
             nc.scalar.activation(
                 out=lsq[:, :, 2:4, :].rearrange("p n b c -> p n (b c)"), in_=ksl[:, :, 1, 1 + NOPE : K_ROW], func=ACT.Square
@@ -395,16 +421,16 @@ def tile_lorentzmla_pa_t_kernel(
         lift_all = {}
 
         def lift_sums(g):
-            sums = outs.tile([P, SUB, 6], F32, tag="lift_sums")
+            sums = four.tile([P, SUB, 6], F32, tag="lift_sums")
             nc.vector.tensor_reduce(
                 out=sums[:].rearrange("p n b -> p (n b)"),
                 in_=lift_sq[g][:].rearrange("p n b c -> p (n b) c"),
                 axis=AXIS.X,
                 op=ALU.add,
             )
-            rope_sum = outs.tile([P, SUB], F32, tag="rope_sum")
+            rope_sum = four.tile([P, SUB], F32, tag="rope_sum")
             nc.vector.tensor_tensor(out=rope_sum[:], in0=sums[:, :, 2], in1=sums[:, :, 3], op=ALU.add)
-            k_sum = outs.tile([P, SUB, HEADS], F32, tag="k_sum")
+            k_sum = four.tile([P, SUB, HEADS], F32, tag="k_sum")
             nc.vector.tensor_tensor(
                 out=k_sum[:], in0=sums[:, :, 0:2], in1=rope_sum[:].unsqueeze(2).to_broadcast([P, SUB, HEADS]), op=ALU.add
             )
@@ -420,34 +446,45 @@ def tile_lorentzmla_pa_t_kernel(
         def live(g):
             return 0 <= g < GROUPS
 
-        for i in range(GROUPS + 4):
-            if live(i):
-                kv_banks(i)
-            if live(i - 2):
-                rope_rotate(i - 2)
-                second_product(i - 2)
-                add_second_bias(i - 2)
-            if live(i):
-                rope_columns(i)
-            if live(i + 4):
+        for i in range(-1, GROUPS + 5):
+            if live(i + 4) and i >= 0:
                 load_x(i + 4)
+            if live(i - 3):
+                rope_rotate(i - 3)
             if live(i + 1):
                 flip_x(i + 1, (0, 1))
-            if live(i - 1):
-                feature_sums(i - 1)
+            if live(i):
+                kv_bank(i, 0)
             if live(i - 4):
-                lift_sums(i - 4)
+                add_second_bias(i - 4)
+            if live(i - 3):
+                second_product(i - 3)
             if live(i - 1):
-                norm_scalars_vector(i - 1)
+                feature_sums(i - 1, (0, 1))
+            if live(i):
+                kv_bank(i, 1)
+            if live(i - 4):
+                lift_squares(i - 4)
+            if live(i - 1):
+                feature_sums(i - 1, (2, 3))
             if live(i + 1):
                 flip_x(i + 1, (2, 3))
             if live(i - 1):
-                norm_scalars_scalar(i - 1)
+                norm_scalars(i - 1)
+            if i == 0:
+                prepare_wa_rope()
+                prepare_vectors()
+                prepare_wkv_b()
+            if live(i - 1):
+                rope_columns(i - 1)
+            if live(i - 5):
+                lift_roots_and_store(i - 5)
+            if live(i - 4):
+                lift_sums(i - 4)
             if live(i + 1):
                 quantise_x(i + 1)
+            if live(i):
+                kv_bank(i, 2)
+                kv_bank(i, 3)
             if live(i - 1):
                 norm(i - 1)
-            if live(i - 3):
-                lift_squares(i - 3)
-            if live(i - 4):
-                lift_roots_and_store(i - 4)

@@ -51,7 +51,6 @@ def tile_lorentzmla_pa_t_kernel(
         psum_y = ctx.enter_context(tc.psum_pool(name="psum_y", bufs=2))
         psum_small = ctx.enter_context(tc.psum_pool(name="psum_small", bufs=2))
         psum_norm = ctx.enter_context(tc.psum_pool(name="psum_norm", bufs=2))
-        ctx.enter_context(tc.manual_schedule())
 
         x_sb = {}
 

@@ -45,12 +45,14 @@ def tile_lorentzmla_pa_t_kernel(
     with ExitStack() as ctx:
         once = ctx.enter_context(tc.tile_pool(name="once", bufs=1))
         twice = ctx.enter_context(tc.tile_pool(name="twice", bufs=2))
-        four = ctx.enter_context(tc.tile_pool(name="four", bufs=4))
+        three = ctx.enter_context(tc.tile_pool(name="three", bufs=3))
         five = ctx.enter_context(tc.tile_pool(name="five", bufs=5))
         psum_flip = ctx.enter_context(tc.psum_pool(name="psum_flip", bufs=2))
         psum_y = ctx.enter_context(tc.psum_pool(name="psum_y", bufs=2))
-        psum_small = ctx.enter_context(tc.psum_pool(name="psum_small", bufs=2))
-        psum_norm = ctx.enter_context(tc.psum_pool(name="psum_norm", bufs=2))
+        psum_small = ctx.enter_context(tc.psum_pool(name="psum_small", bufs=1))
+        psum_kv2 = ctx.enter_context(tc.psum_pool(name="psum_kv2", bufs=1))
+        psum_norm = ctx.enter_context(tc.psum_pool(name="psum_norm", bufs=1))
+        psum_spread = ctx.enter_context(tc.psum_pool(name="psum_spread", bufs=1))
 
         x_sb = {}
 
@@ -107,21 +109,21 @@ def tile_lorentzmla_pa_t_kernel(
         nsin_t = once.tile([P, TABLE_HALVES, SUB, HALF], BF16)
         nc.vector.tensor_scalar(out=nsin_t[:], in0=sin_t[:], scalar1=-1.0, scalar2=None, op0=ALU.mult)
 
-        def flip_place(rows_sb, grouped, n):
+        def flip_place(rows_sb, grouped, n, copy):
             rows_words = rows_sb[:].bitcast(F32)[:, n, :]
             flipped = psum_flip.tile([P, 4, P], F32, tag="flip")
             for c in range(4):
                 nc.tensor.transpose(flipped[:, c, :], rows_words[:, c * P : (c + 1) * P], ident[:])
-            nc.scalar.copy(
-                out=grouped[:].bitcast(F32)[:, :, n, :, :], in_=flipped[:].rearrange("q (a u) r -> q a r u", u=2)
-            )
+            copy(out=grouped[:].bitcast(F32)[:, :, n, :, :], in_=flipped[:].rearrange("q (a u) r -> q a r u", u=2))
 
         wa_kv_codes = once.tile([P, PASSES, KV_RANK], U32, align_bytes=64)
         wa_kv_scales = once.tile([P, PASSES, KV_RANK], U8, align_bytes=64)
         wa_grouped = once.tile([P, PASSES, SUB, P, 4], BF16, align_bytes=64)
 
-        def prepare_wa_tile(t):
-            flip_place(wa_kv_sb, wa_grouped, t)
+        def flip_wa(t):
+            flip_place(wa_kv_sb, wa_grouped, t, nc.vector.tensor_copy)
+
+        def quantise_wa(t):
             for a in range(PASSES):
                 nc.vector.quantize_mx(
                     out=wa_kv_codes[:, a, t * P : (t + 1) * P].bitcast(FP8X4),
@@ -133,8 +135,10 @@ def tile_lorentzmla_pa_t_kernel(
         wa_pe_scales = once.tile([P, PASSES, ROPE], U8, align_bytes=64)
         pe_grouped = once.tile([P, PASSES, 1, P, 4], BF16, align_bytes=64)
 
-        def prepare_wa_rope():
-            flip_place(wa_pe_sb, pe_grouped, 0)
+        def flip_wa_rope():
+            flip_place(wa_pe_sb, pe_grouped, 0, nc.vector.tensor_copy)
+
+        def quantise_wa_rope():
             for a in range(PASSES):
                 nc.vector.quantize_mx(
                     out=wa_pe_codes[:, a, :].bitcast(FP8X4),
@@ -146,12 +150,11 @@ def tile_lorentzmla_pa_t_kernel(
         x_codes = {}
         x_scales = {}
 
-        def flip_x(g, places):
-            if places[0] == 0:
+        def flip_x(g, n):
+            if n == 0:
                 grouped = twice.tile([P, PASSES, SUB, P, 4], BF16, tag="grouped", align_bytes=64)
                 x_grouped[g] = grouped
-            for n in places:
-                flip_place(x_sb[g], x_grouped[g], n)
+            flip_place(x_sb[g], x_grouped[g], n, nc.scalar.copy)
 
         def quantise_x(g):
             codes = twice.tile([P, PASSES, GROUP], U32, tag="x_codes", align_bytes=64)
@@ -172,10 +175,10 @@ def tile_lorentzmla_pa_t_kernel(
         wb0_all = once.tile([P, KV2], F32)
 
         def prepare_vectors():
-            vec_bank = psum_small.tile([P, 512], F32, tag="small")
+            vec_bank = psum_kv2.tile([P, 512], F32, tag="kv2")
             nc.tensor.matmul(out=vec_bank[:], lhsT=ones_bf[:], rhs=vec_rows[:], start=True, stop=True)
-            nc.scalar.copy(out=bb_all[:], in_=vec_bank[:, 0:KV2])
-            nc.scalar.copy(out=bpe_all[:], in_=vec_bank[:, KV2 : KV2 + ROPE].rearrange("p (j e) -> p e j", e=2))
+            nc.vector.tensor_copy(out=bb_all[:], in_=vec_bank[:, 0:KV2])
+            nc.vector.tensor_copy(out=bpe_all[:], in_=vec_bank[:, KV2 : KV2 + ROPE].rearrange("p (j e) -> p e j", e=2))
 
         def prepare_wkv_b():
             wb_even = once.tile([P, 2, KV_RANK], BF16)
@@ -186,7 +189,7 @@ def tile_lorentzmla_pa_t_kernel(
                 for u in range(2):
                     nc.tensor.transpose(wb_flipped[:, 2 * o + u, :], wb_words[:, o, u, :], ident[:])
             wb_grouped = once.tile([P, KV2, 4], BF16, align_bytes=64)
-            nc.scalar.copy(
+            nc.vector.tensor_copy(
                 out=wb_grouped[:].bitcast(F32).rearrange("q (o r) u -> q o r u", o=2),
                 in_=wb_flipped[:].rearrange("q (o u) r -> q o r u", u=2),
             )
@@ -195,28 +198,19 @@ def tile_lorentzmla_pa_t_kernel(
             )
             wb0_col = once.tile([P, 2], F32)
             nc.vector.tensor_copy(out=wb0_col[:], in_=wb_full[:, :, 0])
-            wb0_bank = psum_small.tile([P, 512], F32, tag="small")
+            wb0_bank = psum_kv2.tile([P, 512], F32, tag="kv2")
             for o in range(2):
                 nc.tensor.transpose(
                     wb0_bank[:, o * P : (o + 1) * P], wb0_col[:, o : o + 1].to_broadcast([P, P]), ident[:]
                 )
-            nc.scalar.copy(out=wb0_all[:], in_=wb0_bank[:, 0:KV2])
+            nc.vector.tensor_copy(out=wb0_all[:], in_=wb0_bank[:, 0:KV2])
 
         squares = {}
         squares_rest = {}
         kv_w = {}
+        kv_y = {}
 
-        def kv_bank(g, t):
-            if g == 0:
-                prepare_wa_tile(t)
-            if t == 0:
-                sq_new = twice.tile([P, SUB, GROUP], F32, tag="sq")
-                rest_new = twice.tile([P, SUB, GROUP], BF16, tag="sq_rest")
-                kw_new = four.tile([P, SUB, GROUP], F32, tag="kw")
-                squares[g] = sq_new
-                squares_rest[g] = rest_new
-                kv_w[g] = kw_new
-            sq = squares[g]
+        def kv_product(g, t):
             y = psum_y.tile([P, GROUP], F32, tag="y")
             for a in range(PASSES):
                 nc.tensor.matmul_mx(
@@ -228,20 +222,56 @@ def tile_lorentzmla_pa_t_kernel(
                     start=(a == 0),
                     stop=(a == PASSES - 1),
                 )
-            nc.scalar.activation(out=sq[:, t, :], in_=y[:], func=ACT.Square, bias=b32[:, t : t + 1], scale=1.0)
+            kv_y[g, t] = y
+
+        def kv_square(g, t):
+            if t == 0:
+                sq_new = twice.tile([P, SUB, GROUP], F32, tag="sq")
+                squares[g] = sq_new
             nc.scalar.activation(
-                out=kv_w[g][:, t, :], in_=y[:], func=ACT.Identity, bias=bw32[:, t : t + 1], scale=w32[:, t : t + 1]
+                out=squares[g][:, t, :], in_=kv_y[g, t][:], func=ACT.Square, bias=b32[:, t : t + 1], scale=1.0
             )
-            nc.vector.tensor_tensor(
-                out=squares_rest[g][:, t, :], in0=sq[:, t, :], in1=upper_halves(sq)[:, t, :], op=ALU.subtract
-            )
+
+        def kv_weighted(g, t, on_vector):
+            if t == 0:
+                kw_new = three.tile([P, SUB, GROUP], F32, tag="kw")
+                kv_w[g] = kw_new
+            if on_vector:
+                nc.vector.tensor_scalar(
+                    out=kv_w[g][:, t, :],
+                    in0=kv_y[g, t][:],
+                    scalar1=w32[:, t : t + 1],
+                    scalar2=bw32[:, t : t + 1],
+                    op0=ALU.mult,
+                    op1=ALU.add,
+                )
+            else:
+                nc.scalar.activation(
+                    out=kv_w[g][:, t, :],
+                    in_=kv_y[g, t][:],
+                    func=ACT.Identity,
+                    bias=bw32[:, t : t + 1],
+                    scale=w32[:, t : t + 1],
+                )
 
         def upper_halves(tile_f32):
             return tile_f32[:].bitcast(BF16).rearrange("p t (c h) -> p t c h", h=2)[:, :, :, 1]
 
+        def square_rest(g, t):
+            if t == 0:
+                rest_new = twice.tile([P, SUB, GROUP], BF16, tag="sq_rest")
+                squares_rest[g] = rest_new
+            nc.vector.tensor_tensor(
+                out=squares_rest[g][:, t, :],
+                in0=squares[g][:, t, :],
+                in1=upper_halves(squares[g])[:, t, :],
+                op=ALU.subtract,
+            )
+
+        rope_pe = {}
         rope_in = {}
 
-        def rope_columns(g):
+        def rope_product(g):
             pe = psum_small.tile([P, SUB, ROPE], F32, tag="small")
             for n in range(SUB):
                 for a in range(PASSES):
@@ -254,10 +284,13 @@ def tile_lorentzmla_pa_t_kernel(
                         start=(a == 0),
                         stop=(a == PASSES - 1),
                     )
-            pb = five.tile([P, SUB, 2, HALF], F32, tag="pb")
+            rope_pe[g] = pe
+
+        def rope_bias(g):
+            pb = three.tile([P, SUB, 2, HALF], F32, tag="pb")
             nc.vector.tensor_tensor(
                 out=pb[:],
-                in0=pe[:].rearrange("p n (e j) -> p n e j", e=2),
+                in0=rope_pe[g][:].rearrange("p n (e j) -> p n e j", e=2),
                 in1=bpe_all[:].unsqueeze(1).to_broadcast([P, SUB, 2, HALF]),
                 op=ALU.add,
             )
@@ -265,97 +298,109 @@ def tile_lorentzmla_pa_t_kernel(
 
         norm_sums = {}
         rstd = {}
+        kw_sums = {}
         time_sp = {}
 
-        def feature_sums(g, places):
-            if places[0] == 0:
+        def feature_sums(g, n):
+            if n == 0:
                 sums_new = psum_norm.tile([P, SUB, 4], F32, tag="norm")
                 norm_sums[g] = sums_new
             upper = upper_halves(squares[g])
-            for n in places:
-                for t in range(SUB):
-                    nc.tensor.matmul(
-                        out=norm_sums[g][:, n, :],
-                        lhsT=upper[:, t, n * P : (n + 1) * P],
-                        rhs=sum_cols[:, t, :],
-                        start=(t == 0),
-                        stop=False,
-                    )
-                    nc.tensor.matmul(
-                        out=norm_sums[g][:, n, :],
-                        lhsT=squares_rest[g][:, t, n * P : (n + 1) * P],
-                        rhs=sum_cols[:, t, :],
-                        start=False,
-                        stop=(t == SUB - 1),
-                    )
+            for t in range(SUB):
+                nc.tensor.matmul(
+                    out=norm_sums[g][:, n, :],
+                    lhsT=upper[:, t, n * P : (n + 1) * P],
+                    rhs=sum_cols[:, t, :],
+                    start=(t == 0),
+                    stop=False,
+                )
+                nc.tensor.matmul(
+                    out=norm_sums[g][:, n, :],
+                    lhsT=squares_rest[g][:, t, n * P : (n + 1) * P],
+                    rhs=sum_cols[:, t, :],
+                    start=False,
+                    stop=(t == SUB - 1),
+                )
 
-        def norm_scalars(g):
-            sums = norm_sums[g]
-            mean_sq = four.tile([P, SUB], F32, tag="mean_sq")
-            nc.vector.tensor_scalar(
-                out=mean_sq[:], in0=sums[:, :, 0], scalar1=1.0 / KV_RANK, scalar2=EPS, op0=ALU.mult, op1=ALU.add
-            )
-            inv_ms = four.tile([P, SUB], F32, tag="inv_ms")
-            nc.vector.reciprocal(out=inv_ms[:], in_=mean_sq[:])
-            kw_sq = four.tile([P, SUB], F32, tag="kw_sq")
-            nc.vector.tensor_reduce(out=kw_sq[:], in_=sums[:, :, 1:3], axis=AXIS.X, op=ALU.add)
-            sp_sq = four.tile([P, SUB], F32, tag="sp_sq")
-            nc.vector.tensor_tensor(out=sp_sq[:], in0=kw_sq[:], in1=inv_ms[:], op=ALU.mult)
-            rs = four.tile([P, SUB], F32, tag="rs")
-            nc.scalar.activation(out=rs[:], in_=inv_ms[:], func=ACT.Sqrt)
-            tm = four.tile([P, SUB], F32, tag="tm")
-            nc.scalar.activation(out=tm[:], in_=sp_sq[:], func=ACT.Sqrt, bias=1.0, scale=1.0)
+        def norm_root(g):
+            rms = three.tile([P, SUB], F32, tag="rms")
+            nc.scalar.activation(out=rms[:], in_=norm_sums[g][:, :, 0], func=ACT.Sqrt, bias=EPS, scale=1.0 / KV_RANK)
+            rs = three.tile([P, SUB], F32, tag="rs")
+            nc.vector.reciprocal(out=rs[:], in_=rms[:])
             rstd[g] = rs
+            kw_sq = three.tile([P, SUB], F32, tag="kw_sq")
+            nc.vector.tensor_reduce(out=kw_sq[:], in_=norm_sums[g][:, :, 1:3], axis=AXIS.X, op=ALU.add)
+            kw_sums[g] = kw_sq
+
+        def time_root(g):
+            inv_ms = three.tile([P, SUB], F32, tag="inv_ms")
+            nc.gpsimd.tensor_tensor(out=inv_ms[:], in0=rstd[g][:], in1=rstd[g][:], op=ALU.mult)
+            sp_sq = three.tile([P, SUB], F32, tag="sp_sq")
+            nc.gpsimd.tensor_tensor(out=sp_sq[:], in0=kw_sums[g][:], in1=inv_ms[:], op=ALU.mult)
+            tm = three.tile([P, SUB], F32, tag="tm")
+            nc.scalar.activation(out=tm[:], in_=sp_sq[:], func=ACT.Sqrt, bias=1.0, scale=1.0)
             time_sp[g] = tm
 
+        sp_rows = {}
         sp_codes = {}
         sp_scales = {}
-        ksl_sb = {}
-        vs_sb = {}
-        lift_sq = {}
+        spread_of = {}
 
-        def norm(g):
-            spread = psum_norm.tile([P, GROUP], F32, tag="norm")
+        def spread_rstd(g):
+            spread = psum_spread.tile([P, GROUP], F32, tag="spread")
             for n in range(SUB):
                 nc.tensor.transpose(
                     spread[:, n * P : (n + 1) * P], rstd[g][:, n : n + 1].to_broadcast([P, P]), ident[:]
                 )
+            spread_of[g] = spread
+
+        def norm(g):
             sp_grouped = once.tile([P, GROUP, SUB], BF16, tag="sp_grouped", align_bytes=64)
             nc.vector.tensor_tensor(
                 out=sp_grouped[:],
                 in0=kv_w[g][:].rearrange("p t c -> p c t"),
-                in1=spread[:].unsqueeze(2).to_broadcast([P, GROUP, SUB]),
+                in1=spread_of[g][:].unsqueeze(2).to_broadcast([P, GROUP, SUB]),
                 op=ALU.mult,
             )
+            sp_rows[g] = sp_grouped
+
+        def quantise_sp(g):
             codes = twice.tile([P, GROUP], U32, tag="sp_codes", align_bytes=64)
             scales = twice.tile([P, GROUP], U8, tag="sp_scales", align_bytes=64)
             nc.vector.quantize_mx(
-                out=codes[:].bitcast(FP8X4), scales=scales[:], in_=sp_grouped[:].rearrange("p c t -> p (c t)")
+                out=codes[:].bitcast(FP8X4), scales=scales[:], in_=sp_rows[g][:].rearrange("p c t -> p (c t)")
             )
             sp_codes[g] = codes
             sp_scales[g] = scales
 
-        kv2_sb = {}
+        ksl_sb = {}
+        vs_sb = {}
+        by_cos = {}
+        by_sin = {}
 
-        def rope_rotate(g):
-            ksl = four.tile([P, SUB, HEADS, K_ROW], F32, tag="ksl")
-            ksl_sb[g] = ksl
+        def rope_products(g):
             half = g % TABLE_HALVES
             pb = rope_in[g]
-            by_cos = once.tile([P, SUB, 2, HALF], F32, tag="by_cos")
+            cos_new = once.tile([P, SUB, 2, HALF], F32, tag="by_cos")
             nc.gpsimd.tensor_tensor(
-                out=by_cos[:],
+                out=cos_new[:],
                 in0=pb[:],
                 in1=cos_t[:, half, :, :].unsqueeze(2).to_broadcast([P, SUB, 2, HALF]),
                 op=ALU.mult,
             )
-            by_sin = once.tile([P, SUB, 2, HALF], F32, tag="by_sin")
-            nc.gpsimd.tensor_tensor(out=by_sin[:, :, 0, :], in0=pb[:, :, 1, :], in1=nsin_t[:, half, :, :], op=ALU.mult)
-            nc.gpsimd.tensor_tensor(out=by_sin[:, :, 1, :], in0=pb[:, :, 0, :], in1=sin_t[:, half, :, :], op=ALU.mult)
+            sin_new = once.tile([P, SUB, 2, HALF], F32, tag="by_sin")
+            nc.gpsimd.tensor_tensor(out=sin_new[:, :, 0, :], in0=pb[:, :, 1, :], in1=nsin_t[:, half, :, :], op=ALU.mult)
+            nc.gpsimd.tensor_tensor(out=sin_new[:, :, 1, :], in0=pb[:, :, 0, :], in1=sin_t[:, half, :, :], op=ALU.mult)
+            by_cos[g] = cos_new
+            by_sin[g] = sin_new
+
+        def rope_rows(g):
+            ksl = three.tile([P, SUB, HEADS, K_ROW], F32, tag="ksl")
+            ksl_sb[g] = ksl
             nc.gpsimd.tensor_tensor(
                 out=ksl[:, :, 0, 1 + NOPE : K_ROW].rearrange("p n (j e) -> p n j e", e=2),
-                in0=by_cos[:].rearrange("p n e j -> p n j e"),
-                in1=by_sin[:].rearrange("p n e j -> p n j e"),
+                in0=by_cos[g][:].rearrange("p n e j -> p n j e"),
+                in1=by_sin[g][:].rearrange("p n e j -> p n j e"),
                 op=ALU.add,
             )
             nc.gpsimd.tensor_scalar(
@@ -367,35 +412,43 @@ def tile_lorentzmla_pa_t_kernel(
                 op1=ALU.add,
             )
 
-        def second_product(g):
-            kv2 = twice.tile([P, SUB, HEADS, NOPE + V_DIM], F32, tag="kv2")
-            for pair in range(SUB // 2):
-                bank = psum_small.tile([P, 2, KV2], F32, tag="small")
-                for i in range(2):
-                    n = 2 * pair + i
-                    nc.tensor.matmul_mx(
-                        out=bank[:, i, :],
-                        lhsT=sp_codes[g][:, n * P : (n + 1) * P].bitcast(FP8X4),
-                        lhsT_scale=sp_scales[g][:, n * P : (n + 1) * P],
-                        rhs=wb_codes[:].bitcast(FP8X4),
-                        rhs_scale=wb_scales[:],
-                        start=True,
-                        stop=True,
-                    )
-                    nc.vector.scalar_tensor_tensor(
-                        out=kv2[:, n, :, :].rearrange("p h c -> p (h c)"),
-                        in0=wb0_all[:],
-                        scalar=time_sp[g][:, n : n + 1],
-                        in1=bank[:, i, :],
-                        op0=ALU.mult,
-                        op1=ALU.add,
-                    )
-            kv2_sb[g] = kv2
+        kv2_sb = {}
+        kv2_banks = {}
+
+        def second_product(g, pair):
+            bank = psum_kv2.tile([P, 2, KV2], F32, tag="kv2")
+            for i in range(2):
+                n = 2 * pair + i
+                nc.tensor.matmul_mx(
+                    out=bank[:, i, :],
+                    lhsT=sp_codes[g][:, n * P : (n + 1) * P].bitcast(FP8X4),
+                    lhsT_scale=sp_scales[g][:, n * P : (n + 1) * P],
+                    rhs=wb_codes[:].bitcast(FP8X4),
+                    rhs_scale=wb_scales[:],
+                    start=True,
+                    stop=True,
+                )
+            kv2_banks[g, pair] = bank
+
+        def add_time_term(g, pair):
+            if pair == 0:
+                kv2_new = twice.tile([P, SUB, HEADS, NOPE + V_DIM], F32, tag="kv2_rows")
+                kv2_sb[g] = kv2_new
+            for i in range(2):
+                n = 2 * pair + i
+                nc.vector.scalar_tensor_tensor(
+                    out=kv2_sb[g][:, n, :, :].rearrange("p h c -> p (h c)"),
+                    in0=wb0_all[:],
+                    scalar=time_sp[g][:, n : n + 1],
+                    in1=kv2_banks[g, pair][:, i, :],
+                    op0=ALU.mult,
+                    op1=ALU.add,
+                )
 
         def add_second_bias(g):
             kv2 = kv2_sb[g]
             ksl = ksl_sb[g]
-            vs = four.tile([P, SUB, HEADS, V_ROW], F32, tag="vs")
+            vs = three.tile([P, SUB, HEADS, V_ROW], F32, tag="vs")
             vs_sb[g] = vs
             bb4 = bb_all[:].rearrange("p (h c) -> p h c", h=HEADS).unsqueeze(1).to_broadcast([P, SUB, HEADS, NOPE + V_DIM])
             nc.gpsimd.tensor_tensor(
@@ -405,85 +458,98 @@ def tile_lorentzmla_pa_t_kernel(
                 out=vs[:, :, :, 1:V_ROW], in0=kv2[:, :, :, NOPE : NOPE + V_DIM], in1=bb4[:, :, :, NOPE : NOPE + V_DIM], op=ALU.add
             )
 
-        def lift_squares(g):
-            ksl = ksl_sb[g]
-            vs = vs_sb[g]
-            lsq = twice.tile([P, SUB, 6, 64], F32, tag="lsq")
-            nc.scalar.activation(out=lsq[:, :, 0:2, :], in_=ksl[:, :, :, 1 : 1 + NOPE], func=ACT.Square)
-            nc.scalar.activation(
-                out=lsq[:, :, 2:4, :].rearrange("p n b c -> p n (b c)"), in_=ksl[:, :, 1, 1 + NOPE : K_ROW], func=ACT.Square
-            )
-            nc.scalar.activation(out=lsq[:, :, 4:6, :], in_=vs[:, :, :, 1:V_ROW], func=ACT.Square)
-            lift_sq[g] = lsq
+        lift_sums = {}
 
-        lift_k = {}
-        lift_all = {}
-
-        def lift_sums(g):
-            sums = four.tile([P, SUB, 6], F32, tag="lift_sums")
-            nc.vector.tensor_reduce(
-                out=sums[:].rearrange("p n b -> p (n b)"),
-                in_=lift_sq[g][:].rearrange("p n b c -> p (n b) c"),
-                axis=AXIS.X,
-                op=ALU.add,
-            )
-            rope_sum = four.tile([P, SUB], F32, tag="rope_sum")
-            nc.vector.tensor_tensor(out=rope_sum[:], in0=sums[:, :, 2], in1=sums[:, :, 3], op=ALU.add)
-            k_sum = four.tile([P, SUB, HEADS], F32, tag="k_sum")
-            nc.vector.tensor_tensor(
-                out=k_sum[:], in0=sums[:, :, 0:2], in1=rope_sum[:].unsqueeze(2).to_broadcast([P, SUB, HEADS]), op=ALU.add
-            )
-            lift_k[g] = k_sum
-            lift_all[g] = sums
+        def lift_squares(g, n):
+            if n == 0:
+                sums_new = three.tile([P, 2, SUB, HEADS], F32, tag="lift_sums")
+                lift_sums[g] = sums_new
+            sums = lift_sums[g]
+            for h in range(HEADS):
+                junk = twice.tile([P, K_ROW - 1], BF16, tag="junk")
+                nc.scalar.activation(
+                    out=junk[:], in_=ksl_sb[g][:, n, h, 1:K_ROW], func=ACT.Square, accum_out=sums[:, 0, n, h : h + 1]
+                )
+                junk_v = twice.tile([P, V_DIM], BF16, tag="junk_v")
+                nc.scalar.activation(
+                    out=junk_v[:], in_=vs_sb[g][:, n, h, 1:V_ROW], func=ACT.Square, accum_out=sums[:, 1, n, h : h + 1]
+                )
 
         def lift_roots_and_store(g):
-            nc.scalar.activation(out=ksl_sb[g][:, :, :, 0], in_=lift_k[g][:], func=ACT.Sqrt, bias=1.0, scale=1.0)
-            nc.scalar.activation(out=vs_sb[g][:, :, :, 0], in_=lift_all[g][:, :, 4:6], func=ACT.Sqrt, bias=1.0, scale=1.0)
+            nc.scalar.activation(out=ksl_sb[g][:, :, :, 0], in_=lift_sums[g][:, 0, :, :], func=ACT.Sqrt, bias=1.0, scale=1.0)
+            nc.scalar.activation(out=vs_sb[g][:, :, :, 0], in_=lift_sums[g][:, 1, :, :], func=ACT.Sqrt, bias=1.0, scale=1.0)
             nc.sync.dma_start(out=ksl_groups[g], in_=ksl_sb[g][:].rearrange("p n h f -> p (n h f)"))
             nc.sync.dma_start(out=vs_groups[g], in_=vs_sb[g][:].rearrange("p n h f -> p (n h f)"))
 
-        def live(g):
-            return 0 <= g < GROUPS
+        def do(stage, g, *args):
+            if 0 <= g < GROUPS:
+                stage(g, *args)
 
-        for i in range(-1, GROUPS + 5):
-            if live(i + 4) and i >= 0:
-                load_x(i + 4)
-            if live(i - 3):
-                rope_rotate(i - 3)
-            if live(i + 1):
-                flip_x(i + 1, (0, 1))
-            if live(i):
-                kv_bank(i, 0)
-            if live(i - 4):
-                add_second_bias(i - 4)
-            if live(i - 3):
-                second_product(i - 3)
-            if live(i - 1):
-                feature_sums(i - 1, (0, 1))
-            if live(i):
-                kv_bank(i, 1)
-            if live(i - 4):
-                lift_squares(i - 4)
-            if live(i - 1):
-                feature_sums(i - 1, (2, 3))
-            if live(i + 1):
-                flip_x(i + 1, (2, 3))
-            if live(i - 1):
-                norm_scalars(i - 1)
-            if i == 0:
-                prepare_wa_rope()
-                prepare_vectors()
-                prepare_wkv_b()
-            if live(i - 1):
-                rope_columns(i - 1)
-            if live(i - 5):
-                lift_roots_and_store(i - 5)
-            if live(i - 4):
-                lift_sums(i - 4)
-            if live(i + 1):
-                quantise_x(i + 1)
-            if live(i):
-                kv_bank(i, 2)
-                kv_bank(i, 3)
-            if live(i - 1):
-                norm(i - 1)
+        with tc.manual_schedule():
+            for n in range(SUB):
+                flip_x(0, n)
+            flip_wa(0)
+            quantise_x(0)
+            quantise_wa(0)
+            flip_x(1, 0)
+            flip_x(1, 1)
+            for i in range(GROUPS + 3):
+                first = i == 0
+                do(load_x, i + 4)
+                do(kv_product, i, 0)
+                do(second_product, i - 2, 0)
+                do(kv_square, i, 0)
+                do(kv_weighted, i, 0, False)
+                do(flip_x, i + 1, 2)
+                do(add_time_term, i - 2, 0)
+                do(rope_products, i - 1)
+                do(feature_sums, i - 1, 0)
+                do(feature_sums, i - 1, 1)
+                do(lift_squares, i - 3, 2)
+                do(square_rest, i, 0)
+                if first:
+                    flip_wa(1)
+                    quantise_wa(1)
+                do(kv_product, i, 1)
+                do(second_product, i - 2, 1)
+                do(feature_sums, i - 1, 2)
+                do(feature_sums, i - 1, 3)
+                do(add_time_term, i - 2, 1)
+                do(kv_square, i, 1)
+                do(kv_weighted, i, 1, True)
+                do(flip_x, i + 1, 3)
+                do(add_second_bias, i - 2)
+                do(square_rest, i, 1)
+                do(norm_root, i - 1)
+                do(lift_squares, i - 3, 3)
+                do(lift_roots_and_store, i - 3)
+                if first:
+                    flip_wa(2)
+                    quantise_wa(2)
+                do(kv_product, i, 2)
+                do(spread_rstd, i - 1)
+                do(quantise_x, i + 1)
+                do(kv_square, i, 2)
+                do(kv_weighted, i, 2, False)
+                do(lift_squares, i - 2, 0)
+                do(norm, i - 1)
+                do(rope_rows, i - 1)
+                if first:
+                    flip_wa(3)
+                    quantise_wa(3)
+                    flip_wa_rope()
+                    quantise_wa_rope()
+                    prepare_vectors()
+                    prepare_wkv_b()
+                do(kv_product, i, 3)
+                do(rope_product, i)
+                do(kv_square, i, 3)
+                do(kv_weighted, i, 3, True)
+                do(square_rest, i, 2)
+                do(quantise_sp, i - 1)
+                do(square_rest, i, 3)
+                do(rope_bias, i)
+                do(time_root, i - 1)
+                do(flip_x, i + 2, 0)
+                do(flip_x, i + 2, 1)
+                do(lift_squares, i - 2, 1)

@@ -49,10 +49,9 @@ def tile_lorentzmla_pa_t_kernel(
         five = ctx.enter_context(tc.tile_pool(name="five", bufs=5))
         psum_flip = ctx.enter_context(tc.psum_pool(name="psum_flip", bufs=2))
         psum_y = ctx.enter_context(tc.psum_pool(name="psum_y", bufs=2))
-        psum_small = ctx.enter_context(tc.psum_pool(name="psum_small", bufs=1))
+        psum_rope = ctx.enter_context(tc.psum_pool(name="psum_rope", bufs=2))
         psum_kv2 = ctx.enter_context(tc.psum_pool(name="psum_kv2", bufs=1))
         psum_norm = ctx.enter_context(tc.psum_pool(name="psum_norm", bufs=1))
-        psum_spread = ctx.enter_context(tc.psum_pool(name="psum_spread", bufs=1))
 
         x_sb = {}
 
@@ -61,7 +60,10 @@ def tile_lorentzmla_pa_t_kernel(
             nc.sync.dma_start(out=x_tile[:], in_=x_groups[g])
             x_sb[g] = x_tile
 
-        load_x(0)
+        x_first = five.tile([P, SUB, DIM], BF16, tag="rows")
+        for n in range(SUB):
+            nc.sync.dma_start(out=x_first[:, n, :], in_=x_groups[0][:, n, :])
+        x_sb[0] = x_first
         wa_kv_sb = five.tile([P, SUB, DIM], BF16, tag="rows")
         wa_kv_rows = wkv_a_w[0:KV_RANK, :].rearrange("(p t) k -> p t k", t=SUB)
         for t in range(SUB):
@@ -77,12 +79,16 @@ def tile_lorentzmla_pa_t_kernel(
         nc.scalar.dma_start(out=b_bf[:], in_=wkv_a_b[0:KV_RANK].rearrange("(p t) -> p t", t=SUB))
         w_bf = once.tile([P, SUB], BF16)
         nc.scalar.dma_start(out=w_bf[:], in_=kv_norm_w.rearrange("(p t) -> p t", t=SUB))
+        bpe_bf = [once.tile([P, 2], BF16, name="bpe_bf%d" % part) for part in range(2)]
+        bpe_rows = wkv_a_b[KV_RANK : KV_RANK + ROPE].rearrange("(j e) -> e j", e=2)
+        for e in range(2):
+            nc.scalar.dma_start(out=bpe_bf[0][e * HALF : (e + 1) * HALF, 0:1], in_=bpe_rows[e].unsqueeze(1))
+            nc.scalar.dma_start(out=bpe_bf[1][e * HALF : (e + 1) * HALF, 0:1], in_=bpe_rows[1 - e].unsqueeze(1))
         wb_full = once.tile([P, 2, KV_RANK + 1], BF16)
         nc.scalar.dma_start(out=wb_full[:], in_=wkv_b_w.rearrange("(o p) k -> p o k", p=P))
-        vec_rows = once.tile([P, 512], BF16)
+        vec_rows = once.tile([P, KV2], BF16)
         nc.vector.memset(vec_rows[:], 0.0)
         nc.scalar.dma_start(out=vec_rows[0:1, 0:KV2], in_=wkv_b_b.unsqueeze(0))
-        nc.scalar.dma_start(out=vec_rows[0:1, KV2 : KV2 + ROPE], in_=wkv_a_b[KV_RANK : KV_RANK + ROPE].unsqueeze(0))
         cos_t = once.tile([P, TABLE_HALVES, SUB, HALF], BF16)
         nc.scalar.dma_start(out=cos_t[:], in_=freqs_cos.rearrange("(a p n) j -> p a n j", p=P, n=SUB))
         sin_t = once.tile([P, TABLE_HALVES, SUB, HALF], BF16)
@@ -106,8 +112,25 @@ def tile_lorentzmla_pa_t_kernel(
         nc.vector.memset(sum_cols[:, :, 0], 1.0)
         nc.vector.tensor_copy(out=sum_cols[:, :, 1], in_=w_sq[:])
         nc.vector.tensor_tensor(out=sum_cols[:, :, 2], in0=w_sq[:], in1=sum_cols[:, :, 1], op=ALU.subtract)
-        nsin_t = once.tile([P, TABLE_HALVES, SUB, HALF], BF16)
-        nc.vector.tensor_scalar(out=nsin_t[:], in0=sin_t[:], scalar1=-1.0, scalar2=None, op0=ALU.mult)
+        bpe32 = once.tile([P, 2], F32)
+        for part in range(2):
+            nc.vector.tensor_copy(out=bpe32[:, part : part + 1], in_=bpe_bf[part][:, 0:1])
+        ident_bf = once.tile([P, P], BF16)
+        make_identity(nc, ident_bf[:])
+        cos_f = once.tile([P, TABLE_HALVES, SUB, P], BF16)
+        sin_f = once.tile([P, TABLE_HALVES, SUB, P], BF16)
+
+        def prepare_rope_tables(half):
+            for table, rows, signs in ((cos_f, cos_t, (1.0, 1.0)), (sin_f, sin_t, (-1.0, 1.0))):
+                twin = twice.tile([P, SUB, 2, HALF], BF16, tag="twin")
+                for e in range(2):
+                    nc.vector.tensor_scalar(
+                        out=twin[:, :, e, :], in0=rows[:, half, :, :], scalar1=signs[e], scalar2=None, op0=ALU.mult
+                    )
+                turned = psum_rope.tile([P, SUB, P], BF16, tag="rope")
+                for n in range(SUB):
+                    nc.tensor.transpose(turned[:, n, :], twin[:, n, :, :].rearrange("p e j -> p (e j)"), ident_bf[:])
+                nc.scalar.copy(out=table[:, half, :, :], in_=turned[:])
 
         def flip_place(rows_sb, grouped, n, copy):
             rows_words = rows_sb[:].bitcast(F32)[:, n, :]
@@ -131,8 +154,8 @@ def tile_lorentzmla_pa_t_kernel(
                     in_=wa_grouped[:, a, t, :, :].rearrange("q r j -> q (r j)"),
                 )
 
-        wa_pe_codes = once.tile([P, PASSES, ROPE], U32, align_bytes=64)
-        wa_pe_scales = once.tile([P, PASSES, ROPE], U8, align_bytes=64)
+        wa_pe_codes = once.tile([P, PASSES, 3 * HALF], U32, align_bytes=64)
+        wa_pe_scales = once.tile([P, PASSES, 3 * HALF], U8, align_bytes=64)
         pe_grouped = once.tile([P, PASSES, 1, P, 4], BF16, align_bytes=64)
 
         def flip_wa_rope():
@@ -140,11 +163,12 @@ def tile_lorentzmla_pa_t_kernel(
 
         def quantise_wa_rope():
             for a in range(PASSES):
-                nc.vector.quantize_mx(
-                    out=wa_pe_codes[:, a, :].bitcast(FP8X4),
-                    scales=wa_pe_scales[:, a, :],
-                    in_=pe_grouped[:, a, 0, :, :].rearrange("q r j -> q (r j)"),
-                )
+                for c0, c1, r1 in ((0, ROPE, ROPE), (ROPE, 3 * HALF, HALF)):
+                    nc.vector.quantize_mx(
+                        out=wa_pe_codes[:, a, c0:c1].bitcast(FP8X4),
+                        scales=wa_pe_scales[:, a, c0:c1],
+                        in_=pe_grouped[:, a, 0, 0:r1, :].rearrange("q r j -> q (r j)"),
+                    )
 
         x_grouped = {}
         x_codes = {}
@@ -169,16 +193,14 @@ def tile_lorentzmla_pa_t_kernel(
             x_scales[g] = scales
 
         bb_all = once.tile([P, KV2], F32)
-        bpe_all = once.tile([P, 2, HALF], F32)
         wb_codes = once.tile([P, KV2], U32, align_bytes=64)
         wb_scales = once.tile([P, KV2], U8, align_bytes=64)
         wb0_all = once.tile([P, KV2], F32)
 
         def prepare_vectors():
             vec_bank = psum_kv2.tile([P, 512], F32, tag="kv2")
-            nc.tensor.matmul(out=vec_bank[:], lhsT=ones_bf[:], rhs=vec_rows[:], start=True, stop=True)
+            nc.tensor.matmul(out=vec_bank[:, 0:KV2], lhsT=ones_bf[:], rhs=vec_rows[:], start=True, stop=True)
             nc.vector.tensor_copy(out=bb_all[:], in_=vec_bank[:, 0:KV2])
-            nc.vector.tensor_copy(out=bpe_all[:], in_=vec_bank[:, KV2 : KV2 + ROPE].rearrange("p (j e) -> p e j", e=2))
 
         def prepare_wkv_b():
             wb_even = once.tile([P, 2, KV_RANK], BF16)
@@ -261,40 +283,68 @@ def tile_lorentzmla_pa_t_kernel(
             if t == 0:
                 rest_new = twice.tile([P, SUB, GROUP], BF16, tag="sq_rest")
                 squares_rest[g] = rest_new
-            nc.vector.tensor_tensor(
+            nc.gpsimd.tensor_tensor(
                 out=squares_rest[g][:, t, :],
                 in0=squares[g][:, t, :],
                 in1=upper_halves(squares[g])[:, t, :],
                 op=ALU.subtract,
             )
 
-        rope_pe = {}
-        rope_in = {}
+        rope_parts = {}
+        rope_banks = {}
 
-        def rope_product(g):
-            pe = psum_small.tile([P, SUB, ROPE], F32, tag="small")
-            for n in range(SUB):
-                for a in range(PASSES):
-                    nc.tensor.matmul_mx(
-                        out=pe[:, n, :],
-                        lhsT=x_codes[g][:, a, n * P : (n + 1) * P].bitcast(FP8X4),
-                        lhsT_scale=x_scales[g][:, a, n * P : (n + 1) * P],
-                        rhs=wa_pe_codes[:, a, :].bitcast(FP8X4),
-                        rhs_scale=wa_pe_scales[:, a, :],
-                        start=(a == 0),
-                        stop=(a == PASSES - 1),
-                    )
-            rope_pe[g] = pe
+        def rope_product(g, part):
+            bank = psum_rope.tile([P, GROUP], F32, tag="rope")
+            cols = slice(part * HALF, part * HALF + ROPE)
+            for a in range(PASSES):
+                nc.tensor.matmul_mx(
+                    out=bank[:],
+                    lhsT=wa_pe_codes[:, a, cols].bitcast(FP8X4),
+                    lhsT_scale=wa_pe_scales[:, a, cols],
+                    rhs=x_codes[g][:, a, :].bitcast(FP8X4),
+                    rhs_scale=x_scales[g][:, a, :],
+                    start=(a == 0),
+                    stop=(a == PASSES - 1),
+                )
+            rope_banks[g, part] = bank
 
-        def rope_bias(g):
-            pb = three.tile([P, SUB, 2, HALF], F32, tag="pb")
-            nc.vector.tensor_tensor(
-                out=pb[:],
-                in0=rope_pe[g][:].rearrange("p n (e j) -> p n e j", e=2),
-                in1=bpe_all[:].unsqueeze(1).to_broadcast([P, SUB, 2, HALF]),
-                op=ALU.add,
+        def rope_multiply(g, part):
+            table = (cos_f, sin_f)[part]
+            result = twice.tile([P, GROUP], F32, tag="rope_part%d" % part)
+            nc.vector.scalar_tensor_tensor(
+                out=result[:],
+                in0=rope_banks[g, part][:],
+                scalar=bpe32[:, part : part + 1],
+                in1=table[:, g % TABLE_HALVES, :, :].rearrange("p n r -> p (n r)"),
+                op0=ALU.add,
+                op1=ALU.mult,
             )
-            rope_in[g] = pb
+            rope_parts[g, part] = result
+
+        kpe_banks = {}
+
+        def rope_turn(g):
+            bank = psum_rope.tile([P, SUB, ROPE], F32, tag="rope")
+            for n in range(SUB):
+                for part in range(2):
+                    nc.tensor.matmul(
+                        out=bank[:, n, :],
+                        lhsT=rope_parts[g, part][:, n * P : (n + 1) * P],
+                        rhs=ident[:],
+                        start=(part == 0),
+                        stop=(part == 1),
+                        is_transpose=True,
+                    )
+            kpe_banks[g] = bank
+
+        def rope_rows(g, h):
+            if h == 0:
+                ksl_new = three.tile([P, SUB, HEADS, K_ROW], F32, tag="ksl")
+                ksl_sb[g] = ksl_new
+            nc.scalar.copy(
+                out=ksl_sb[g][:, :, h, 1 + NOPE : K_ROW].rearrange("p n (j e) -> p n j e", e=2),
+                in_=kpe_banks[g][:].rearrange("p n (e j) -> p n j e", e=2),
+            )
 
         norm_sums = {}
         rstd = {}
@@ -347,7 +397,7 @@ def tile_lorentzmla_pa_t_kernel(
         spread_of = {}
 
         def spread_rstd(g):
-            spread = psum_spread.tile([P, GROUP], F32, tag="spread")
+            spread = psum_norm.tile([P, GROUP], F32, tag="norm")
             for n in range(SUB):
                 nc.tensor.transpose(
                     spread[:, n * P : (n + 1) * P], rstd[g][:, n : n + 1].to_broadcast([P, P]), ident[:]
@@ -375,43 +425,6 @@ def tile_lorentzmla_pa_t_kernel(
 
         ksl_sb = {}
         vs_sb = {}
-        by_cos = {}
-        by_sin = {}
-
-        def rope_products(g):
-            half = g % TABLE_HALVES
-            pb = rope_in[g]
-            cos_new = once.tile([P, SUB, 2, HALF], F32, tag="by_cos")
-            nc.gpsimd.tensor_tensor(
-                out=cos_new[:],
-                in0=pb[:],
-                in1=cos_t[:, half, :, :].unsqueeze(2).to_broadcast([P, SUB, 2, HALF]),
-                op=ALU.mult,
-            )
-            sin_new = once.tile([P, SUB, 2, HALF], F32, tag="by_sin")
-            nc.gpsimd.tensor_tensor(out=sin_new[:, :, 0, :], in0=pb[:, :, 1, :], in1=nsin_t[:, half, :, :], op=ALU.mult)
-            nc.gpsimd.tensor_tensor(out=sin_new[:, :, 1, :], in0=pb[:, :, 0, :], in1=sin_t[:, half, :, :], op=ALU.mult)
-            by_cos[g] = cos_new
-            by_sin[g] = sin_new
-
-        def rope_rows(g):
-            ksl = three.tile([P, SUB, HEADS, K_ROW], F32, tag="ksl")
-            ksl_sb[g] = ksl
-            nc.gpsimd.tensor_tensor(
-                out=ksl[:, :, 0, 1 + NOPE : K_ROW].rearrange("p n (j e) -> p n j e", e=2),
-                in0=by_cos[g][:].rearrange("p n e j -> p n j e"),
-                in1=by_sin[g][:].rearrange("p n e j -> p n j e"),
-                op=ALU.add,
-            )
-            nc.gpsimd.tensor_scalar(
-                out=ksl[:, :, 1, 1 + NOPE : K_ROW],
-                in0=ksl[:, :, 0, 1 + NOPE : K_ROW],
-                scalar1=1.0,
-                scalar2=0.0,
-                op0=ALU.mult,
-                op1=ALU.add,
-            )
-
         kv2_sb = {}
         kv2_banks = {}
 
@@ -460,24 +473,38 @@ def tile_lorentzmla_pa_t_kernel(
 
         lift_sums = {}
 
-        def lift_squares(g, n):
+        def lift_stats(g, n):
             if n == 0:
-                sums_new = three.tile([P, 2, SUB, HEADS], F32, tag="lift_sums")
-                lift_sums[g] = sums_new
-            sums = lift_sums[g]
+                stats_new = twice.tile([P, SUB, 2, 2, 3], F32, tag="stats")
+                v_new = twice.tile([P, SUB, HEADS], F32, tag="v_sums")
+                lift_sums[g] = (stats_new, v_new)
+            stats, v_sums = lift_sums[g]
+            rows = (
+                ksl_sb[g][:, n, :, 1 : 1 + NOPE].rearrange("p h c -> p c h"),
+                ksl_sb[g][:, n, 0, 1 + NOPE : K_ROW],
+            )
+            for k in range(2):
+                nc.vector.bn_stats(out=stats[:, n, k, :, :].rearrange("p e s -> p (e s)"), in_=rows[k])
             for h in range(HEADS):
-                junk = twice.tile([P, K_ROW - 1], BF16, tag="junk")
-                nc.scalar.activation(
-                    out=junk[:], in_=ksl_sb[g][:, n, h, 1:K_ROW], func=ACT.Square, accum_out=sums[:, 0, n, h : h + 1]
-                )
                 junk_v = twice.tile([P, V_DIM], BF16, tag="junk_v")
                 nc.scalar.activation(
-                    out=junk_v[:], in_=vs_sb[g][:, n, h, 1:V_ROW], func=ACT.Square, accum_out=sums[:, 1, n, h : h + 1]
+                    out=junk_v[:], in_=vs_sb[g][:, n, h, 1:V_ROW], func=ACT.Square, accum_out=v_sums[:, n, h : h + 1]
                 )
 
         def lift_roots_and_store(g):
-            nc.scalar.activation(out=ksl_sb[g][:, :, :, 0], in_=lift_sums[g][:, 0, :, :], func=ACT.Sqrt, bias=1.0, scale=1.0)
-            nc.scalar.activation(out=vs_sb[g][:, :, :, 0], in_=lift_sums[g][:, 1, :, :], func=ACT.Sqrt, bias=1.0, scale=1.0)
+            stats, v_sums = lift_sums[g]
+            mean_part = twice.tile([P, SUB, 2, 2], F32, tag="mean_part")
+            nc.scalar.activation(out=mean_part[:], in_=stats[:, :, :, :, 1], func=ACT.Square, scale=8.0)
+            sums = twice.tile([P, SUB, 2, 2], F32, tag="square_sums")
+            nc.vector.tensor_tensor(out=sums[:], in0=mean_part[:], in1=stats[:, :, :, :, 2], op=ALU.add)
+            rope_sum = twice.tile([P, SUB], F32, tag="rope_sum")
+            nc.vector.tensor_tensor(out=rope_sum[:], in0=sums[:, :, 1, 0], in1=sums[:, :, 1, 1], op=ALU.add)
+            k_sum = twice.tile([P, SUB, HEADS], F32, tag="k_sum")
+            nc.vector.tensor_tensor(
+                out=k_sum[:], in0=sums[:, :, 0, :], in1=rope_sum[:].unsqueeze(2).to_broadcast([P, SUB, HEADS]), op=ALU.add
+            )
+            nc.scalar.activation(out=ksl_sb[g][:, :, :, 0], in_=k_sum[:], func=ACT.Sqrt, bias=1.0, scale=1.0)
+            nc.scalar.activation(out=vs_sb[g][:, :, :, 0], in_=v_sums[:], func=ACT.Sqrt, bias=1.0, scale=1.0)
             nc.sync.dma_start(out=ksl_groups[g], in_=ksl_sb[g][:].rearrange("p n h f -> p (n h f)"))
             nc.sync.dma_start(out=vs_groups[g], in_=vs_sb[g][:].rearrange("p n h f -> p (n h f)"))
 
@@ -485,71 +512,47 @@ def tile_lorentzmla_pa_t_kernel(
             if 0 <= g < GROUPS:
                 stage(g, *args)
 
-        with tc.manual_schedule():
+        for n in range(SUB):
+            flip_x(0, n)
+        for t in range(SUB):
+            flip_wa(t)
+            quantise_wa(t)
+        quantise_x(0)
+        flip_wa_rope()
+        quantise_wa_rope()
+        for i in range(GROUPS + 4):
+            do(load_x, i + 4)
+            do(lift_roots_and_store, i - 3)
             for n in range(SUB):
-                flip_x(0, n)
-            flip_wa(0)
-            quantise_x(0)
-            quantise_wa(0)
-            flip_x(1, 0)
-            flip_x(1, 1)
-            for i in range(GROUPS + 3):
-                first = i == 0
-                do(load_x, i + 4)
-                do(kv_product, i, 0)
-                do(second_product, i - 2, 0)
-                do(kv_square, i, 0)
-                do(kv_weighted, i, 0, False)
-                do(flip_x, i + 1, 2)
-                do(add_time_term, i - 2, 0)
-                do(rope_products, i - 1)
-                do(feature_sums, i - 1, 0)
-                do(feature_sums, i - 1, 1)
-                do(lift_squares, i - 3, 2)
-                do(square_rest, i, 0)
-                if first:
-                    flip_wa(1)
-                    quantise_wa(1)
-                do(kv_product, i, 1)
-                do(second_product, i - 2, 1)
-                do(feature_sums, i - 1, 2)
-                do(feature_sums, i - 1, 3)
-                do(add_time_term, i - 2, 1)
-                do(kv_square, i, 1)
-                do(kv_weighted, i, 1, True)
-                do(flip_x, i + 1, 3)
-                do(add_second_bias, i - 2)
-                do(square_rest, i, 1)
-                do(norm_root, i - 1)
-                do(lift_squares, i - 3, 3)
-                do(lift_roots_and_store, i - 3)
-                if first:
-                    flip_wa(2)
-                    quantise_wa(2)
-                do(kv_product, i, 2)
-                do(spread_rstd, i - 1)
-                do(quantise_x, i + 1)
-                do(kv_square, i, 2)
-                do(kv_weighted, i, 2, False)
-                do(lift_squares, i - 2, 0)
-                do(norm, i - 1)
-                do(rope_rows, i - 1)
-                if first:
-                    flip_wa(3)
-                    quantise_wa(3)
-                    flip_wa_rope()
-                    quantise_wa_rope()
-                    prepare_vectors()
-                    prepare_wkv_b()
-                do(kv_product, i, 3)
-                do(rope_product, i)
-                do(kv_square, i, 3)
-                do(kv_weighted, i, 3, True)
-                do(square_rest, i, 2)
-                do(quantise_sp, i - 1)
-                do(square_rest, i, 3)
-                do(rope_bias, i)
-                do(time_root, i - 1)
-                do(flip_x, i + 2, 0)
-                do(flip_x, i + 2, 1)
-                do(lift_squares, i - 2, 1)
+                do(feature_sums, i - 1, n)
+            do(norm_root, i - 1)
+            do(time_root, i - 1)
+            do(spread_rstd, i - 1)
+            do(norm, i - 1)
+            do(quantise_sp, i - 1)
+            for pair in range(2):
+                do(second_product, i - 2, pair)
+                do(add_time_term, i - 2, pair)
+            do(add_second_bias, i - 2)
+            for n in range(SUB):
+                do(lift_stats, i - 2, n)
+            do(rope_turn, i - 1)
+            do(rope_rows, i - 1, 0)
+            do(rope_rows, i - 1, 1)
+            for t in range(SUB):
+                do(kv_product, i, t)
+                do(kv_square, i, t)
+                do(kv_weighted, i, t, t == 3)
+                do(square_rest, i, t)
+                do(flip_x, i + 1, t)
+            do(quantise_x, i + 1)
+            if i == 0:
+                prepare_rope_tables(0)
+                prepare_rope_tables(1)
+            do(rope_product, i, 0)
+            do(rope_product, i, 1)
+            do(rope_multiply, i, 0)
+            do(rope_multiply, i, 1)
+            if i == 0:
+                prepare_vectors()
+                prepare_wkv_b()

@@ -79,11 +79,10 @@ def tile_lorentzmla_pa_t_kernel(
         nc.scalar.dma_start(out=b_bf[:], in_=wkv_a_b[0:KV_RANK].rearrange("(p t) -> p t", t=SUB))
         w_bf = once.tile([P, SUB], BF16)
         nc.scalar.dma_start(out=w_bf[:], in_=kv_norm_w.rearrange("(p t) -> p t", t=SUB))
-        bpe_bf = [once.tile([P, 2], BF16, name="bpe_bf%d" % part) for part in range(2)]
+        bpe_bf = once.tile([P, 2], BF16)
         bpe_rows = wkv_a_b[KV_RANK : KV_RANK + ROPE].rearrange("(j e) -> e j", e=2)
         for e in range(2):
-            nc.scalar.dma_start(out=bpe_bf[0][e * HALF : (e + 1) * HALF, 0:1], in_=bpe_rows[e].unsqueeze(1))
-            nc.scalar.dma_start(out=bpe_bf[1][e * HALF : (e + 1) * HALF, 0:1], in_=bpe_rows[1 - e].unsqueeze(1))
+            nc.scalar.dma_start(out=bpe_bf[e * HALF : (e + 1) * HALF, 0:1], in_=bpe_rows[e].unsqueeze(1))
         wb_full = once.tile([P, 2, KV_RANK + 1], BF16)
         nc.scalar.dma_start(out=wb_full[:], in_=wkv_b_w.rearrange("(o p) k -> p o k", p=P))
         vec_rows = once.tile([P, KV2], BF16)
@@ -112,25 +111,35 @@ def tile_lorentzmla_pa_t_kernel(
         nc.vector.memset(sum_cols[:, :, 0], 1.0)
         nc.vector.tensor_copy(out=sum_cols[:, :, 1], in_=w_sq[:])
         nc.vector.tensor_tensor(out=sum_cols[:, :, 2], in0=w_sq[:], in1=sum_cols[:, :, 1], op=ALU.subtract)
-        bpe32 = once.tile([P, 2], F32)
-        for part in range(2):
-            nc.vector.tensor_copy(out=bpe32[:, part : part + 1], in_=bpe_bf[part][:, 0:1])
+        bpe32 = once.tile([P, 1], F32)
+        nc.vector.tensor_copy(out=bpe32[:], in_=bpe_bf[:, 0:1])
+        pair_own = once.tile([P, P], F32)
+        pair_swap = once.tile([P, P], F32)
+        for e in range(2):
+            source = ident[:, e * HALF : (e + 1) * HALF]
+            nc.vector.tensor_copy(out=pair_own[:].rearrange("p (j e) -> p e j", e=2)[:, e, :], in_=source)
+            nc.vector.tensor_copy(out=pair_swap[:].rearrange("p (j e) -> p e j", e=2)[:, 1 - e, :], in_=source)
         ident_bf = once.tile([P, P], BF16)
         make_identity(nc, ident_bf[:])
         cos_f = once.tile([P, TABLE_HALVES, SUB, P], BF16)
         sin_f = once.tile([P, TABLE_HALVES, SUB, P], BF16)
 
-        def prepare_rope_tables(half):
-            for table, rows, signs in ((cos_f, cos_t, (1.0, 1.0)), (sin_f, sin_t, (-1.0, 1.0))):
-                twin = twice.tile([P, SUB, 2, HALF], BF16, tag="twin")
+        cos_twin = once.tile([P, TABLE_HALVES, SUB, 2, HALF], BF16)
+        sin_twin = once.tile([P, TABLE_HALVES, SUB, 2, HALF], BF16)
+
+        def twin_tables():
+            for twin, rows, signs in ((cos_twin, cos_t, (1.0, 1.0)), (sin_twin, sin_t, (1.0, -1.0))):
                 for e in range(2):
                     nc.vector.tensor_scalar(
-                        out=twin[:, :, e, :], in0=rows[:, half, :, :], scalar1=signs[e], scalar2=None, op0=ALU.mult
+                        out=twin[:, :, :, e, :], in0=rows[:], scalar1=signs[e], scalar2=None, op0=ALU.mult
                     )
+
+        def turn_tables(half):
+            for table, twin in ((cos_f, cos_twin), (sin_f, sin_twin)):
                 turned = psum_rope.tile([P, SUB, P], BF16, tag="rope")
                 for n in range(SUB):
-                    nc.tensor.transpose(turned[:, n, :], twin[:, n, :, :].rearrange("p e j -> p (e j)"), ident_bf[:])
-                nc.scalar.copy(out=table[:, half, :, :], in_=turned[:])
+                    nc.tensor.transpose(turned[:, n, :], twin[:, half, n, :, :].rearrange("p e j -> p (e j)"), ident_bf[:])
+                nc.vector.tensor_copy(out=table[:, half, :, :], in_=turned[:])
 
         def flip_place(rows_sb, grouped, n, copy):
             rows_words = rows_sb[:].bitcast(F32)[:, n, :]
@@ -154,8 +163,8 @@ def tile_lorentzmla_pa_t_kernel(
                     in_=wa_grouped[:, a, t, :, :].rearrange("q r j -> q (r j)"),
                 )
 
-        wa_pe_codes = once.tile([P, PASSES, 3 * HALF], U32, align_bytes=64)
-        wa_pe_scales = once.tile([P, PASSES, 3 * HALF], U8, align_bytes=64)
+        wa_pe_codes = once.tile([P, PASSES, ROPE], U32, align_bytes=64)
+        wa_pe_scales = once.tile([P, PASSES, ROPE], U8, align_bytes=64)
         pe_grouped = once.tile([P, PASSES, 1, P, 4], BF16, align_bytes=64)
 
         def flip_wa_rope():
@@ -163,12 +172,11 @@ def tile_lorentzmla_pa_t_kernel(
 
         def quantise_wa_rope():
             for a in range(PASSES):
-                for c0, c1, r1 in ((0, ROPE, ROPE), (ROPE, 3 * HALF, HALF)):
-                    nc.vector.quantize_mx(
-                        out=wa_pe_codes[:, a, c0:c1].bitcast(FP8X4),
-                        scales=wa_pe_scales[:, a, c0:c1],
-                        in_=pe_grouped[:, a, 0, 0:r1, :].rearrange("q r j -> q (r j)"),
-                    )
+                nc.vector.quantize_mx(
+                    out=wa_pe_codes[:, a, :].bitcast(FP8X4),
+                    scales=wa_pe_scales[:, a, :],
+                    in_=pe_grouped[:, a, 0, :, :].rearrange("q r j -> q (r j)"),
+                )
 
         x_grouped = {}
         x_codes = {}
@@ -202,24 +210,31 @@ def tile_lorentzmla_pa_t_kernel(
             nc.tensor.matmul(out=vec_bank[:, 0:KV2], lhsT=ones_bf[:], rhs=vec_rows[:], start=True, stop=True)
             nc.vector.tensor_copy(out=bb_all[:], in_=vec_bank[:, 0:KV2])
 
-        def prepare_wkv_b():
-            wb_even = once.tile([P, 2, KV_RANK], BF16)
+        wb_even = once.tile([P, 2, KV_RANK], BF16)
+        wb_grouped = once.tile([P, KV2, 4], BF16, align_bytes=64)
+        wb0_col = once.tile([P, 2], F32)
+
+        def align_wkv_b():
             nc.vector.tensor_copy(out=wb_even[:], in_=wb_full[:, :, 1 : KV_RANK + 1])
+            nc.vector.tensor_copy(out=wb0_col[:], in_=wb_full[:, :, 0])
+
+        def flip_wkv_b():
             wb_words = wb_even[:].bitcast(F32).rearrange("r o (q u) -> r o u q", u=2)
             wb_flipped = psum_flip.tile([P, 4, P], F32, tag="flip")
             for o in range(2):
                 for u in range(2):
                     nc.tensor.transpose(wb_flipped[:, 2 * o + u, :], wb_words[:, o, u, :], ident[:])
-            wb_grouped = once.tile([P, KV2, 4], BF16, align_bytes=64)
-            nc.vector.tensor_copy(
+            nc.scalar.copy(
                 out=wb_grouped[:].bitcast(F32).rearrange("q (o r) u -> q o r u", o=2),
                 in_=wb_flipped[:].rearrange("q (o u) r -> q o r u", u=2),
             )
+
+        def quantise_wkv_b():
             nc.vector.quantize_mx(
                 out=wb_codes[:].bitcast(FP8X4), scales=wb_scales[:], in_=wb_grouped[:].rearrange("q c j -> q (c j)")
             )
-            wb0_col = once.tile([P, 2], F32)
-            nc.vector.tensor_copy(out=wb0_col[:], in_=wb_full[:, :, 0])
+
+        def spread_wb0():
             wb0_bank = psum_kv2.tile([P, 512], F32, tag="kv2")
             for o in range(2):
                 nc.tensor.transpose(
@@ -283,7 +298,7 @@ def tile_lorentzmla_pa_t_kernel(
             if t == 0:
                 rest_new = twice.tile([P, SUB, GROUP], BF16, tag="sq_rest")
                 squares_rest[g] = rest_new
-            nc.gpsimd.tensor_tensor(
+            (nc.gpsimd if g > 0 else nc.vector).tensor_tensor(
                 out=squares_rest[g][:, t, :],
                 in0=squares[g][:, t, :],
                 in1=upper_halves(squares[g])[:, t, :],
@@ -293,28 +308,27 @@ def tile_lorentzmla_pa_t_kernel(
         rope_parts = {}
         rope_banks = {}
 
-        def rope_product(g, part):
+        def rope_product(g):
             bank = psum_rope.tile([P, GROUP], F32, tag="rope")
-            cols = slice(part * HALF, part * HALF + ROPE)
             for a in range(PASSES):
                 nc.tensor.matmul_mx(
                     out=bank[:],
-                    lhsT=wa_pe_codes[:, a, cols].bitcast(FP8X4),
-                    lhsT_scale=wa_pe_scales[:, a, cols],
+                    lhsT=wa_pe_codes[:, a, :].bitcast(FP8X4),
+                    lhsT_scale=wa_pe_scales[:, a, :],
                     rhs=x_codes[g][:, a, :].bitcast(FP8X4),
                     rhs_scale=x_scales[g][:, a, :],
                     start=(a == 0),
                     stop=(a == PASSES - 1),
                 )
-            rope_banks[g, part] = bank
+            rope_banks[g] = bank
 
         def rope_multiply(g, part):
             table = (cos_f, sin_f)[part]
             result = twice.tile([P, GROUP], F32, tag="rope_part%d" % part)
             nc.vector.scalar_tensor_tensor(
                 out=result[:],
-                in0=rope_banks[g, part][:],
-                scalar=bpe32[:, part : part + 1],
+                in0=rope_banks[g][:],
+                scalar=bpe32[:, 0:1],
                 in1=table[:, g % TABLE_HALVES, :, :].rearrange("p n r -> p (n r)"),
                 op0=ALU.add,
                 op1=ALU.mult,
@@ -330,20 +344,19 @@ def tile_lorentzmla_pa_t_kernel(
                     nc.tensor.matmul(
                         out=bank[:, n, :],
                         lhsT=rope_parts[g, part][:, n * P : (n + 1) * P],
-                        rhs=ident[:],
+                        rhs=(pair_own, pair_swap)[part][:],
                         start=(part == 0),
                         stop=(part == 1),
                         is_transpose=True,
                     )
             kpe_banks[g] = bank
 
-        def rope_rows(g, h):
-            if h == 0:
-                ksl_new = three.tile([P, SUB, HEADS, K_ROW], F32, tag="ksl")
-                ksl_sb[g] = ksl_new
+        def rope_rows(g):
+            ksl_new = three.tile([P, SUB, HEADS, K_ROW], F32, tag="ksl")
+            ksl_sb[g] = ksl_new
             nc.scalar.copy(
-                out=ksl_sb[g][:, :, h, 1 + NOPE : K_ROW].rearrange("p n (j e) -> p n j e", e=2),
-                in_=kpe_banks[g][:].rearrange("p n (e j) -> p n j e", e=2),
+                out=ksl_new[:, :, :, 1 + NOPE : K_ROW],
+                in_=kpe_banks[g][:].unsqueeze(2).to_broadcast([P, SUB, HEADS, ROPE]),
             )
 
         norm_sums = {}
@@ -382,13 +395,18 @@ def tile_lorentzmla_pa_t_kernel(
             nc.vector.tensor_reduce(out=kw_sq[:], in_=norm_sums[g][:, :, 1:3], axis=AXIS.X, op=ALU.add)
             kw_sums[g] = kw_sq
 
-        def time_root(g):
+        sp_squares = {}
+
+        def time_square(g):
             inv_ms = three.tile([P, SUB], F32, tag="inv_ms")
             nc.gpsimd.tensor_tensor(out=inv_ms[:], in0=rstd[g][:], in1=rstd[g][:], op=ALU.mult)
             sp_sq = three.tile([P, SUB], F32, tag="sp_sq")
             nc.gpsimd.tensor_tensor(out=sp_sq[:], in0=kw_sums[g][:], in1=inv_ms[:], op=ALU.mult)
+            sp_squares[g] = sp_sq
+
+        def time_root(g):
             tm = three.tile([P, SUB], F32, tag="tm")
-            nc.scalar.activation(out=tm[:], in_=sp_sq[:], func=ACT.Sqrt, bias=1.0, scale=1.0)
+            nc.scalar.activation(out=tm[:], in_=sp_squares[g][:], func=ACT.Sqrt, bias=1.0, scale=1.0)
             time_sp[g] = tm
 
         sp_rows = {}
@@ -491,18 +509,24 @@ def tile_lorentzmla_pa_t_kernel(
                     out=junk_v[:], in_=vs_sb[g][:, n, h, 1:V_ROW], func=ACT.Square, accum_out=v_sums[:, n, h : h + 1]
                 )
 
-        def lift_roots_and_store(g):
-            stats, v_sums = lift_sums[g]
-            mean_part = twice.tile([P, SUB, 2, 2], F32, tag="mean_part")
-            nc.scalar.activation(out=mean_part[:], in_=stats[:, :, :, :, 1], func=ACT.Square, scale=8.0)
-            sums = twice.tile([P, SUB, 2, 2], F32, tag="square_sums")
-            nc.vector.tensor_tensor(out=sums[:], in0=mean_part[:], in1=stats[:, :, :, :, 2], op=ALU.add)
+        k_sums = {}
+
+        def lift_combine(g):
+            stats = lift_sums[g][0]
+            nc.scalar.activation(out=stats[:, :, :, :, 0], in_=stats[:, :, :, :, 1], func=ACT.Square, scale=8.0)
+            nope_sum = twice.tile([P, SUB, HEADS], F32, tag="nope_sum")
+            nc.vector.tensor_reduce(out=nope_sum[:], in_=stats[:, :, 0, :, 0::2], axis=AXIS.X, op=ALU.add)
             rope_sum = twice.tile([P, SUB], F32, tag="rope_sum")
-            nc.vector.tensor_tensor(out=rope_sum[:], in0=sums[:, :, 1, 0], in1=sums[:, :, 1, 1], op=ALU.add)
+            nc.vector.tensor_reduce(out=rope_sum[:], in_=stats[:, :, 1, :, 0::2], axis=AXIS.XY, op=ALU.add)
             k_sum = twice.tile([P, SUB, HEADS], F32, tag="k_sum")
-            nc.vector.tensor_tensor(
-                out=k_sum[:], in0=sums[:, :, 0, :], in1=rope_sum[:].unsqueeze(2).to_broadcast([P, SUB, HEADS]), op=ALU.add
+            nc.gpsimd.tensor_tensor(
+                out=k_sum[:], in0=nope_sum[:], in1=rope_sum[:].unsqueeze(2).to_broadcast([P, SUB, HEADS]), op=ALU.add
             )
+            k_sums[g] = k_sum
+
+        def lift_roots_and_store(g):
+            k_sum = k_sums[g]
+            v_sums = lift_sums[g][1]
             nc.scalar.activation(out=ksl_sb[g][:, :, :, 0], in_=k_sum[:], func=ACT.Sqrt, bias=1.0, scale=1.0)
             nc.scalar.activation(out=vs_sb[g][:, :, :, 0], in_=v_sums[:], func=ACT.Sqrt, bias=1.0, scale=1.0)
             nc.sync.dma_start(out=ksl_groups[g], in_=ksl_sb[g][:].rearrange("p n h f -> p (n h f)"))
@@ -512,47 +536,81 @@ def tile_lorentzmla_pa_t_kernel(
             if 0 <= g < GROUPS:
                 stage(g, *args)
 
-        for n in range(SUB):
-            flip_x(0, n)
-        for t in range(SUB):
-            flip_wa(t)
-            quantise_wa(t)
-        quantise_x(0)
-        flip_wa_rope()
-        quantise_wa_rope()
-        for i in range(GROUPS + 4):
-            do(load_x, i + 4)
-            do(lift_roots_and_store, i - 3)
+        with tc.manual_schedule():
             for n in range(SUB):
-                do(feature_sums, i - 1, n)
-            do(norm_root, i - 1)
-            do(time_root, i - 1)
-            do(spread_rstd, i - 1)
-            do(norm, i - 1)
-            do(quantise_sp, i - 1)
-            for pair in range(2):
-                do(second_product, i - 2, pair)
-                do(add_time_term, i - 2, pair)
-            do(add_second_bias, i - 2)
-            for n in range(SUB):
-                do(lift_stats, i - 2, n)
-            do(rope_turn, i - 1)
-            do(rope_rows, i - 1, 0)
-            do(rope_rows, i - 1, 1)
+                flip_x(0, n)
             for t in range(SUB):
-                do(kv_product, i, t)
-                do(kv_square, i, t)
-                do(kv_weighted, i, t, t == 3)
-                do(square_rest, i, t)
-                do(flip_x, i + 1, t)
-            do(quantise_x, i + 1)
-            if i == 0:
-                prepare_rope_tables(0)
-                prepare_rope_tables(1)
-            do(rope_product, i, 0)
-            do(rope_product, i, 1)
-            do(rope_multiply, i, 0)
-            do(rope_multiply, i, 1)
-            if i == 0:
-                prepare_vectors()
-                prepare_wkv_b()
+                flip_wa(t)
+                if t == 1:
+                    quantise_x(0)
+                quantise_wa(t)
+            for i in range(GROUPS + 3):
+                first = i == 0
+                do(load_x, i + 4)
+                do(kv_product, i, 0)
+                do(kv_square, i, 0)
+                do(kv_weighted, i, 0, first)
+                do(square_rest, i, 0)
+                if first:
+                    flip_x(1, 0)
+                    twin_tables()
+                    align_wkv_b()
+                    prepare_vectors()
+                do(lift_stats, i - 3, 0)
+                do(lift_stats, i - 3, 1)
+                do(second_product, i - 2, 0)
+                do(add_time_term, i - 2, 0)
+                do(lift_stats, i - 3, 2)
+                do(lift_stats, i - 3, 3)
+                do(feature_sums, i - 1, 0)
+                do(feature_sums, i - 1, 1)
+                do(kv_product, i, 1)
+                if not first:
+                    do(quantise_x, i + 1)
+                do(kv_square, i, 1)
+                do(lift_combine, i - 3)
+                do(lift_roots_and_store, i - 3)
+                do(second_product, i - 2, 1)
+                do(add_time_term, i - 2, 1)
+                do(kv_weighted, i, 1, True)
+                if first:
+                    flip_x(1, 1)
+                    flip_wa_rope()
+                    quantise_wa_rope()
+                    spread_wb0()
+                do(square_rest, i, 1)
+                do(add_second_bias, i - 2)
+                do(feature_sums, i - 1, 2)
+                do(feature_sums, i - 1, 3)
+                do(norm_root, i - 1)
+                do(kv_product, i, 2)
+                do(kv_square, i, 2)
+                do(kv_weighted, i, 2, first)
+                if first:
+                    flip_x(1, 2)
+                    flip_x(1, 3)
+                    quantise_x(1)
+                    turn_tables(0)
+                do(spread_rstd, i - 1)
+                do(flip_x, i + 2, 0)
+                do(flip_x, i + 2, 1)
+                do(norm, i - 1)
+                do(rope_turn, i - 1)
+                do(kv_product, i, 3)
+                do(rope_rows, i - 1)
+                do(kv_square, i, 3)
+                do(kv_weighted, i, 3, first)
+                do(rope_product, i)
+                do(square_rest, i, 2)
+                do(time_square, i - 1)
+                do(time_root, i - 1)
+                do(square_rest, i, 3)
+                do(flip_x, i + 2, 2)
+                do(flip_x, i + 2, 3)
+                if first:
+                    turn_tables(1)
+                    flip_wkv_b()
+                    quantise_wkv_b()
+                do(quantise_sp, i - 1)
+                do(rope_multiply, i, 0)
+                do(rope_multiply, i, 1)

@@ -53,6 +53,11 @@ def tile_lorentzmla_pa_t_kernel(
         psum_kv2 = ctx.enter_context(tc.psum_pool(name="psum_kv2", bufs=1))
         psum_norm = ctx.enter_context(tc.psum_pool(name="psum_norm", bufs=1))
 
+        one = once.tile([P, 1], F32)
+        nc.vector.memset(one[:], 1.0)
+        root = once.tile([P, 1], F32)
+        nc.scalar.activation(out=root[:], in_=one[:], func=ACT.Sqrt)
+
         x_sb = {}
 
         def load_x(g):
@@ -64,6 +69,14 @@ def tile_lorentzmla_pa_t_kernel(
         for n in range(SUB):
             nc.sync.dma_start(out=x_first[:, n, :], in_=x_groups[0][:, n, :])
         x_sb[0] = x_first
+        b_bf = once.tile([P, SUB], BF16)
+        nc.sync.dma_start(out=b_bf[:], in_=wkv_a_b[0:KV_RANK].rearrange("(p t) -> p t", t=SUB))
+        w_bf = once.tile([P, SUB], BF16)
+        nc.sync.dma_start(out=w_bf[:], in_=kv_norm_w.rearrange("(p t) -> p t", t=SUB))
+        bpe_bf = once.tile([P, 2], BF16)
+        bpe_rows = wkv_a_b[KV_RANK : KV_RANK + ROPE].rearrange("(j e) -> e j", e=2)
+        for e in range(2):
+            nc.sync.dma_start(out=bpe_bf[e * HALF : (e + 1) * HALF, 0:1], in_=bpe_rows[e].unsqueeze(1))
         wa_kv_sb = five.tile([P, SUB, DIM], BF16, tag="rows")
         wa_kv_rows = wkv_a_w[0:KV_RANK, :].rearrange("(p t) k -> p t k", t=SUB)
         for t in range(SUB):
@@ -72,74 +85,81 @@ def tile_lorentzmla_pa_t_kernel(
         wa_pe_rows = wkv_a_w[KV_RANK : KV_RANK + ROPE, :].rearrange("(j e) k -> e j k", e=2)
         for e in range(2):
             nc.sync.dma_start(out=wa_pe_sb[e * HALF : (e + 1) * HALF, 0, :], in_=wa_pe_rows[e])
-        for g in range(1, 4):
-            load_x(g)
 
-        b_bf = once.tile([P, SUB], BF16)
-        nc.scalar.dma_start(out=b_bf[:], in_=wkv_a_b[0:KV_RANK].rearrange("(p t) -> p t", t=SUB))
-        w_bf = once.tile([P, SUB], BF16)
-        nc.scalar.dma_start(out=w_bf[:], in_=kv_norm_w.rearrange("(p t) -> p t", t=SUB))
-        bpe_bf = once.tile([P, 2], BF16)
-        bpe_rows = wkv_a_b[KV_RANK : KV_RANK + ROPE].rearrange("(j e) -> e j", e=2)
-        for e in range(2):
-            nc.scalar.dma_start(out=bpe_bf[e * HALF : (e + 1) * HALF, 0:1], in_=bpe_rows[e].unsqueeze(1))
         wb_full = once.tile([P, 2, KV_RANK + 1], BF16)
-        nc.scalar.dma_start(out=wb_full[:], in_=wkv_b_w.rearrange("(o p) k -> p o k", p=P))
+        nc.sync.dma_start(out=wb_full[:], in_=wkv_b_w.rearrange("(o p) k -> p o k", p=P))
         vec_rows = once.tile([P, KV2], BF16)
         nc.vector.memset(vec_rows[:], 0.0)
-        nc.scalar.dma_start(out=vec_rows[0:1, 0:KV2], in_=wkv_b_b.unsqueeze(0))
+        nc.sync.dma_start(out=vec_rows[0:1, 0:KV2], in_=wkv_b_b.unsqueeze(0))
         cos_t = once.tile([P, TABLE_HALVES, SUB, HALF], BF16)
-        nc.scalar.dma_start(out=cos_t[:], in_=freqs_cos.rearrange("(a p n) j -> p a n j", p=P, n=SUB))
+        nc.sync.dma_start(out=cos_t[:], in_=freqs_cos.rearrange("(a p n) j -> p a n j", p=P, n=SUB))
         sin_t = once.tile([P, TABLE_HALVES, SUB, HALF], BF16)
-        nc.scalar.dma_start(out=sin_t[:], in_=freqs_sin.rearrange("(a p n) j -> p a n j", p=P, n=SUB))
+        nc.sync.dma_start(out=sin_t[:], in_=freqs_sin.rearrange("(a p n) j -> p a n j", p=P, n=SUB))
+        for g in range(1, 4):
+            load_x(g)
 
         ident = once.tile([P, P], F32)
         make_identity(nc, ident[:])
         ones_bf = once.tile([P, P], BF16)
         nc.vector.memset(ones_bf[:], 1.0)
 
+        def keep_warm(count, pool, tag):
+            bank = pool.tile([P, 512], F32, tag=tag)
+            for k in range(count):
+                nc.tensor.matmul(out=bank[:], lhsT=ones_bf[:], rhs=warm_rows[:], start=True, stop=True)
+
+        warm_rows = once.tile([P, 512], BF16)
+        nc.vector.memset(warm_rows[:], 0.0)
+
         b32 = once.tile([P, SUB], F32)
-        nc.vector.tensor_copy(out=b32[:], in_=b_bf[:])
         w32 = once.tile([P, SUB], F32)
-        nc.vector.tensor_copy(out=w32[:], in_=w_bf[:])
         bw32 = once.tile([P, SUB], F32)
-        nc.vector.tensor_tensor(out=bw32[:], in0=b32[:], in1=w32[:], op=ALU.mult)
         w_sq = once.tile([P, SUB], F32)
-        nc.vector.tensor_tensor(out=w_sq[:], in0=w32[:], in1=w32[:], op=ALU.mult)
         sum_cols = once.tile([P, SUB, 4], BF16)
-        nc.vector.memset(sum_cols[:], 0.0)
-        nc.vector.memset(sum_cols[:, :, 0], 1.0)
-        nc.vector.tensor_copy(out=sum_cols[:, :, 1], in_=w_sq[:])
-        nc.vector.tensor_tensor(out=sum_cols[:, :, 2], in0=w_sq[:], in1=sum_cols[:, :, 1], op=ALU.subtract)
         bpe32 = once.tile([P, 1], F32)
-        nc.vector.tensor_copy(out=bpe32[:], in_=bpe_bf[:, 0:1])
         pair_own = once.tile([P, P], F32)
         pair_swap = once.tile([P, P], F32)
-        for e in range(2):
-            source = ident[:, e * HALF : (e + 1) * HALF]
-            nc.vector.tensor_copy(out=pair_own[:].rearrange("p (j e) -> p e j", e=2)[:, e, :], in_=source)
-            nc.vector.tensor_copy(out=pair_swap[:].rearrange("p (j e) -> p e j", e=2)[:, 1 - e, :], in_=source)
+
+        def feature_constants():
+            nc.vector.tensor_copy(out=b32[:], in_=b_bf[:])
+            nc.vector.tensor_copy(out=w32[:], in_=w_bf[:])
+            nc.vector.tensor_tensor(out=bw32[:], in0=b32[:], in1=w32[:], op=ALU.mult)
+
+        def sum_constants():
+            nc.vector.tensor_tensor(out=w_sq[:], in0=w32[:], in1=w32[:], op=ALU.mult)
+            nc.vector.memset(sum_cols[:], 0.0)
+            nc.vector.memset(sum_cols[:, :, 0], 1.0)
+            nc.vector.tensor_copy(out=sum_cols[:, :, 1], in_=w_sq[:])
+            nc.vector.tensor_tensor(out=sum_cols[:, :, 2], in0=w_sq[:], in1=sum_cols[:, :, 1], op=ALU.subtract)
+
+        def pair_constants():
+            nc.vector.tensor_copy(out=bpe32[:], in_=bpe_bf[:, 0:1])
+            for e in range(2):
+                source = ident[:, e * HALF : (e + 1) * HALF]
+                nc.vector.tensor_copy(out=pair_own[:].rearrange("p (j e) -> p e j", e=2)[:, e, :], in_=source)
+                nc.vector.tensor_copy(out=pair_swap[:].rearrange("p (j e) -> p e j", e=2)[:, 1 - e, :], in_=source)
+
         ident_bf = once.tile([P, P], BF16)
         make_identity(nc, ident_bf[:])
-        cos_f = once.tile([P, TABLE_HALVES, SUB, P], BF16)
-        sin_f = once.tile([P, TABLE_HALVES, SUB, P], BF16)
+        rope_tables = once.tile([P, TABLE_HALVES, 2, SUB, P], BF16)
+        twins = once.tile([P, 2, TABLE_HALVES, SUB, 2, HALF], BF16)
 
-        cos_twin = once.tile([P, TABLE_HALVES, SUB, 2, HALF], BF16)
-        sin_twin = once.tile([P, TABLE_HALVES, SUB, 2, HALF], BF16)
+        def twin_table(k):
+            rows = (cos_t, sin_t)[k]
+            for e in range(2):
+                sign = -1.0 if k == 1 and e == 1 else 1.0
+                nc.gpsimd.tensor_scalar(
+                    out=twins[:, k, :, :, e, :], in0=rows[:], scalar1=sign, scalar2=0.0, op0=ALU.mult, op1=ALU.add
+                )
 
-        def twin_tables():
-            for twin, rows, signs in ((cos_twin, cos_t, (1.0, 1.0)), (sin_twin, sin_t, (1.0, -1.0))):
-                for e in range(2):
-                    nc.vector.tensor_scalar(
-                        out=twin[:, :, :, e, :], in0=rows[:], scalar1=signs[e], scalar2=None, op0=ALU.mult
-                    )
-
-        def turn_tables(half):
-            for table, twin in ((cos_f, cos_twin), (sin_f, sin_twin)):
-                turned = psum_rope.tile([P, SUB, P], BF16, tag="rope")
+        def turn_tables(half, pool, tag):
+            turned = pool.tile([P, 2, SUB, P], BF16, tag=tag)
+            for k in range(2):
                 for n in range(SUB):
-                    nc.tensor.transpose(turned[:, n, :], twin[:, half, n, :, :].rearrange("p e j -> p (e j)"), ident_bf[:])
-                nc.vector.tensor_copy(out=table[:, half, :, :], in_=turned[:])
+                    nc.tensor.transpose(
+                        turned[:, k, n, :], twins[:, k, half, n, :, :].rearrange("p e j -> p (e j)"), ident_bf[:]
+                    )
+            nc.scalar.copy(out=rope_tables[:, half, :, :, :], in_=turned[:])
 
         def flip_place(rows_sb, grouped, n, copy):
             rows_words = rows_sb[:].bitcast(F32)[:, n, :]
@@ -152,8 +172,8 @@ def tile_lorentzmla_pa_t_kernel(
         wa_kv_scales = once.tile([P, PASSES, KV_RANK], U8, align_bytes=64)
         wa_grouped = once.tile([P, PASSES, SUB, P, 4], BF16, align_bytes=64)
 
-        def flip_wa(t):
-            flip_place(wa_kv_sb, wa_grouped, t, nc.vector.tensor_copy)
+        def flip_wa(t, copy):
+            flip_place(wa_kv_sb, wa_grouped, t, copy)
 
         def quantise_wa(t):
             for a in range(PASSES):
@@ -168,7 +188,7 @@ def tile_lorentzmla_pa_t_kernel(
         pe_grouped = once.tile([P, PASSES, 1, P, 4], BF16, align_bytes=64)
 
         def flip_wa_rope():
-            flip_place(wa_pe_sb, pe_grouped, 0, nc.vector.tensor_copy)
+            flip_place(wa_pe_sb, pe_grouped, 0, nc.scalar.copy)
 
         def quantise_wa_rope():
             for a in range(PASSES):
@@ -182,11 +202,11 @@ def tile_lorentzmla_pa_t_kernel(
         x_codes = {}
         x_scales = {}
 
-        def flip_x(g, n):
+        def flip_x(g, n, copy=nc.scalar.copy):
             if n == 0:
                 grouped = twice.tile([P, PASSES, SUB, P, 4], BF16, tag="grouped", align_bytes=64)
                 x_grouped[g] = grouped
-            flip_place(x_sb[g], x_grouped[g], n, nc.scalar.copy)
+            flip_place(x_sb[g], x_grouped[g], n, copy)
 
         def quantise_x(g):
             codes = twice.tile([P, PASSES, GROUP], U32, tag="x_codes", align_bytes=64)
@@ -200,15 +220,11 @@ def tile_lorentzmla_pa_t_kernel(
             x_codes[g] = codes
             x_scales[g] = scales
 
-        bb_all = once.tile([P, KV2], F32)
+        second_vectors = once.tile([P, 2, KV2], F32)
+        bb_all = second_vectors[:, 0, :]
+        wb0_all = second_vectors[:, 1, :]
         wb_codes = once.tile([P, KV2], U32, align_bytes=64)
         wb_scales = once.tile([P, KV2], U8, align_bytes=64)
-        wb0_all = once.tile([P, KV2], F32)
-
-        def prepare_vectors():
-            vec_bank = psum_kv2.tile([P, 512], F32, tag="kv2")
-            nc.tensor.matmul(out=vec_bank[:, 0:KV2], lhsT=ones_bf[:], rhs=vec_rows[:], start=True, stop=True)
-            nc.vector.tensor_copy(out=bb_all[:], in_=vec_bank[:, 0:KV2])
 
         wb_even = once.tile([P, 2, KV_RANK], BF16)
         wb_grouped = once.tile([P, KV2, 4], BF16, align_bytes=64)
@@ -234,13 +250,19 @@ def tile_lorentzmla_pa_t_kernel(
                 out=wb_codes[:].bitcast(FP8X4), scales=wb_scales[:], in_=wb_grouped[:].rearrange("q c j -> q (c j)")
             )
 
-        def spread_wb0():
-            wb0_bank = psum_kv2.tile([P, 512], F32, tag="kv2")
+        second_bank = []
+
+        def prepare_second_product():
+            bank = psum_kv2.tile([P, 2, KV2], F32, tag="kv2")
+            nc.tensor.matmul(out=bank[:, 0, :], lhsT=ones_bf[:], rhs=vec_rows[:], start=True, stop=True)
             for o in range(2):
                 nc.tensor.transpose(
-                    wb0_bank[:, o * P : (o + 1) * P], wb0_col[:, o : o + 1].to_broadcast([P, P]), ident[:]
+                    bank[:, 1, o * P : (o + 1) * P], wb0_col[:, o : o + 1].to_broadcast([P, P]), ident[:]
                 )
-            nc.vector.tensor_copy(out=wb0_all[:], in_=wb0_bank[:, 0:KV2])
+            second_bank.append(bank)
+
+        def copy_second():
+            nc.vector.tensor_copy(out=second_vectors[:], in_=second_bank[0][:])
 
         squares = {}
         squares_rest = {}
@@ -294,11 +316,11 @@ def tile_lorentzmla_pa_t_kernel(
         def upper_halves(tile_f32):
             return tile_f32[:].bitcast(BF16).rearrange("p t (c h) -> p t c h", h=2)[:, :, :, 1]
 
-        def square_rest(g, t):
+        def square_rest(g, t, engine):
             if t == 0:
                 rest_new = twice.tile([P, SUB, GROUP], BF16, tag="sq_rest")
                 squares_rest[g] = rest_new
-            (nc.gpsimd if g > 0 else nc.vector).tensor_tensor(
+            engine.tensor_tensor(
                 out=squares_rest[g][:, t, :],
                 in0=squares[g][:, t, :],
                 in1=upper_halves(squares[g])[:, t, :],
@@ -323,13 +345,12 @@ def tile_lorentzmla_pa_t_kernel(
             rope_banks[g] = bank
 
         def rope_multiply(g, part):
-            table = (cos_f, sin_f)[part]
             result = twice.tile([P, GROUP], F32, tag="rope_part%d" % part)
             nc.vector.scalar_tensor_tensor(
                 out=result[:],
                 in0=rope_banks[g][:],
                 scalar=bpe32[:, 0:1],
-                in1=table[:, g % TABLE_HALVES, :, :].rearrange("p n r -> p (n r)"),
+                in1=rope_tables[:, g % TABLE_HALVES, part, :, :].rearrange("p n r -> p (n r)"),
                 op0=ALU.add,
                 op1=ALU.mult,
             )
@@ -422,24 +443,31 @@ def tile_lorentzmla_pa_t_kernel(
                 )
             spread_of[g] = spread
 
-        def norm(g):
-            sp_grouped = once.tile([P, GROUP, SUB], BF16, tag="sp_grouped", align_bytes=64)
+        def norm(g, places):
+            if places.start == 0:
+                rows_new = once.tile([P, GROUP, SUB], BF16, tag="sp_grouped", align_bytes=64)
+                sp_rows[g] = rows_new
+            cols = slice(places.start * P, places.stop * P)
+            width = cols.stop - cols.start
             nc.vector.tensor_tensor(
-                out=sp_grouped[:],
-                in0=kv_w[g][:].rearrange("p t c -> p c t"),
-                in1=spread_of[g][:].unsqueeze(2).to_broadcast([P, GROUP, SUB]),
+                out=sp_rows[g][:, cols, :],
+                in0=kv_w[g][:, :, cols].rearrange("p t c -> p c t"),
+                in1=spread_of[g][:, cols].unsqueeze(2).to_broadcast([P, width, SUB]),
                 op=ALU.mult,
             )
-            sp_rows[g] = sp_grouped
 
-        def quantise_sp(g):
-            codes = twice.tile([P, GROUP], U32, tag="sp_codes", align_bytes=64)
-            scales = twice.tile([P, GROUP], U8, tag="sp_scales", align_bytes=64)
+        def quantise_sp(g, places):
+            if places.start == 0:
+                codes_new = twice.tile([P, GROUP], U32, tag="sp_codes", align_bytes=64)
+                scales_new = twice.tile([P, GROUP], U8, tag="sp_scales", align_bytes=64)
+                sp_codes[g] = codes_new
+                sp_scales[g] = scales_new
+            cols = slice(places.start * P, places.stop * P)
             nc.vector.quantize_mx(
-                out=codes[:].bitcast(FP8X4), scales=scales[:], in_=sp_rows[g][:].rearrange("p c t -> p (c t)")
+                out=sp_codes[g][:, cols].bitcast(FP8X4),
+                scales=sp_scales[g][:, cols],
+                in_=sp_rows[g][:, cols, :].rearrange("p c t -> p (c t)"),
             )
-            sp_codes[g] = codes
-            sp_scales[g] = scales
 
         ksl_sb = {}
         vs_sb = {}
@@ -469,24 +497,31 @@ def tile_lorentzmla_pa_t_kernel(
                 n = 2 * pair + i
                 nc.vector.scalar_tensor_tensor(
                     out=kv2_sb[g][:, n, :, :].rearrange("p h c -> p (h c)"),
-                    in0=wb0_all[:],
+                    in0=wb0_all,
                     scalar=time_sp[g][:, n : n + 1],
                     in1=kv2_banks[g, pair][:, i, :],
                     op0=ALU.mult,
                     op1=ALU.add,
                 )
 
-        def add_second_bias(g):
+        def add_second_bias(g, places, engine):
             kv2 = kv2_sb[g]
-            ksl = ksl_sb[g]
-            vs = three.tile([P, SUB, HEADS, V_ROW], F32, tag="vs")
-            vs_sb[g] = vs
-            bb4 = bb_all[:].rearrange("p (h c) -> p h c", h=HEADS).unsqueeze(1).to_broadcast([P, SUB, HEADS, NOPE + V_DIM])
-            nc.gpsimd.tensor_tensor(
-                out=ksl[:, :, :, 1 : 1 + NOPE], in0=kv2[:, :, :, 0:NOPE], in1=bb4[:, :, :, 0:NOPE], op=ALU.add
+            if places.start == 0:
+                vs_new = three.tile([P, SUB, HEADS, V_ROW], F32, tag="vs")
+                vs_sb[g] = vs_new
+            count = places.stop - places.start
+            bias = bb_all.rearrange("p (h c) -> p h c", h=HEADS).unsqueeze(1).to_broadcast([P, count, HEADS, NOPE + V_DIM])
+            engine.tensor_tensor(
+                out=ksl_sb[g][:, places, :, 1 : 1 + NOPE],
+                in0=kv2[:, places, :, 0:NOPE],
+                in1=bias[:, :, :, 0:NOPE],
+                op=ALU.add,
             )
-            nc.gpsimd.tensor_tensor(
-                out=vs[:, :, :, 1:V_ROW], in0=kv2[:, :, :, NOPE : NOPE + V_DIM], in1=bb4[:, :, :, NOPE : NOPE + V_DIM], op=ALU.add
+            engine.tensor_tensor(
+                out=vs_sb[g][:, places, :, 1:V_ROW],
+                in0=kv2[:, places, :, NOPE : NOPE + V_DIM],
+                in1=bias[:, :, :, NOPE : NOPE + V_DIM],
+                op=ALU.add,
             )
 
         lift_sums = {}
@@ -532,85 +567,188 @@ def tile_lorentzmla_pa_t_kernel(
             nc.sync.dma_start(out=ksl_groups[g], in_=ksl_sb[g][:].rearrange("p n h f -> p (n h f)"))
             nc.sync.dma_start(out=vs_groups[g], in_=vs_sb[g][:].rearrange("p n h f -> p (n h f)"))
 
+        ALL = slice(0, SUB)
+
         def do(stage, g, *args):
             if 0 <= g < GROUPS:
                 stage(g, *args)
 
         with tc.manual_schedule():
+            keep_warm(3, psum_kv2, "kv2")
             for n in range(SUB):
-                flip_x(0, n)
-            for t in range(SUB):
-                flip_wa(t)
-                if t == 1:
-                    quantise_x(0)
-                quantise_wa(t)
-            for i in range(GROUPS + 3):
-                first = i == 0
-                do(load_x, i + 4)
-                do(kv_product, i, 0)
-                do(kv_square, i, 0)
-                do(kv_weighted, i, 0, first)
-                do(square_rest, i, 0)
-                if first:
-                    flip_x(1, 0)
-                    twin_tables()
-                    align_wkv_b()
-                    prepare_vectors()
+                flip_x(0, n, nc.vector.tensor_copy if n % 2 == 1 else nc.scalar.copy)
+            quantise_x(0)
+            flip_wa(0, nc.scalar.copy)
+            quantise_wa(0)
+            feature_constants()
+            flip_wa(1, nc.scalar.copy)
+            quantise_wa(1)
+            sum_constants()
+            flip_wa(2, nc.scalar.copy)
+            kv_product(0, 0)
+            quantise_wa(2)
+            align_wkv_b()
+            kv_square(0, 0)
+            kv_weighted(0, 0, True)
+            square_rest(0, 0, nc.gpsimd)
+            flip_wa(3, nc.scalar.copy)
+            kv_product(0, 1)
+            quantise_wa(3)
+            kv_square(0, 1)
+            kv_weighted(0, 1, True)
+            square_rest(0, 1, nc.vector)
+            flip_wa_rope()
+            kv_product(0, 2)
+            kv_square(0, 2)
+            kv_weighted(0, 2, True)
+            square_rest(0, 2, nc.gpsimd)
+            twin_table(0)
+            twin_table(1)
+            flip_x(1, 0)
+            kv_product(0, 3)
+            kv_square(0, 3)
+            kv_weighted(0, 3, True)
+            square_rest(0, 3, nc.vector)
+            flip_x(1, 1)
+            flip_x(1, 2)
+            prepare_second_product()
+            flip_x(1, 3)
+            quantise_wa_rope()
+            flip_wkv_b()
+            rope_product(0)
+            quantise_x(1)
+            feature_sums(0, 0)
+            feature_sums(0, 1)
+            pair_constants()
+            copy_second()
+            load_x(4)
+            kv_product(1, 0)
+            feature_sums(0, 2)
+            feature_sums(0, 3)
+            kv_product(1, 1)
+            quantise_wkv_b()
+            kv_square(1, 0)
+            norm_root(0)
+            kv_weighted(1, 0, False)
+            square_rest(1, 0, nc.gpsimd)
+            turn_tables(0, psum_rope, "rope")
+            spread_rstd(0)
+            turn_tables(1, psum_kv2, "kv2")
+            rope_multiply(0, 0)
+            rope_multiply(0, 1)
+            flip_x(2, 0)
+            kv_square(1, 1)
+            kv_weighted(1, 1, False)
+            kv_product(1, 2)
+            flip_x(2, 1)
+            norm(0, ALL)
+            square_rest(1, 1, nc.gpsimd)
+            rope_turn(0)
+            quantise_sp(0, ALL)
+            time_square(0)
+            kv_square(1, 2)
+            flip_x(2, 2)
+            kv_weighted(1, 2, True)
+            kv_product(1, 3)
+            flip_x(2, 3, nc.vector.tensor_copy)
+            quantise_x(2)
+            square_rest(1, 2, nc.gpsimd)
+            kv_square(1, 3)
+            kv_weighted(1, 3, True)
+            square_rest(1, 3, nc.gpsimd)
+            time_root(0)
+            second_product(0, 0)
+            flip_x(3, 0)
+            flip_x(3, 1, nc.vector.tensor_copy)
+            rope_product(1)
+            flip_x(3, 2)
+            flip_x(3, 3, nc.vector.tensor_copy)
+            for i in range(2, GROUPS):
                 do(lift_stats, i - 3, 0)
+                do(kv_product, i, 0)
                 do(lift_stats, i - 3, 1)
-                do(second_product, i - 2, 0)
                 do(add_time_term, i - 2, 0)
-                do(lift_stats, i - 3, 2)
-                do(lift_stats, i - 3, 3)
                 do(feature_sums, i - 1, 0)
+                do(quantise_x, i + 1)
                 do(feature_sums, i - 1, 1)
-                do(kv_product, i, 1)
-                if not first:
-                    do(quantise_x, i + 1)
-                do(kv_square, i, 1)
-                do(lift_combine, i - 3)
-                do(lift_roots_and_store, i - 3)
+                do(lift_stats, i - 3, 2)
+                do(rope_multiply, i - 1, 0)
+                do(kv_square, i, 0)
                 do(second_product, i - 2, 1)
+                do(kv_weighted, i, 0, False)
+                do(kv_product, i, 1)
+                do(rope_rows, i - 2)
                 do(add_time_term, i - 2, 1)
-                do(kv_weighted, i, 1, True)
-                if first:
-                    flip_x(1, 1)
-                    flip_wa_rope()
-                    quantise_wa_rope()
-                    spread_wb0()
-                do(square_rest, i, 1)
-                do(add_second_bias, i - 2)
+                do(square_rest, i, 0, nc.gpsimd)
+                do(rope_multiply, i - 1, 1)
+                do(load_x, i + 3)
                 do(feature_sums, i - 1, 2)
+                do(add_second_bias, i - 2, ALL, nc.gpsimd)
+                do(kv_square, i, 1)
                 do(feature_sums, i - 1, 3)
+                do(lift_stats, i - 3, 3)
                 do(norm_root, i - 1)
-                do(kv_product, i, 2)
-                do(kv_square, i, 2)
-                do(kv_weighted, i, 2, first)
-                if first:
-                    flip_x(1, 2)
-                    flip_x(1, 3)
-                    quantise_x(1)
-                    turn_tables(0)
-                do(spread_rstd, i - 1)
+                do(kv_weighted, i, 1, True)
                 do(flip_x, i + 2, 0)
+                do(kv_product, i, 2)
+                do(spread_rstd, i - 1)
+                do(lift_combine, i - 3)
+                do(kv_square, i, 2)
                 do(flip_x, i + 2, 1)
-                do(norm, i - 1)
-                do(rope_turn, i - 1)
-                do(kv_product, i, 3)
-                do(rope_rows, i - 1)
-                do(kv_square, i, 3)
-                do(kv_weighted, i, 3, first)
-                do(rope_product, i)
-                do(square_rest, i, 2)
-                do(time_square, i - 1)
-                do(time_root, i - 1)
-                do(square_rest, i, 3)
+                do(lift_roots_and_store, i - 3)
                 do(flip_x, i + 2, 2)
+                do(kv_weighted, i, 2, False)
+                do(square_rest, i, 1, nc.gpsimd)
+                do(kv_product, i, 3)
+                do(square_rest, i, 2, nc.gpsimd)
+                do(time_square, i - 1)
+                do(norm, i - 1, ALL)
+                do(kv_square, i, 3)
+                do(square_rest, i, 3, nc.gpsimd)
+                do(rope_turn, i - 1)
                 do(flip_x, i + 2, 3)
-                if first:
-                    turn_tables(1)
-                    flip_wkv_b()
-                    quantise_wkv_b()
-                do(quantise_sp, i - 1)
-                do(rope_multiply, i, 0)
-                do(rope_multiply, i, 1)
+                do(time_root, i - 1)
+                do(kv_weighted, i, 3, False)
+                do(quantise_sp, i - 1, ALL)
+                do(rope_product, i)
+                do(second_product, i - 1, 0)
+            second_product(6, 1)
+            add_time_term(6, 0)
+            for n in range(SUB):
+                feature_sums(7, n)
+            lift_stats(5, 0)
+            lift_stats(5, 1)
+            rope_rows(6)
+            add_time_term(6, 1)
+            rope_multiply(7, 0)
+            rope_multiply(7, 1)
+            add_second_bias(6, ALL, nc.gpsimd)
+            norm_root(7)
+            keep_warm(2, psum_y, "y")
+            spread_rstd(7)
+            time_square(7)
+            time_root(7)
+            rope_turn(7)
+            lift_stats(5, 2)
+            lift_stats(5, 3)
+            norm(7, slice(0, 2))
+            quantise_sp(7, slice(0, 2))
+            second_product(7, 0)
+            norm(7, slice(2, 4))
+            lift_combine(5)
+            lift_roots_and_store(5)
+            rope_rows(7)
+            add_time_term(7, 0)
+            quantise_sp(7, slice(2, 4))
+            second_product(7, 1)
+            add_second_bias(7, slice(0, 2), nc.vector)
+            for n in range(SUB):
+                lift_stats(6, n)
+            add_time_term(7, 1)
+            add_second_bias(7, slice(2, 4), nc.vector)
+            lift_combine(6)
+            lift_roots_and_store(6)
+            for n in range(SUB):
+                lift_stats(7, n)
+            lift_combine(7)
+            lift_roots_and_store(7)

@@ -449,10 +449,11 @@ def tile_lorentzmla_pa_t_kernel(
                 sp_rows[g] = rows_new
             cols = slice(places.start * P, places.stop * P)
             width = cols.stop - cols.start
+            quads = width // 4
             nc.vector.tensor_tensor(
-                out=sp_rows[g][:, cols, :],
-                in0=kv_w[g][:, :, cols].rearrange("p t c -> p c t"),
-                in1=spread_of[g][:, cols].unsqueeze(2).to_broadcast([P, width, SUB]),
+                out=sp_rows[g][:, cols, :].rearrange("p (c i) t -> p c t i", i=4),
+                in0=kv_w[g][:, :, cols].rearrange("p t (c i) -> p c t i", i=4),
+                in1=spread_of[g][:, cols].rearrange("p (c i) -> p c i", i=4).unsqueeze(2).to_broadcast([P, quads, SUB, 4]),
                 op=ALU.mult,
             )
 

@@ -448,8 +448,7 @@ def tile_lorentzmla_pa_t_kernel(
                 rows_new = once.tile([P, GROUP, SUB], BF16, tag="sp_grouped", align_bytes=64)
                 sp_rows[g] = rows_new
             cols = slice(places.start * P, places.stop * P)
-            width = cols.stop - cols.start
-            quads = width // 4
+            quads = (cols.stop - cols.start) // 4
             nc.vector.tensor_tensor(
                 out=sp_rows[g][:, cols, :].rearrange("p (c i) t -> p c t i", i=4),
                 in0=kv_w[g][:, :, cols].rearrange("p t (c i) -> p c t i", i=4),
@@ -505,50 +504,70 @@ def tile_lorentzmla_pa_t_kernel(
                     op1=ALU.add,
                 )
 
-        def add_second_bias(g, places, engine):
-            kv2 = kv2_sb[g]
+        def second_bias(places):
+            rows = bb_all.rearrange("p (h c) -> p h c", h=HEADS).unsqueeze(1)
+            return rows.to_broadcast([P, places.stop - places.start, HEADS, NOPE + V_DIM])
+
+        def bias_k(g, places, engine):
+            engine.tensor_tensor(
+                out=ksl_sb[g][:, places, :, 1 : 1 + NOPE],
+                in0=kv2_sb[g][:, places, :, 0:NOPE],
+                in1=second_bias(places)[:, :, :, 0:NOPE],
+                op=ALU.add,
+            )
+
+        def bias_v(g, places, engine):
             if places.start == 0:
                 vs_new = three.tile([P, SUB, HEADS, V_ROW], F32, tag="vs")
                 vs_sb[g] = vs_new
-            count = places.stop - places.start
-            bias = bb_all.rearrange("p (h c) -> p h c", h=HEADS).unsqueeze(1).to_broadcast([P, count, HEADS, NOPE + V_DIM])
-            engine.tensor_tensor(
-                out=ksl_sb[g][:, places, :, 1 : 1 + NOPE],
-                in0=kv2[:, places, :, 0:NOPE],
-                in1=bias[:, :, :, 0:NOPE],
-                op=ALU.add,
-            )
             engine.tensor_tensor(
                 out=vs_sb[g][:, places, :, 1:V_ROW],
-                in0=kv2[:, places, :, NOPE : NOPE + V_DIM],
-                in1=bias[:, :, :, NOPE : NOPE + V_DIM],
+                in0=kv2_sb[g][:, places, :, NOPE : NOPE + V_DIM],
+                in1=second_bias(places)[:, :, :, NOPE : NOPE + V_DIM],
                 op=ALU.add,
             )
 
-        lift_sums = {}
-
-        def lift_stats(g, n):
-            if n == 0:
-                stats_new = twice.tile([P, SUB, 2, 2, 3], F32, tag="stats")
-                v_new = twice.tile([P, SUB, HEADS], F32, tag="v_sums")
-                lift_sums[g] = (stats_new, v_new)
-            stats, v_sums = lift_sums[g]
-            rows = (
-                ksl_sb[g][:, n, :, 1 : 1 + NOPE].rearrange("p h c -> p c h"),
-                ksl_sb[g][:, n, 0, 1 + NOPE : K_ROW],
-            )
-            for k in range(2):
-                nc.vector.bn_stats(out=stats[:, n, k, :, :].rearrange("p e s -> p (e s)"), in_=rows[k])
-            for h in range(HEADS):
-                junk_v = twice.tile([P, V_DIM], BF16, tag="junk_v")
-                nc.scalar.activation(
-                    out=junk_v[:], in_=vs_sb[g][:, n, h, 1:V_ROW], func=ACT.Square, accum_out=v_sums[:, n, h : h + 1]
-                )
-
+        k_stats = {}
+        v_sums = {}
         k_sums = {}
 
+        def stats_of(g):
+            if g not in k_stats:
+                stats_new = twice.tile([P, SUB, 2, 2, 3], F32, tag="stats")
+                k_stats[g] = stats_new
+            return k_stats[g]
+
+        def lift_nope(g, n):
+            nc.vector.bn_stats(
+                out=stats_of(g)[:, n, 0, :, :].rearrange("p e s -> p (e s)"),
+                in_=ksl_sb[g][:, n, :, 1 : 1 + NOPE].rearrange("p h c -> p c h"),
+            )
+
+        def lift_rope(g, n):
+            nc.vector.bn_stats(
+                out=stats_of(g)[:, n, 1, :, :].rearrange("p e s -> p (e s)"), in_=ksl_sb[g][:, n, 0, 1 + NOPE : K_ROW]
+            )
+
+        def sum_squares(out, in_):
+            junk = twice.tile([P, K_ROW], BF16, tag="junk")
+            nc.scalar.activation(out=junk[:, 0 : in_.shape[1]], in_=in_, func=ACT.Square, accum_out=out)
+
+        def lift_rows(g, n):
+            if n == 0:
+                sums_new = twice.tile([P, SUB, HEADS], F32, tag="k_sum")
+                k_sums[g] = sums_new
+            for h in range(HEADS):
+                sum_squares(k_sums[g][:, n, h : h + 1], ksl_sb[g][:, n, h, 1:K_ROW])
+
+        def lift_v(g, n):
+            if n == 0:
+                v_new = twice.tile([P, SUB, HEADS], F32, tag="v_sums")
+                v_sums[g] = v_new
+            for h in range(HEADS):
+                sum_squares(v_sums[g][:, n, h : h + 1], vs_sb[g][:, n, h, 1:V_ROW])
+
         def lift_combine(g):
-            stats = lift_sums[g][0]
+            stats = k_stats[g]
             nc.scalar.activation(out=stats[:, :, :, :, 0], in_=stats[:, :, :, :, 1], func=ACT.Square, scale=8.0)
             nope_sum = twice.tile([P, SUB, HEADS], F32, tag="nope_sum")
             nc.vector.tensor_reduce(out=nope_sum[:], in_=stats[:, :, 0, :, 0::2], axis=AXIS.X, op=ALU.add)
@@ -560,12 +579,12 @@ def tile_lorentzmla_pa_t_kernel(
             )
             k_sums[g] = k_sum
 
-        def lift_roots_and_store(g):
-            k_sum = k_sums[g]
-            v_sums = lift_sums[g][1]
-            nc.scalar.activation(out=ksl_sb[g][:, :, :, 0], in_=k_sum[:], func=ACT.Sqrt, bias=1.0, scale=1.0)
-            nc.scalar.activation(out=vs_sb[g][:, :, :, 0], in_=v_sums[:], func=ACT.Sqrt, bias=1.0, scale=1.0)
+        def finish_k(g):
+            nc.scalar.activation(out=ksl_sb[g][:, :, :, 0], in_=k_sums[g][:], func=ACT.Sqrt, bias=1.0, scale=1.0)
             nc.sync.dma_start(out=ksl_groups[g], in_=ksl_sb[g][:].rearrange("p n h f -> p (n h f)"))
+
+        def finish_v(g):
+            nc.scalar.activation(out=vs_sb[g][:, :, :, 0], in_=v_sums[g][:], func=ACT.Sqrt, bias=1.0, scale=1.0)
             nc.sync.dma_start(out=vs_groups[g], in_=vs_sb[g][:].rearrange("p n h f -> p (n h f)"))
 
         ALL = slice(0, SUB)
@@ -578,178 +597,206 @@ def tile_lorentzmla_pa_t_kernel(
             keep_warm(3, psum_kv2, "kv2")
             for n in range(SUB):
                 flip_x(0, n, nc.vector.tensor_copy if n % 2 == 1 else nc.scalar.copy)
-            quantise_x(0)
             flip_wa(0, nc.scalar.copy)
-            quantise_wa(0)
-            feature_constants()
             flip_wa(1, nc.scalar.copy)
+            quantise_x(0)
+            feature_constants()
+            quantise_wa(0)
             quantise_wa(1)
-            sum_constants()
             flip_wa(2, nc.scalar.copy)
             kv_product(0, 0)
-            quantise_wa(2)
-            align_wkv_b()
-            kv_square(0, 0)
-            kv_weighted(0, 0, True)
-            square_rest(0, 0, nc.gpsimd)
             flip_wa(3, nc.scalar.copy)
-            kv_product(0, 1)
-            quantise_wa(3)
-            kv_square(0, 1)
-            kv_weighted(0, 1, True)
-            square_rest(0, 1, nc.vector)
-            flip_wa_rope()
-            kv_product(0, 2)
-            kv_square(0, 2)
-            kv_weighted(0, 2, True)
-            square_rest(0, 2, nc.gpsimd)
+            align_wkv_b()
             twin_table(0)
-            twin_table(1)
+            flip_wa_rope()
+            kv_product(0, 1)
+            sum_constants()
+            kv_square(0, 0)
+            prepare_second_product()
+            quantise_wa(2)
             flip_x(1, 0)
+            kv_square(0, 1)
+            flip_x(1, 1)
+            twin_table(1)
+            quantise_wa(3)
+            kv_weighted(0, 0, True)
+            kv_product(0, 2)
+            kv_weighted(0, 1, True)
+            kv_square(0, 2)
+            flip_x(1, 2)
+            flip_wkv_b()
             kv_product(0, 3)
             kv_square(0, 3)
-            kv_weighted(0, 3, True)
-            square_rest(0, 3, nc.vector)
-            flip_x(1, 1)
-            flip_x(1, 2)
-            prepare_second_product()
-            flip_x(1, 3)
             quantise_wa_rope()
-            flip_wkv_b()
+            square_rest(0, 0, nc.gpsimd)
+            turn_tables(0, psum_rope, "rope")
+            flip_x(1, 3)
             rope_product(0)
+            square_rest(0, 1, nc.vector)
+            pair_constants()
+            kv_weighted(0, 2, True)
+            square_rest(0, 2, nc.gpsimd)
+            square_rest(0, 3, nc.vector)
+            quantise_wkv_b()
             quantise_x(1)
             feature_sums(0, 0)
             feature_sums(0, 1)
-            pair_constants()
             copy_second()
-            load_x(4)
             kv_product(1, 0)
             feature_sums(0, 2)
             feature_sums(0, 3)
+            kv_weighted(0, 3, True)
             kv_product(1, 1)
-            quantise_wkv_b()
             kv_square(1, 0)
             norm_root(0)
             kv_weighted(1, 0, False)
-            square_rest(1, 0, nc.gpsimd)
-            turn_tables(0, psum_rope, "rope")
-            spread_rstd(0)
-            turn_tables(1, psum_kv2, "kv2")
-            rope_multiply(0, 0)
-            rope_multiply(0, 1)
-            flip_x(2, 0)
             kv_square(1, 1)
+            flip_x(2, 0)
+            square_rest(1, 0, nc.gpsimd)
             kv_weighted(1, 1, False)
-            kv_product(1, 2)
-            flip_x(2, 1)
-            norm(0, ALL)
+            spread_rstd(0)
+            rope_multiply(0, 0)
             square_rest(1, 1, nc.gpsimd)
-            rope_turn(0)
-            quantise_sp(0, ALL)
-            time_square(0)
-            kv_square(1, 2)
+            flip_x(2, 1)
+            kv_product(1, 2)
             flip_x(2, 2)
-            kv_weighted(1, 2, True)
-            kv_product(1, 3)
+            turn_tables(1, psum_kv2, "kv2")
+            rope_multiply(0, 1)
+            norm(0, ALL)
             flip_x(2, 3, nc.vector.tensor_copy)
-            quantise_x(2)
-            square_rest(1, 2, nc.gpsimd)
-            kv_square(1, 3)
-            kv_weighted(1, 3, True)
-            square_rest(1, 3, nc.gpsimd)
-            time_root(0)
-            second_product(0, 0)
+            kv_square(1, 2)
+            time_square(0)
+            kv_product(1, 3)
             flip_x(3, 0)
-            flip_x(3, 1, nc.vector.tensor_copy)
+            square_rest(1, 2, nc.gpsimd)
+            flip_x(3, 1)
+            quantise_x(2)
             rope_product(1)
+            kv_square(1, 3)
             flip_x(3, 2)
-            flip_x(3, 3, nc.vector.tensor_copy)
+            kv_weighted(1, 2, True)
+            kv_weighted(1, 3, True)
+            rope_turn(0)
+            time_root(0)
+            quantise_sp(0, ALL)
+            flip_x(3, 3)
+            square_rest(1, 3, nc.gpsimd)
+            load_x(4)
             for i in range(2, GROUPS):
-                do(lift_stats, i - 3, 0)
+                do(load_x, i + 3)
                 do(kv_product, i, 0)
-                do(lift_stats, i - 3, 1)
-                do(add_time_term, i - 2, 0)
                 do(feature_sums, i - 1, 0)
-                do(quantise_x, i + 1)
                 do(feature_sums, i - 1, 1)
-                do(lift_stats, i - 3, 2)
+                do(kv_product, i, 1)
                 do(rope_multiply, i - 1, 0)
                 do(kv_square, i, 0)
-                do(second_product, i - 2, 1)
                 do(kv_weighted, i, 0, False)
-                do(kv_product, i, 1)
-                do(rope_rows, i - 2)
-                do(add_time_term, i - 2, 1)
-                do(square_rest, i, 0, nc.gpsimd)
+                do(second_product, i - 2, 0)
                 do(rope_multiply, i - 1, 1)
-                do(load_x, i + 3)
                 do(feature_sums, i - 1, 2)
-                do(add_second_bias, i - 2, ALL, nc.gpsimd)
-                do(kv_square, i, 1)
                 do(feature_sums, i - 1, 3)
-                do(lift_stats, i - 3, 3)
-                do(norm_root, i - 1)
-                do(kv_weighted, i, 1, True)
-                do(flip_x, i + 2, 0)
+                do(bias_v, i - 3, ALL, nc.gpsimd)
+                do(lift_nope, i - 3, 0)
+                do(lift_rope, i - 3, 0)
+                do(kv_square, i, 1)
+                do(square_rest, i, 0, nc.gpsimd)
                 do(kv_product, i, 2)
-                do(spread_rstd, i - 1)
-                do(lift_combine, i - 3)
+                do(quantise_x, i + 1)
+                do(add_time_term, i - 2, 0)
+                do(second_product, i - 2, 1)
+                do(lift_nope, i - 3, 1)
+                do(lift_rope, i - 3, 1)
+                do(kv_weighted, i, 1, True)
+                do(rope_rows, i - 2)
+                do(norm_root, i - 1)
                 do(kv_square, i, 2)
-                do(flip_x, i + 2, 1)
-                do(lift_roots_and_store, i - 3)
-                do(flip_x, i + 2, 2)
-                do(kv_weighted, i, 2, False)
+                do(add_time_term, i - 2, 1)
+                do(lift_v, i - 3, 0)
+                do(lift_nope, i - 3, 2)
+                do(lift_rope, i - 3, 2)
+                do(lift_nope, i - 3, 3)
+                do(lift_rope, i - 3, 3)
+                do(flip_x, i + 2, 0)
                 do(square_rest, i, 1, nc.gpsimd)
+                do(flip_x, i + 2, 1)
+                do(lift_v, i - 3, 1)
+                do(spread_rstd, i - 1)
                 do(kv_product, i, 3)
-                do(square_rest, i, 2, nc.gpsimd)
-                do(time_square, i - 1)
-                do(norm, i - 1, ALL)
                 do(kv_square, i, 3)
+                do(square_rest, i, 2, nc.gpsimd)
+                do(bias_k, i - 2, ALL, nc.gpsimd)
+                do(norm, i - 1, ALL)
+                do(kv_weighted, i, 2, False)
                 do(square_rest, i, 3, nc.gpsimd)
-                do(rope_turn, i - 1)
-                do(flip_x, i + 2, 3)
-                do(time_root, i - 1)
+                do(lift_combine, i - 3)
+                do(lift_v, i - 3, 2)
                 do(kv_weighted, i, 3, False)
                 do(quantise_sp, i - 1, ALL)
+                do(lift_v, i - 3, 3)
+                do(rope_turn, i - 1)
+                do(flip_x, i + 2, 2)
                 do(rope_product, i)
-                do(second_product, i - 1, 0)
-            second_product(6, 1)
-            add_time_term(6, 0)
-            for n in range(SUB):
-                feature_sums(7, n)
-            lift_stats(5, 0)
-            lift_stats(5, 1)
-            rope_rows(6)
-            add_time_term(6, 1)
+                do(finish_k, i - 3)
+                do(flip_x, i + 2, 3)
+                do(finish_v, i - 3)
+                do(time_square, i - 1)
+                do(time_root, i - 1)
+            feature_sums(7, 0)
+            feature_sums(7, 1)
+            second_product(6, 0)
+            feature_sums(7, 2)
+            feature_sums(7, 3)
             rope_multiply(7, 0)
+            bias_v(5, ALL, nc.gpsimd)
+            rope_rows(6)
+            add_time_term(6, 0)
+            second_product(6, 1)
             rope_multiply(7, 1)
-            add_second_bias(6, ALL, nc.gpsimd)
+            for n in range(3):
+                lift_rows(5, n)
             norm_root(7)
-            keep_warm(2, psum_y, "y")
-            spread_rstd(7)
+            add_time_term(6, 1)
             time_square(7)
-            time_root(7)
+            bias_k(6, ALL, nc.gpsimd)
+            bias_v(6, ALL, nc.gpsimd)
+            spread_rstd(7)
             rope_turn(7)
-            lift_stats(5, 2)
-            lift_stats(5, 3)
+            lift_rows(5, 3)
+            finish_k(5)
+            time_root(7)
+            for n in range(SUB):
+                lift_v(5, n)
+            finish_v(5)
+            lift_rows(6, 0)
+            rope_rows(7)
             norm(7, slice(0, 2))
             quantise_sp(7, slice(0, 2))
+            keep_warm(1, psum_y, "y")
             second_product(7, 0)
             norm(7, slice(2, 4))
-            lift_combine(5)
-            lift_roots_and_store(5)
-            rope_rows(7)
+            lift_rows(6, 1)
+            lift_rows(6, 2)
+            lift_rows(6, 3)
+            finish_k(6)
             add_time_term(7, 0)
             quantise_sp(7, slice(2, 4))
             second_product(7, 1)
-            add_second_bias(7, slice(0, 2), nc.vector)
+            bias_k(7, slice(0, 2), nc.vector)
+            bias_v(7, slice(0, 2), nc.gpsimd)
             for n in range(SUB):
-                lift_stats(6, n)
+                lift_v(6, n)
+            finish_v(6)
+            for n in range(SUB):
+                lift_rope(7, n)
             add_time_term(7, 1)
-            add_second_bias(7, slice(2, 4), nc.vector)
-            lift_combine(6)
-            lift_roots_and_store(6)
+            bias_v(7, slice(2, 4), nc.gpsimd)
+            bias_k(7, slice(2, 4), nc.vector)
             for n in range(SUB):
-                lift_stats(7, n)
+                lift_nope(7, n)
+            lift_v(7, 0)
+            lift_v(7, 1)
             lift_combine(7)
-            lift_roots_and_store(7)
+            lift_v(7, 2)
+            finish_k(7)
+            lift_v(7, 3)
+            finish_v(7)

@@ -211,12 +211,11 @@ def tile_lorentzmla_pa_t_kernel(
         def quantise_x(g):
             codes = twice.tile([P, PASSES, GROUP], U32, tag="x_codes", align_bytes=64)
             scales = twice.tile([P, PASSES, GROUP], U8, tag="x_scales", align_bytes=64)
-            for a in range(PASSES):
-                nc.vector.quantize_mx(
-                    out=codes[:, a, :].bitcast(FP8X4),
-                    scales=scales[:, a, :],
-                    in_=x_grouped[g][:, a, :, :, :].rearrange("q n r j -> q (n r j)"),
-                )
+            nc.vector.quantize_mx(
+                out=codes[:].rearrange("q a c -> q (a c)").bitcast(FP8X4),
+                scales=scales[:].rearrange("q a c -> q (a c)"),
+                in_=x_grouped[g][:].rearrange("q a n r j -> q (a n r j)"),
+            )
             x_codes[g] = codes
             x_scales[g] = scales
 
@@ -420,7 +419,7 @@ def tile_lorentzmla_pa_t_kernel(
 
         def time_square(g):
             inv_ms = three.tile([P, SUB], F32, tag="inv_ms")
-            nc.gpsimd.tensor_tensor(out=inv_ms[:], in0=rstd[g][:], in1=rstd[g][:], op=ALU.mult)
+            nc.scalar.activation(out=inv_ms[:], in_=rstd[g][:], func=ACT.Square)
             sp_sq = three.tile([P, SUB], F32, tag="sp_sq")
             nc.gpsimd.tensor_tensor(out=sp_sq[:], in0=kw_sums[g][:], in1=inv_ms[:], op=ALU.mult)
             sp_squares[g] = sp_sq
@@ -531,22 +530,18 @@ def tile_lorentzmla_pa_t_kernel(
         v_sums = {}
         k_sums = {}
 
-        def stats_of(g):
-            if g not in k_stats:
-                stats_new = twice.tile([P, SUB, 2, 2, 3], F32, tag="stats")
+        def lift_k(g, n):
+            if n == 0:
+                stats_new = twice.tile([P, SUB, 4, 3], F32, tag="stats")
                 k_stats[g] = stats_new
-            return k_stats[g]
-
-        def lift_nope(g, n):
-            nc.vector.bn_stats(
-                out=stats_of(g)[:, n, 0, :, :].rearrange("p e s -> p (e s)"),
-                in_=ksl_sb[g][:, n, :, 1 : 1 + NOPE].rearrange("p h c -> p c h"),
-            )
-
-        def lift_rope(g, n):
-            nc.vector.bn_stats(
-                out=stats_of(g)[:, n, 1, :, :].rearrange("p e s -> p (e s)"), in_=ksl_sb[g][:, n, 0, 1 + NOPE : K_ROW]
-            )
+            row = ksl_sb[g][:, n, :, :].rearrange("p h f -> p (h f)")
+            first = row[:, 1 : 1 + 2 * NOPE].rearrange("p (u c) -> p c u", u=2)
+            start = 1 + 2 * NOPE
+            second = row[:, start : start + 2 * (NOPE + 1)].rearrange("p (u c) -> p u c", u=2)[:, :, 0:NOPE]
+            for k, runs in enumerate((first, second.rearrange("p u c -> p c u"))):
+                nc.vector.bn_stats(
+                    out=k_stats[g][:, n, 2 * k : 2 * k + 2, :].rearrange("p u s -> p (u s)"), in_=runs
+                )
 
         def sum_squares(out, in_):
             junk = twice.tile([P, K_ROW], BF16, tag="junk")
@@ -568,15 +563,12 @@ def tile_lorentzmla_pa_t_kernel(
 
         def lift_combine(g):
             stats = k_stats[g]
-            nc.scalar.activation(out=stats[:, :, :, :, 0], in_=stats[:, :, :, :, 1], func=ACT.Square, scale=8.0)
-            nope_sum = twice.tile([P, SUB, HEADS], F32, tag="nope_sum")
-            nc.vector.tensor_reduce(out=nope_sum[:], in_=stats[:, :, 0, :, 0::2], axis=AXIS.X, op=ALU.add)
-            rope_sum = twice.tile([P, SUB], F32, tag="rope_sum")
-            nc.vector.tensor_reduce(out=rope_sum[:], in_=stats[:, :, 1, :, 0::2], axis=AXIS.XY, op=ALU.add)
+            nc.scalar.activation(out=stats[:, :, :, 0], in_=stats[:, :, :, 1], func=ACT.Square, scale=8.0)
             k_sum = twice.tile([P, SUB, HEADS], F32, tag="k_sum")
-            nc.gpsimd.tensor_tensor(
-                out=k_sum[:], in0=nope_sum[:], in1=rope_sum[:].unsqueeze(2).to_broadcast([P, SUB, HEADS]), op=ALU.add
-            )
+            for h in range(HEADS):
+                nc.vector.tensor_reduce(
+                    out=k_sum[:, :, h], in_=stats[:, :, h : h + 3, 0::2], axis=AXIS.XY, op=ALU.add
+                )
             k_sums[g] = k_sum
 
         def finish_k(g):
@@ -598,148 +590,144 @@ def tile_lorentzmla_pa_t_kernel(
             for n in range(SUB):
                 flip_x(0, n, nc.vector.tensor_copy if n % 2 == 1 else nc.scalar.copy)
             flip_wa(0, nc.scalar.copy)
-            flip_wa(1, nc.scalar.copy)
             quantise_x(0)
             feature_constants()
             quantise_wa(0)
-            quantise_wa(1)
-            flip_wa(2, nc.scalar.copy)
-            kv_product(0, 0)
-            flip_wa(3, nc.scalar.copy)
-            align_wkv_b()
-            twin_table(0)
+            flip_wa(1, nc.scalar.copy)
             flip_wa_rope()
-            kv_product(0, 1)
-            sum_constants()
+            kv_product(0, 0)
             kv_square(0, 0)
-            prepare_second_product()
-            quantise_wa(2)
-            flip_x(1, 0)
+            quantise_wa(1)
+            sum_constants()
+            twin_table(0)
+            align_wkv_b()
+            flip_wa(2, nc.scalar.copy)
+            flip_wa(3, nc.scalar.copy)
+            kv_product(0, 1)
             kv_square(0, 1)
+            prepare_second_product()
+            flip_x(1, 0)
             flip_x(1, 1)
+            quantise_wa(2)
             twin_table(1)
-            quantise_wa(3)
             kv_weighted(0, 0, True)
             kv_product(0, 2)
-            kv_weighted(0, 1, True)
             kv_square(0, 2)
-            flip_x(1, 2)
             flip_wkv_b()
-            kv_product(0, 3)
-            kv_square(0, 3)
-            quantise_wa_rope()
+            flip_x(1, 2)
             square_rest(0, 0, nc.gpsimd)
             turn_tables(0, psum_rope, "rope")
-            flip_x(1, 3)
-            rope_product(0)
+            quantise_wa(3)
+            quantise_wa_rope()
+            kv_weighted(0, 1, True)
+            kv_product(0, 3)
+            kv_square(0, 3)
             square_rest(0, 1, nc.vector)
-            pair_constants()
-            kv_weighted(0, 2, True)
             square_rest(0, 2, nc.gpsimd)
+            kv_weighted(0, 2, True)
+            flip_x(1, 3)
             square_rest(0, 3, nc.vector)
-            quantise_wkv_b()
-            quantise_x(1)
-            feature_sums(0, 0)
-            feature_sums(0, 1)
-            copy_second()
-            kv_product(1, 0)
-            feature_sums(0, 2)
-            feature_sums(0, 3)
-            kv_weighted(0, 3, True)
-            kv_product(1, 1)
-            kv_square(1, 0)
-            norm_root(0)
-            kv_weighted(1, 0, False)
-            kv_square(1, 1)
             flip_x(2, 0)
-            square_rest(1, 0, nc.gpsimd)
-            kv_weighted(1, 1, False)
-            spread_rstd(0)
-            rope_multiply(0, 0)
-            square_rest(1, 1, nc.gpsimd)
+            rope_product(0)
+            feature_sums(0, 0)
+            quantise_x(1)
             flip_x(2, 1)
-            kv_product(1, 2)
-            flip_x(2, 2)
-            turn_tables(1, psum_kv2, "kv2")
+            feature_sums(0, 1)
+            pair_constants()
+            kv_product(1, 0)
+            kv_weighted(0, 3, True)
+            copy_second()
+            kv_square(1, 0)
+            rope_multiply(0, 0)
+            feature_sums(0, 2)
+            kv_weighted(1, 0, False)
+            feature_sums(0, 3)
             rope_multiply(0, 1)
-            norm(0, ALL)
-            flip_x(2, 3, nc.vector.tensor_copy)
-            kv_square(1, 2)
+            kv_product(1, 1)
+            norm_root(0)
+            square_rest(1, 0, nc.gpsimd)
             time_square(0)
-            kv_product(1, 3)
+            kv_square(1, 1)
+            flip_x(2, 2)
+            flip_x(2, 3, nc.vector.tensor_copy)
+            spread_rstd(0)
+            quantise_wkv_b()
+            kv_weighted(1, 1, False)
+            kv_product(1, 2)
+            rope_turn(0)
+            kv_square(1, 2)
             flip_x(3, 0)
-            square_rest(1, 2, nc.gpsimd)
             flip_x(3, 1)
             quantise_x(2)
-            rope_product(1)
-            kv_square(1, 3)
-            flip_x(3, 2)
             kv_weighted(1, 2, True)
-            kv_weighted(1, 3, True)
-            rope_turn(0)
-            time_root(0)
-            quantise_sp(0, ALL)
-            flip_x(3, 3)
-            square_rest(1, 3, nc.gpsimd)
+            kv_product(1, 3)
+            rope_product(1)
+            square_rest(1, 1, nc.gpsimd)
+            square_rest(1, 2, nc.gpsimd)
+            norm(0, ALL)
             load_x(4)
+            kv_square(1, 3)
+            time_root(0)
+            flip_x(3, 2)
+            kv_weighted(1, 3, True)
+            flip_x(3, 3)
+            quantise_sp(0, ALL)
+            square_rest(1, 3, nc.gpsimd)
+            turn_tables(1, psum_kv2, "kv2")
             for i in range(2, GROUPS):
                 do(load_x, i + 3)
                 do(kv_product, i, 0)
+                do(lift_k, i - 3, 0)
+                do(rope_multiply, i - 1, 0)
                 do(feature_sums, i - 1, 0)
                 do(feature_sums, i - 1, 1)
-                do(kv_product, i, 1)
-                do(rope_multiply, i - 1, 0)
                 do(kv_square, i, 0)
+                do(rope_multiply, i - 1, 1)
+                do(quantise_x, i + 1)
+                do(kv_product, i, 1)
                 do(kv_weighted, i, 0, False)
                 do(second_product, i - 2, 0)
-                do(rope_multiply, i - 1, 1)
-                do(feature_sums, i - 1, 2)
-                do(feature_sums, i - 1, 3)
                 do(bias_v, i - 3, ALL, nc.gpsimd)
-                do(lift_nope, i - 3, 0)
-                do(lift_rope, i - 3, 0)
-                do(kv_square, i, 1)
-                do(square_rest, i, 0, nc.gpsimd)
-                do(kv_product, i, 2)
-                do(quantise_x, i + 1)
+                do(lift_k, i - 3, 1)
                 do(add_time_term, i - 2, 0)
-                do(second_product, i - 2, 1)
-                do(lift_nope, i - 3, 1)
-                do(lift_rope, i - 3, 1)
+                do(feature_sums, i - 1, 2)
+                do(kv_square, i, 1)
+                do(feature_sums, i - 1, 3)
                 do(kv_weighted, i, 1, True)
+                do(kv_product, i, 2)
                 do(rope_rows, i - 2)
                 do(norm_root, i - 1)
-                do(kv_square, i, 2)
-                do(add_time_term, i - 2, 1)
+                do(square_rest, i, 0, nc.gpsimd)
                 do(lift_v, i - 3, 0)
-                do(lift_nope, i - 3, 2)
-                do(lift_rope, i - 3, 2)
-                do(lift_nope, i - 3, 3)
-                do(lift_rope, i - 3, 3)
-                do(flip_x, i + 2, 0)
+                do(lift_k, i - 3, 2)
+                do(second_product, i - 2, 1)
                 do(square_rest, i, 1, nc.gpsimd)
-                do(flip_x, i + 2, 1)
-                do(lift_v, i - 3, 1)
+                do(kv_square, i, 2)
+                do(flip_x, i + 2, 0)
                 do(spread_rstd, i - 1)
-                do(kv_product, i, 3)
-                do(kv_square, i, 3)
+                do(lift_v, i - 3, 1)
+                do(add_time_term, i - 2, 1)
                 do(square_rest, i, 2, nc.gpsimd)
-                do(bias_k, i - 2, ALL, nc.gpsimd)
+                do(kv_product, i, 3)
+                do(lift_k, i - 3, 3)
                 do(norm, i - 1, ALL)
+                do(flip_x, i + 2, 1)
+                do(kv_square, i, 3)
                 do(kv_weighted, i, 2, False)
-                do(square_rest, i, 3, nc.gpsimd)
-                do(lift_combine, i - 3)
-                do(lift_v, i - 3, 2)
-                do(kv_weighted, i, 3, False)
-                do(quantise_sp, i - 1, ALL)
-                do(lift_v, i - 3, 3)
                 do(rope_turn, i - 1)
-                do(flip_x, i + 2, 2)
+                do(bias_k, i - 2, ALL, nc.gpsimd)
+                do(lift_v, i - 3, 2)
+                do(square_rest, i, 3, nc.vector)
+                do(kv_weighted, i, 3, False)
                 do(rope_product, i)
-                do(finish_k, i - 3)
-                do(flip_x, i + 2, 3)
-                do(finish_v, i - 3)
+                do(quantise_sp, i - 1, ALL)
+                do(lift_combine, i - 3)
                 do(time_square, i - 1)
+                do(flip_x, i + 2, 2)
+                do(lift_v, i - 3, 3)
+                do(finish_v, i - 3)
+                do(flip_x, i + 2, 3)
+                do(finish_k, i - 3)
                 do(time_root, i - 1)
             feature_sums(7, 0)
             feature_sums(7, 1)
@@ -786,13 +774,11 @@ def tile_lorentzmla_pa_t_kernel(
             for n in range(SUB):
                 lift_v(6, n)
             finish_v(6)
-            for n in range(SUB):
-                lift_rope(7, n)
             add_time_term(7, 1)
             bias_v(7, slice(2, 4), nc.gpsimd)
             bias_k(7, slice(2, 4), nc.vector)
             for n in range(SUB):
-                lift_nope(7, n)
+                lift_k(7, n)
             lift_v(7, 0)
             lift_v(7, 1)
             lift_combine(7)

@@ -55,8 +55,8 @@ def tile_lorentzmla_pa_t_kernel(
 
         one = once.tile([P, 1], F32)
         nc.vector.memset(one[:], 1.0)
-        root = once.tile([P, 1], F32)
-        nc.scalar.activation(out=root[:], in_=one[:], func=ACT.Sqrt)
+        root_of_one = once.tile([P, 1], F32)
+        nc.scalar.activation(out=root_of_one[:], in_=one[:], func=ACT.Sqrt)
 
         x_sb = {}
 
@@ -103,13 +103,13 @@ def tile_lorentzmla_pa_t_kernel(
         ones_bf = once.tile([P, P], BF16)
         nc.vector.memset(ones_bf[:], 1.0)
 
+        warm_rows = once.tile([P, 512], BF16)
+        nc.vector.memset(warm_rows[:], 0.0)
+
         def keep_warm(count, pool, tag):
             bank = pool.tile([P, 512], F32, tag=tag)
             for k in range(count):
                 nc.tensor.matmul(out=bank[:], lhsT=ones_bf[:], rhs=warm_rows[:], start=True, stop=True)
-
-        warm_rows = once.tile([P, 512], BF16)
-        nc.vector.memset(warm_rows[:], 0.0)
 
         b32 = once.tile([P, SUB], F32)
         w32 = once.tile([P, SUB], F32)
@@ -148,8 +148,8 @@ def tile_lorentzmla_pa_t_kernel(
             rows = (cos_t, sin_t)[k]
             for e in range(2):
                 sign = -1.0 if k == 1 and e == 1 else 1.0
-                nc.gpsimd.tensor_scalar(
-                    out=twins[:, k, :, :, e, :], in0=rows[:], scalar1=sign, scalar2=0.0, op0=ALU.mult, op1=ALU.add
+                nc.vector.tensor_scalar(
+                    out=twins[:, k, :, :, e, :], in0=rows[:], scalar1=sign, scalar2=None, op0=ALU.mult
                 )
 
         def turn_tables(half, pool, tag):
@@ -161,9 +161,9 @@ def tile_lorentzmla_pa_t_kernel(
                     )
             nc.scalar.copy(out=rope_tables[:, half, :, :, :], in_=turned[:])
 
-        def flip_place(rows_sb, grouped, n, copy):
+        def flip_place(rows_sb, grouped, n, copy, pool=psum_flip, tag="flip"):
             rows_words = rows_sb[:].bitcast(F32)[:, n, :]
-            flipped = psum_flip.tile([P, 4, P], F32, tag="flip")
+            flipped = pool.tile([P, 4, P], F32, tag=tag)
             for c in range(4):
                 nc.tensor.transpose(flipped[:, c, :], rows_words[:, c * P : (c + 1) * P], ident[:])
             copy(out=grouped[:].bitcast(F32)[:, :, n, :, :], in_=flipped[:].rearrange("q (a u) r -> q a r u", u=2))
@@ -172,8 +172,8 @@ def tile_lorentzmla_pa_t_kernel(
         wa_kv_scales = once.tile([P, PASSES, KV_RANK], U8, align_bytes=64)
         wa_grouped = once.tile([P, PASSES, SUB, P, 4], BF16, align_bytes=64)
 
-        def flip_wa(t, copy):
-            flip_place(wa_kv_sb, wa_grouped, t, copy)
+        def flip_wa(t, copy, pool=psum_flip, tag="flip"):
+            flip_place(wa_kv_sb, wa_grouped, t, copy, pool, tag)
 
         def quantise_wa(t):
             for a in range(PASSES):
@@ -202,22 +202,35 @@ def tile_lorentzmla_pa_t_kernel(
         x_codes = {}
         x_scales = {}
 
-        def flip_x(g, n, copy=nc.scalar.copy):
+        def flip_x(g, n, copy=nc.scalar.copy, pool=psum_flip, tag="flip"):
             if n == 0:
                 grouped = twice.tile([P, PASSES, SUB, P, 4], BF16, tag="grouped", align_bytes=64)
                 x_grouped[g] = grouped
-            flip_place(x_sb[g], x_grouped[g], n, copy)
+            flip_place(x_sb[g], x_grouped[g], n, copy, pool, tag)
 
-        def quantise_x(g):
+        def new_codes(g):
             codes = twice.tile([P, PASSES, GROUP], U32, tag="x_codes", align_bytes=64)
             scales = twice.tile([P, PASSES, GROUP], U8, tag="x_scales", align_bytes=64)
-            nc.vector.quantize_mx(
-                out=codes[:].rearrange("q a c -> q (a c)").bitcast(FP8X4),
-                scales=scales[:].rearrange("q a c -> q (a c)"),
-                in_=x_grouped[g][:].rearrange("q a n r j -> q (a n r j)"),
-            )
             x_codes[g] = codes
             x_scales[g] = scales
+
+        def quantise_x(g):
+            new_codes(g)
+            nc.vector.quantize_mx(
+                out=x_codes[g][:].rearrange("q a c -> q (a c)").bitcast(FP8X4),
+                scales=x_scales[g][:].rearrange("q a c -> q (a c)"),
+                in_=x_grouped[g][:].rearrange("q a n r j -> q (a n r j)"),
+            )
+
+        def quantise_place(g, n):
+            if n == 0:
+                new_codes(g)
+            for a in range(PASSES):
+                nc.vector.quantize_mx(
+                    out=x_codes[g][:, a, n * P : (n + 1) * P].bitcast(FP8X4),
+                    scales=x_scales[g][:, a, n * P : (n + 1) * P],
+                    in_=x_grouped[g][:, a, n, :, :].rearrange("q r j -> q (r j)"),
+                )
 
         second_vectors = once.tile([P, 2, KV2], F32)
         bb_all = second_vectors[:, 0, :]
@@ -249,19 +262,19 @@ def tile_lorentzmla_pa_t_kernel(
                 out=wb_codes[:].bitcast(FP8X4), scales=wb_scales[:], in_=wb_grouped[:].rearrange("q c j -> q (c j)")
             )
 
-        second_bank = []
+        second_banks = []
 
-        def prepare_second_product():
+        def second_vector_products():
             bank = psum_kv2.tile([P, 2, KV2], F32, tag="kv2")
             nc.tensor.matmul(out=bank[:, 0, :], lhsT=ones_bf[:], rhs=vec_rows[:], start=True, stop=True)
             for o in range(2):
                 nc.tensor.transpose(
                     bank[:, 1, o * P : (o + 1) * P], wb0_col[:, o : o + 1].to_broadcast([P, P]), ident[:]
                 )
-            second_bank.append(bank)
+            second_banks.append(bank)
 
-        def copy_second():
-            nc.vector.tensor_copy(out=second_vectors[:], in_=second_bank[0][:])
+        def second_vector_copies():
+            nc.vector.tensor_copy(out=second_vectors[:], in_=second_banks[0][:])
 
         squares = {}
         squares_rest = {}
@@ -451,7 +464,10 @@ def tile_lorentzmla_pa_t_kernel(
             nc.vector.tensor_tensor(
                 out=sp_rows[g][:, cols, :].rearrange("p (c i) t -> p c t i", i=4),
                 in0=kv_w[g][:, :, cols].rearrange("p t (c i) -> p c t i", i=4),
-                in1=spread_of[g][:, cols].rearrange("p (c i) -> p c i", i=4).unsqueeze(2).to_broadcast([P, quads, SUB, 4]),
+                in1=spread_of[g][:, cols]
+                .rearrange("p (c i) -> p c i", i=4)
+                .unsqueeze(2)
+                .to_broadcast([P, quads, SUB, 4]),
                 op=ALU.mult,
             )
 
@@ -587,29 +603,35 @@ def tile_lorentzmla_pa_t_kernel(
 
         with tc.manual_schedule():
             keep_warm(3, psum_kv2, "kv2")
-            for n in range(SUB):
-                flip_x(0, n, nc.vector.tensor_copy if n % 2 == 1 else nc.scalar.copy)
-            flip_wa(0, nc.scalar.copy)
-            quantise_x(0)
-            feature_constants()
+            flip_x(0, 0)
+            flip_x(0, 1, nc.vector.tensor_copy)
+            quantise_place(0, 0)
+            flip_x(0, 2, nc.scalar.copy, psum_rope, "rope")
+            flip_x(0, 3, nc.vector.tensor_copy, psum_rope, "rope")
+            keep_warm(1, psum_kv2, "kv2")
+            flip_wa(0, nc.scalar.copy, psum_y, "y")
+            quantise_place(0, 1)
+            quantise_place(0, 2)
+            quantise_place(0, 3)
             quantise_wa(0)
+            feature_constants()
             flip_wa(1, nc.scalar.copy)
             flip_wa_rope()
             kv_product(0, 0)
             kv_square(0, 0)
             quantise_wa(1)
             sum_constants()
-            twin_table(0)
             align_wkv_b()
+            twin_table(0)
+            twin_table(1)
             flip_wa(2, nc.scalar.copy)
             flip_wa(3, nc.scalar.copy)
             kv_product(0, 1)
             kv_square(0, 1)
-            prepare_second_product()
+            second_vector_products()
             flip_x(1, 0)
             flip_x(1, 1)
             quantise_wa(2)
-            twin_table(1)
             kv_weighted(0, 0, True)
             kv_product(0, 2)
             kv_square(0, 2)
@@ -636,7 +658,7 @@ def tile_lorentzmla_pa_t_kernel(
             pair_constants()
             kv_product(1, 0)
             kv_weighted(0, 3, True)
-            copy_second()
+            second_vector_copies()
             kv_square(1, 0)
             rope_multiply(0, 0)
             feature_sums(0, 2)
@@ -676,113 +698,114 @@ def tile_lorentzmla_pa_t_kernel(
             turn_tables(1, psum_kv2, "kv2")
             for i in range(2, GROUPS):
                 do(load_x, i + 3)
-                do(kv_product, i, 0)
-                do(lift_k, i - 3, 0)
                 do(rope_multiply, i - 1, 0)
+                do(kv_product, i, 0)
+                do(bias_v, i - 3, ALL, nc.gpsimd)
+                do(rope_rows, i - 2)
+                do(lift_k, i - 3, 0)
+                do(lift_k, i - 3, 1)
                 do(feature_sums, i - 1, 0)
                 do(feature_sums, i - 1, 1)
-                do(kv_square, i, 0)
-                do(rope_multiply, i - 1, 1)
-                do(quantise_x, i + 1)
+                do(lift_k, i - 3, 2)
                 do(kv_product, i, 1)
+                do(kv_square, i, 0)
                 do(kv_weighted, i, 0, False)
                 do(second_product, i - 2, 0)
-                do(bias_v, i - 3, ALL, nc.gpsimd)
-                do(lift_k, i - 3, 1)
-                do(add_time_term, i - 2, 0)
+                do(quantise_x, i + 1)
                 do(feature_sums, i - 1, 2)
-                do(kv_square, i, 1)
-                do(feature_sums, i - 1, 3)
-                do(kv_weighted, i, 1, True)
-                do(kv_product, i, 2)
-                do(rope_rows, i - 2)
-                do(norm_root, i - 1)
-                do(square_rest, i, 0, nc.gpsimd)
-                do(lift_v, i - 3, 0)
-                do(lift_k, i - 3, 2)
-                do(second_product, i - 2, 1)
-                do(square_rest, i, 1, nc.gpsimd)
-                do(kv_square, i, 2)
-                do(flip_x, i + 2, 0)
-                do(spread_rstd, i - 1)
-                do(lift_v, i - 3, 1)
-                do(add_time_term, i - 2, 1)
-                do(square_rest, i, 2, nc.gpsimd)
-                do(kv_product, i, 3)
                 do(lift_k, i - 3, 3)
-                do(norm, i - 1, ALL)
-                do(flip_x, i + 2, 1)
-                do(kv_square, i, 3)
-                do(kv_weighted, i, 2, False)
-                do(rope_turn, i - 1)
-                do(bias_k, i - 2, ALL, nc.gpsimd)
-                do(lift_v, i - 3, 2)
-                do(square_rest, i, 3, nc.vector)
-                do(kv_weighted, i, 3, False)
-                do(rope_product, i)
-                do(quantise_sp, i - 1, ALL)
+                do(add_time_term, i - 2, 0)
+                do(rope_multiply, i - 1, 1)
                 do(lift_combine, i - 3)
-                do(time_square, i - 1)
-                do(flip_x, i + 2, 2)
-                do(lift_v, i - 3, 3)
-                do(finish_v, i - 3)
-                do(flip_x, i + 2, 3)
+                do(kv_square, i, 1)
+                do(square_rest, i, 0, nc.gpsimd)
+                do(feature_sums, i - 1, 3)
+                do(norm_root, i - 1)
+                do(kv_weighted, i, 1, True)
+                do(lift_v, i - 3, 0)
+                do(square_rest, i, 1, nc.gpsimd)
+                do(kv_product, i, 2)
+                do(kv_square, i, 2)
+                do(second_product, i - 2, 1)
+                do(lift_v, i - 3, 1)
                 do(finish_k, i - 3)
+                do(square_rest, i, 2, nc.gpsimd)
+                do(flip_x, i + 2, 0)
+                do(lift_v, i - 3, 2)
+                do(spread_rstd, i - 1)
+                do(kv_product, i, 3)
+                do(kv_square, i, 3)
+                do(lift_v, i - 3, 3)
+                do(add_time_term, i - 2, 1)
+                do(bias_k, i - 2, ALL, nc.gpsimd)
+                do(flip_x, i + 2, 1)
+                do(kv_weighted, i, 2, False)
+                do(norm, i - 1, ALL)
+                do(kv_weighted, i, 3, False)
+                do(time_square, i - 1)
+                do(rope_turn, i - 1)
+                do(flip_x, i + 2, 2)
+                do(square_rest, i, 3, nc.vector)
+                do(quantise_sp, i - 1, ALL)
+                do(rope_product, i)
+                do(flip_x, i + 2, 3)
+                do(finish_v, i - 3)
                 do(time_root, i - 1)
-            feature_sums(7, 0)
-            feature_sums(7, 1)
-            second_product(6, 0)
-            feature_sums(7, 2)
-            feature_sums(7, 3)
-            rope_multiply(7, 0)
-            bias_v(5, ALL, nc.gpsimd)
-            rope_rows(6)
-            add_time_term(6, 0)
-            second_product(6, 1)
-            rope_multiply(7, 1)
+            last = GROUPS - 1
+            feature_sums(last, 0)
+            feature_sums(last, 1)
+            second_product(last - 1, 0)
+            feature_sums(last, 2)
+            feature_sums(last, 3)
+            rope_multiply(last, 0)
+            bias_v(last - 2, ALL, nc.gpsimd)
+            rope_rows(last - 1)
+            add_time_term(last - 1, 0)
+            second_product(last - 1, 1)
+            rope_multiply(last, 1)
             for n in range(3):
-                lift_rows(5, n)
-            norm_root(7)
-            add_time_term(6, 1)
-            time_square(7)
-            bias_k(6, ALL, nc.gpsimd)
-            bias_v(6, ALL, nc.gpsimd)
-            spread_rstd(7)
-            rope_turn(7)
-            lift_rows(5, 3)
-            finish_k(5)
-            time_root(7)
+                lift_rows(last - 2, n)
+            norm_root(last)
+            add_time_term(last - 1, 1)
+            time_square(last)
+            bias_k(last - 1, ALL, nc.gpsimd)
+            bias_v(last - 1, ALL, nc.gpsimd)
+            spread_rstd(last)
+            rope_turn(last)
+            lift_rows(last - 2, 3)
+            finish_k(last - 2)
+            time_root(last)
             for n in range(SUB):
-                lift_v(5, n)
-            finish_v(5)
-            lift_rows(6, 0)
-            rope_rows(7)
-            norm(7, slice(0, 2))
-            quantise_sp(7, slice(0, 2))
+                lift_v(last - 2, n)
+            finish_v(last - 2)
+            lift_rows(last - 1, 0)
+            rope_rows(last)
+            norm(last, slice(0, 2))
+            quantise_sp(last, slice(0, 2))
             keep_warm(1, psum_y, "y")
-            second_product(7, 0)
-            norm(7, slice(2, 4))
-            lift_rows(6, 1)
-            lift_rows(6, 2)
-            lift_rows(6, 3)
-            finish_k(6)
-            add_time_term(7, 0)
-            quantise_sp(7, slice(2, 4))
-            second_product(7, 1)
-            bias_k(7, slice(0, 2), nc.vector)
-            bias_v(7, slice(0, 2), nc.gpsimd)
+            second_product(last, 0)
+            norm(last, slice(2, 4))
+            lift_rows(last - 1, 1)
+            lift_rows(last - 1, 2)
+            lift_rows(last - 1, 3)
+            finish_k(last - 1)
+            add_time_term(last, 0)
+            quantise_sp(last, slice(2, 4))
+            second_product(last, 1)
+            bias_k(last, slice(0, 2), nc.vector)
+            bias_v(last, slice(0, 2), nc.gpsimd)
             for n in range(SUB):
-                lift_v(6, n)
-            finish_v(6)
-            add_time_term(7, 1)
-            bias_v(7, slice(2, 4), nc.gpsimd)
-            bias_k(7, slice(2, 4), nc.vector)
+                lift_v(last - 1, n)
+            finish_v(last - 1)
+            add_time_term(last, 1)
+            bias_v(last, slice(2, 4), nc.gpsimd)
+            bias_k(last, slice(2, 4), nc.vector)
             for n in range(SUB):
-                lift_k(7, n)
-            lift_v(7, 0)
-            lift_v(7, 1)
-            lift_combine(7)
-            lift_v(7, 2)
-            finish_k(7)
-            lift_v(7, 3)
-            finish_v(7)
+                lift_k(last, n)
+            lift_v(last, 0)
+            lift_v(last, 1)
+            lift_combine(last)
+            lift_v(last, 2)
+            finish_k(last)
+            lift_v(last, 3)
+            finish_v(last)

@@ -621,6 +621,7 @@ def tile_lorentzmla_pa_t_kernel(
             kv_square(0, 0)
             quantise_wa(1)
             sum_constants()
+            load_x(4)
             align_wkv_b()
             twin_table(0)
             twin_table(1)
@@ -687,7 +688,6 @@ def tile_lorentzmla_pa_t_kernel(
             square_rest(1, 1, nc.gpsimd)
             square_rest(1, 2, nc.gpsimd)
             norm(0, ALL)
-            load_x(4)
             kv_square(1, 3)
             time_root(0)
             flip_x(3, 2)
@@ -752,60 +752,67 @@ def tile_lorentzmla_pa_t_kernel(
                 do(finish_v, i - 3)
                 do(time_root, i - 1)
             last = GROUPS - 1
-            feature_sums(last, 0)
-            feature_sums(last, 1)
-            second_product(last - 1, 0)
-            feature_sums(last, 2)
-            feature_sums(last, 3)
             rope_multiply(last, 0)
             bias_v(last - 2, ALL, nc.gpsimd)
-            rope_rows(last - 1)
+            feature_sums(last, 0)
+            lift_rows(last - 2, 0)
+            feature_sums(last, 1)
+            lift_rows(last - 2, 1)
+            keep_warm(1, psum_y, "y")
+            lift_v(last - 2, 0)
+            second_product(last - 1, 0)
+            lift_v(last - 2, 1)
+            feature_sums(last, 2)
             add_time_term(last - 1, 0)
-            second_product(last - 1, 1)
             rope_multiply(last, 1)
-            for n in range(3):
-                lift_rows(last - 2, n)
+            feature_sums(last, 3)
             norm_root(last)
+            second_product(last - 1, 1)
             add_time_term(last - 1, 1)
-            time_square(last)
-            bias_k(last - 1, ALL, nc.gpsimd)
-            bias_v(last - 1, ALL, nc.gpsimd)
+            lift_rows(last - 2, 2)
+            rope_rows(last - 1)
             spread_rstd(last)
-            rope_turn(last)
             lift_rows(last - 2, 3)
             finish_k(last - 2)
-            time_root(last)
-            for n in range(SUB):
-                lift_v(last - 2, n)
-            finish_v(last - 2)
-            lift_rows(last - 1, 0)
-            rope_rows(last)
             norm(last, slice(0, 2))
+            rope_turn(last)
+            bias_k(last - 1, ALL, nc.gpsimd)
             quantise_sp(last, slice(0, 2))
-            keep_warm(1, psum_y, "y")
-            second_product(last, 0)
-            norm(last, slice(2, 4))
+            lift_rows(last - 1, 0)
             lift_rows(last - 1, 1)
             lift_rows(last - 1, 2)
+            time_square(last)
+            time_root(last)
+            second_product(last, 0)
+            norm(last, slice(2, 4))
             lift_rows(last - 1, 3)
             finish_k(last - 1)
+            lift_v(last - 2, 2)
+            lift_v(last - 2, 3)
+            finish_v(last - 2)
             add_time_term(last, 0)
+            bias_v(last - 1, ALL, nc.gpsimd)
+            rope_rows(last)
+            lift_v(last - 1, 0)
+            lift_v(last - 1, 1)
+            lift_v(last - 1, 2)
             quantise_sp(last, slice(2, 4))
             second_product(last, 1)
             bias_k(last, slice(0, 2), nc.vector)
-            bias_v(last, slice(0, 2), nc.gpsimd)
-            for n in range(SUB):
-                lift_v(last - 1, n)
-            finish_v(last - 1)
             add_time_term(last, 1)
-            bias_v(last, slice(2, 4), nc.gpsimd)
             bias_k(last, slice(2, 4), nc.vector)
-            for n in range(SUB):
-                lift_k(last, n)
+            lift_k(last, 0)
+            lift_k(last, 1)
+            bias_v(last, slice(0, 2), nc.gpsimd)
+            lift_v(last - 1, 3)
+            finish_v(last - 1)
             lift_v(last, 0)
             lift_v(last, 1)
-            lift_combine(last)
+            bias_v(last, slice(2, 4), nc.gpsimd)
             lift_v(last, 2)
-            finish_k(last)
             lift_v(last, 3)
             finish_v(last)
+            lift_k(last, 2)
+            lift_k(last, 3)
+            lift_combine(last)
+            finish_k(last)

from contextlib import ExitStack

import concourse.mybir as mybir
from concourse.masks import make_identity

F32 = mybir.dt.float32
BF16 = mybir.dt.bfloat16
U32 = mybir.dt.uint32
U8 = mybir.dt.uint8
FP8X4 = mybir.dt.float8_e4m3fn_x4
ALU = mybir.AluOpType
ACT = mybir.ActivationFunctionType
AXIS = mybir.AxisListType

P = 128
TOKENS = 4 * 1024
DIM = 1024
PASSES = DIM // (4 * P)
KV_RANK = 512
ROPE = 128
HALF = ROPE // 2
HEADS = 2
NOPE = 64
V_DIM = 64
KV2 = HEADS * (NOPE + V_DIM)
K_ROW = 1 + NOPE + ROPE
V_ROW = 1 + V_DIM
SUB = 4
GROUP = P * SUB
GROUPS = TOKENS // GROUP
TABLE_HALVES = 1024 // GROUP
EPS = 1e-6

FLOPS = 2 * TOKENS * DIM * (KV_RANK + ROPE) + 2 * TOKENS * KV_RANK * KV2


def tile_lorentzmla_pa_t_kernel(
    tc, x, freqs_cos, freqs_sin, wkv_a_w, wkv_a_b, kv_norm_w, wkv_b_w, wkv_b_b, out_0, out_1
):
    nc = tc.nc
    x_groups = x.flatten_outer_dims().rearrange("(g p n) k -> g p n k", p=P, n=SUB)
    ksl_groups = out_0.rearrange("b s h f -> (b s) (h f)").rearrange("(g p n) f -> g p (n f)", p=P, n=SUB)
    vs_groups = out_1.rearrange("b s h f -> (b s) (h f)").rearrange("(g p n) f -> g p (n f)", p=P, n=SUB)

    with ExitStack() as ctx:
        once = ctx.enter_context(tc.tile_pool(name="once", bufs=1))
        twice = ctx.enter_context(tc.tile_pool(name="twice", bufs=2))
        three = ctx.enter_context(tc.tile_pool(name="three", bufs=3))
        five = ctx.enter_context(tc.tile_pool(name="five", bufs=5))
        psum_flip = ctx.enter_context(tc.psum_pool(name="psum_flip", bufs=2))
        psum_y = ctx.enter_context(tc.psum_pool(name="psum_y", bufs=2))
        psum_rope = ctx.enter_context(tc.psum_pool(name="psum_rope", bufs=2))
        psum_kv2 = ctx.enter_context(tc.psum_pool(name="psum_kv2", bufs=1))
        psum_norm = ctx.enter_context(tc.psum_pool(name="psum_norm", bufs=1))

        one = once.tile([P, 1], F32)
        nc.vector.memset(one[:], 1.0)
        root_of_one = once.tile([P, 1], F32)
        nc.scalar.activation(out=root_of_one[:], in_=one[:], func=ACT.Sqrt)

        x_sb = {}

        def load_x(g):
            x_tile = five.tile([P, SUB, DIM], BF16, tag="rows")
            nc.sync.dma_start(out=x_tile[:], in_=x_groups[g])
            x_sb[g] = x_tile

        x_first = five.tile([P, SUB, DIM], BF16, tag="rows")
        for n in range(SUB):
            nc.sync.dma_start(out=x_first[:, n, :], in_=x_groups[0][:, n, :])
        x_sb[0] = x_first
        b_bf = once.tile([P, SUB], BF16)
        nc.sync.dma_start(out=b_bf[:], in_=wkv_a_b[0:KV_RANK].rearrange("(p t) -> p t", t=SUB))
        w_bf = once.tile([P, SUB], BF16)
        nc.sync.dma_start(out=w_bf[:], in_=kv_norm_w.rearrange("(p t) -> p t", t=SUB))
        bpe_bf = once.tile([P, 2], BF16)
        bpe_rows = wkv_a_b[KV_RANK : KV_RANK + ROPE].rearrange("(j e) -> e j", e=2)
        for e in range(2):
            nc.sync.dma_start(out=bpe_bf[e * HALF : (e + 1) * HALF, 0:1], in_=bpe_rows[e].unsqueeze(1))
        wa_kv_sb = five.tile([P, SUB, DIM], BF16, tag="rows")
        wa_kv_rows = wkv_a_w[0:KV_RANK, :].rearrange("(p t) k -> p t k", t=SUB)
        for t in range(SUB):
            nc.sync.dma_start(out=wa_kv_sb[:, t, :], in_=wa_kv_rows[:, t, :])
        wa_pe_sb = once.tile([P, 1, DIM], BF16)
        wa_pe_rows = wkv_a_w[KV_RANK : KV_RANK + ROPE, :].rearrange("(j e) k -> e j k", e=2)
        for e in range(2):
            nc.sync.dma_start(out=wa_pe_sb[e * HALF : (e + 1) * HALF, 0, :], in_=wa_pe_rows[e])

        wb_full = once.tile([P, 2, KV_RANK + 1], BF16)
        nc.sync.dma_start(out=wb_full[:], in_=wkv_b_w.rearrange("(o p) k -> p o k", p=P))
        vec_rows = once.tile([P, KV2], BF16)
        nc.vector.memset(vec_rows[:], 0.0)
        nc.sync.dma_start(out=vec_rows[0:1, 0:KV2], in_=wkv_b_b.unsqueeze(0))
        cos_t = once.tile([P, TABLE_HALVES, SUB, HALF], BF16)
        nc.sync.dma_start(out=cos_t[:], in_=freqs_cos.rearrange("(a p n) j -> p a n j", p=P, n=SUB))
        sin_t = once.tile([P, TABLE_HALVES, SUB, HALF], BF16)
        nc.sync.dma_start(out=sin_t[:], in_=freqs_sin.rearrange("(a p n) j -> p a n j", p=P, n=SUB))
        for g in range(1, 4):
            load_x(g)

        ident = once.tile([P, P], F32)
        make_identity(nc, ident[:])
        ones_bf = once.tile([P, P], BF16)
        nc.vector.memset(ones_bf[:], 1.0)

        warm_rows = once.tile([P, 512], BF16)
        nc.vector.memset(warm_rows[:], 0.0)

        def keep_warm(count, pool, tag):
            bank = pool.tile([P, 512], F32, tag=tag)
            for k in range(count):
                nc.tensor.matmul(out=bank[:], lhsT=ones_bf[:], rhs=warm_rows[:], start=True, stop=True)

        b32 = once.tile([P, SUB], F32)
        w32 = once.tile([P, SUB], F32)
        bw32 = once.tile([P, SUB], F32)
        w_sq = once.tile([P, SUB], F32)
        sum_cols = once.tile([P, SUB, 4], BF16)
        bpe32 = once.tile([P, 1], F32)
        pair_own = once.tile([P, P], F32)
        pair_swap = once.tile([P, P], F32)

        def feature_constants():
            nc.vector.tensor_copy(out=b32[:], in_=b_bf[:])
            nc.vector.tensor_copy(out=w32[:], in_=w_bf[:])
            nc.vector.tensor_tensor(out=bw32[:], in0=b32[:], in1=w32[:], op=ALU.mult)

        def sum_constants():
            nc.vector.tensor_tensor(out=w_sq[:], in0=w32[:], in1=w32[:], op=ALU.mult)
            nc.vector.memset(sum_cols[:], 0.0)
            nc.vector.memset(sum_cols[:, :, 0], 1.0)
            nc.vector.tensor_copy(out=sum_cols[:, :, 1], in_=w_sq[:])
            nc.vector.tensor_tensor(out=sum_cols[:, :, 2], in0=w_sq[:], in1=sum_cols[:, :, 1], op=ALU.subtract)

        def pair_constants():
            nc.vector.tensor_copy(out=bpe32[:], in_=bpe_bf[:, 0:1])
            for e in range(2):
                source = ident[:, e * HALF : (e + 1) * HALF]
                nc.vector.tensor_copy(out=pair_own[:].rearrange("p (j e) -> p e j", e=2)[:, e, :], in_=source)
                nc.vector.tensor_copy(out=pair_swap[:].rearrange("p (j e) -> p e j", e=2)[:, 1 - e, :], in_=source)

        ident_bf = once.tile([P, P], BF16)
        make_identity(nc, ident_bf[:])
        rope_tables = once.tile([P, TABLE_HALVES, 2, SUB, P], BF16)
        twins = once.tile([P, 2, TABLE_HALVES, SUB, 2, HALF], BF16)

        def twin_table(k):
            rows = (cos_t, sin_t)[k]
            for e in range(2):
                sign = -1.0 if k == 1 and e == 1 else 1.0
                nc.vector.tensor_scalar(
                    out=twins[:, k, :, :, e, :], in0=rows[:], scalar1=sign, scalar2=None, op0=ALU.mult
                )

        def turn_tables(half, pool, tag):
            turned = pool.tile([P, 2, SUB, P], BF16, tag=tag)
            for k in range(2):
                for n in range(SUB):
                    nc.tensor.transpose(
                        turned[:, k, n, :], twins[:, k, half, n, :, :].rearrange("p e j -> p (e j)"), ident_bf[:]
                    )
            nc.scalar.copy(out=rope_tables[:, half, :, :, :], in_=turned[:])

        def flip_place(rows_sb, grouped, n, copy, pool=psum_flip, tag="flip"):
            rows_words = rows_sb[:].bitcast(F32)[:, n, :]
            flipped = pool.tile([P, 4, P], F32, tag=tag)
            for c in range(4):
                nc.tensor.transpose(flipped[:, c, :], rows_words[:, c * P : (c + 1) * P], ident[:])
            copy(out=grouped[:].bitcast(F32)[:, :, n, :, :], in_=flipped[:].rearrange("q (a u) r -> q a r u", u=2))

        wa_kv_codes = once.tile([P, PASSES, KV_RANK], U32, align_bytes=64)
        wa_kv_scales = once.tile([P, PASSES, KV_RANK], U8, align_bytes=64)
        wa_grouped = once.tile([P, PASSES, SUB, P, 4], BF16, align_bytes=64)

        def flip_wa(t, copy, pool=psum_flip, tag="flip"):
            flip_place(wa_kv_sb, wa_grouped, t, copy, pool, tag)

        def quantise_wa(t):
            for a in range(PASSES):
                nc.vector.quantize_mx(
                    out=wa_kv_codes[:, a, t * P : (t + 1) * P].bitcast(FP8X4),
                    scales=wa_kv_scales[:, a, t * P : (t + 1) * P],
                    in_=wa_grouped[:, a, t, :, :].rearrange("q r j -> q (r j)"),
                )

        wa_pe_codes = once.tile([P, PASSES, ROPE], U32, align_bytes=64)
        wa_pe_scales = once.tile([P, PASSES, ROPE], U8, align_bytes=64)
        pe_grouped = once.tile([P, PASSES, 1, P, 4], BF16, align_bytes=64)

        def flip_wa_rope():
            flip_place(wa_pe_sb, pe_grouped, 0, nc.scalar.copy)

        def quantise_wa_rope():
            for a in range(PASSES):
                nc.vector.quantize_mx(
                    out=wa_pe_codes[:, a, :].bitcast(FP8X4),
                    scales=wa_pe_scales[:, a, :],
                    in_=pe_grouped[:, a, 0, :, :].rearrange("q r j -> q (r j)"),
                )

        x_grouped = {}
        x_codes = {}
        x_scales = {}

        def flip_x(g, n, copy=nc.scalar.copy, pool=psum_flip, tag="flip"):
            if n == 0:
                grouped = twice.tile([P, PASSES, SUB, P, 4], BF16, tag="grouped", align_bytes=64)
                x_grouped[g] = grouped
            flip_place(x_sb[g], x_grouped[g], n, copy, pool, tag)

        def new_codes(g):
            codes = twice.tile([P, PASSES, GROUP], U32, tag="x_codes", align_bytes=64)
            scales = twice.tile([P, PASSES, GROUP], U8, tag="x_scales", align_bytes=64)
            x_codes[g] = codes
            x_scales[g] = scales

        def quantise_x(g):
            new_codes(g)
            nc.vector.quantize_mx(
                out=x_codes[g][:].rearrange("q a c -> q (a c)").bitcast(FP8X4),
                scales=x_scales[g][:].rearrange("q a c -> q (a c)"),
                in_=x_grouped[g][:].rearrange("q a n r j -> q (a n r j)"),
            )

        def quantise_place(g, n):
            if n == 0:
                new_codes(g)
            for a in range(PASSES):
                nc.vector.quantize_mx(
                    out=x_codes[g][:, a, n * P : (n + 1) * P].bitcast(FP8X4),
                    scales=x_scales[g][:, a, n * P : (n + 1) * P],
                    in_=x_grouped[g][:, a, n, :, :].rearrange("q r j -> q (r j)"),
                )

        second_vectors = once.tile([P, 2, KV2], F32)
        bb_all = second_vectors[:, 0, :]
        wb0_all = second_vectors[:, 1, :]
        wb_codes = once.tile([P, KV2], U32, align_bytes=64)
        wb_scales = once.tile([P, KV2], U8, align_bytes=64)

        wb_even = once.tile([P, 2, KV_RANK], BF16)
        wb_grouped = once.tile([P, KV2, 4], BF16, align_bytes=64)
        wb0_col = once.tile([P, 2], F32)

        def align_wkv_b():
            nc.vector.tensor_copy(out=wb_even[:], in_=wb_full[:, :, 1 : KV_RANK + 1])
            nc.vector.tensor_copy(out=wb0_col[:], in_=wb_full[:, :, 0])

        def flip_wkv_b():
            wb_words = wb_even[:].bitcast(F32).rearrange("r o (q u) -> r o u q", u=2)
            wb_flipped = psum_flip.tile([P, 4, P], F32, tag="flip")
            for o in range(2):
                for u in range(2):
                    nc.tensor.transpose(wb_flipped[:, 2 * o + u, :], wb_words[:, o, u, :], ident[:])
            nc.scalar.copy(
                out=wb_grouped[:].bitcast(F32).rearrange("q (o r) u -> q o r u", o=2),
                in_=wb_flipped[:].rearrange("q (o u) r -> q o r u", u=2),
            )

        def quantise_wkv_b():
            nc.vector.quantize_mx(
                out=wb_codes[:].bitcast(FP8X4), scales=wb_scales[:], in_=wb_grouped[:].rearrange("q c j -> q (c j)")
            )

        second_banks = []

        def second_vector_products():
            bank = psum_kv2.tile([P, 2, KV2], F32, tag="kv2")
            nc.tensor.matmul(out=bank[:, 0, :], lhsT=ones_bf[:], rhs=vec_rows[:], start=True, stop=True)
            for o in range(2):
                nc.tensor.transpose(
                    bank[:, 1, o * P : (o + 1) * P], wb0_col[:, o : o + 1].to_broadcast([P, P]), ident[:]
                )
            second_banks.append(bank)

        def second_vector_copies():
            nc.vector.tensor_copy(out=second_vectors[:], in_=second_banks[0][:])

        squares = {}
        squares_rest = {}
        kv_w = {}
        kv_y = {}

        def kv_product(g, t):
            y = psum_y.tile([P, GROUP], F32, tag="y")
            for a in range(PASSES):
                nc.tensor.matmul_mx(
                    out=y[:],
                    lhsT=wa_kv_codes[:, a, t * P : (t + 1) * P].bitcast(FP8X4),
                    lhsT_scale=wa_kv_scales[:, a, t * P : (t + 1) * P],
                    rhs=x_codes[g][:, a, :].bitcast(FP8X4),
                    rhs_scale=x_scales[g][:, a, :],
                    start=(a == 0),
                    stop=(a == PASSES - 1),
                )
            kv_y[g, t] = y

        def kv_square(g, t):
            if t == 0:
                sq_new = twice.tile([P, SUB, GROUP], F32, tag="sq")
                squares[g] = sq_new
            nc.scalar.activation(
                out=squares[g][:, t, :], in_=kv_y[g, t][:], func=ACT.Square, bias=b32[:, t : t + 1], scale=1.0
            )

        def kv_weighted(g, t, on_vector):
            if t == 0:
                kw_new = three.tile([P, SUB, GROUP], F32, tag="kw")
                kv_w[g] = kw_new
            if on_vector:
                nc.vector.tensor_scalar(
                    out=kv_w[g][:, t, :],
                    in0=kv_y[g, t][:],
                    scalar1=w32[:, t : t + 1],
                    scalar2=bw32[:, t : t + 1],
                    op0=ALU.mult,
                    op1=ALU.add,
                )
            else:
                nc.scalar.activation(
                    out=kv_w[g][:, t, :],
                    in_=kv_y[g, t][:],
                    func=ACT.Identity,
                    bias=bw32[:, t : t + 1],
                    scale=w32[:, t : t + 1],
                )

        def upper_halves(tile_f32):
            return tile_f32[:].bitcast(BF16).rearrange("p t (c h) -> p t c h", h=2)[:, :, :, 1]

        def square_rest(g, t, engine):
            if t == 0:
                rest_new = twice.tile([P, SUB, GROUP], BF16, tag="sq_rest")
                squares_rest[g] = rest_new
            engine.tensor_tensor(
                out=squares_rest[g][:, t, :],
                in0=squares[g][:, t, :],
                in1=upper_halves(squares[g])[:, t, :],
                op=ALU.subtract,
            )

        rope_parts = {}
        rope_banks = {}

        def rope_product(g):
            bank = psum_rope.tile([P, GROUP], F32, tag="rope")
            for a in range(PASSES):
                nc.tensor.matmul_mx(
                    out=bank[:],
                    lhsT=wa_pe_codes[:, a, :].bitcast(FP8X4),
                    lhsT_scale=wa_pe_scales[:, a, :],
                    rhs=x_codes[g][:, a, :].bitcast(FP8X4),
                    rhs_scale=x_scales[g][:, a, :],
                    start=(a == 0),
                    stop=(a == PASSES - 1),
                )
            rope_banks[g] = bank

        def rope_multiply(g, part):
            result = twice.tile([P, GROUP], F32, tag="rope_part%d" % part)
            nc.vector.scalar_tensor_tensor(
                out=result[:],
                in0=rope_banks[g][:],
                scalar=bpe32[:, 0:1],
                in1=rope_tables[:, g % TABLE_HALVES, part, :, :].rearrange("p n r -> p (n r)"),
                op0=ALU.add,
                op1=ALU.mult,
            )
            rope_parts[g, part] = result

        kpe_banks = {}

        def rope_turn(g):
            bank = psum_rope.tile([P, SUB, ROPE], F32, tag="rope")
            for n in range(SUB):
                for part in range(2):
                    nc.tensor.matmul(
                        out=bank[:, n, :],
                        lhsT=rope_parts[g, part][:, n * P : (n + 1) * P],
                        rhs=(pair_own, pair_swap)[part][:],
                        start=(part == 0),
                        stop=(part == 1),
                        is_transpose=True,
                    )
            kpe_banks[g] = bank

        def rope_rows(g):
            ksl_new = three.tile([P, SUB, HEADS, K_ROW], F32, tag="ksl")
            ksl_sb[g] = ksl_new
            nc.scalar.copy(
                out=ksl_new[:, :, :, 1 + NOPE : K_ROW],
                in_=kpe_banks[g][:].unsqueeze(2).to_broadcast([P, SUB, HEADS, ROPE]),
            )

        norm_sums = {}
        rstd = {}
        kw_sums = {}
        time_sp = {}

        def feature_sums(g, n):
            if n == 0:
                sums_new = psum_norm.tile([P, SUB, 4], F32, tag="norm")
                norm_sums[g] = sums_new
            upper = upper_halves(squares[g])
            for t in range(SUB):
                nc.tensor.matmul(
                    out=norm_sums[g][:, n, :],
                    lhsT=upper[:, t, n * P : (n + 1) * P],
                    rhs=sum_cols[:, t, :],
                    start=(t == 0),
                    stop=False,
                )
                nc.tensor.matmul(
                    out=norm_sums[g][:, n, :],
                    lhsT=squares_rest[g][:, t, n * P : (n + 1) * P],
                    rhs=sum_cols[:, t, :],
                    start=False,
                    stop=(t == SUB - 1),
                )

        def norm_root(g):
            rms = three.tile([P, SUB], F32, tag="rms")
            nc.scalar.activation(out=rms[:], in_=norm_sums[g][:, :, 0], func=ACT.Sqrt, bias=EPS, scale=1.0 / KV_RANK)
            rs = three.tile([P, SUB], F32, tag="rs")
            nc.vector.reciprocal(out=rs[:], in_=rms[:])
            rstd[g] = rs
            kw_sq = three.tile([P, SUB], F32, tag="kw_sq")
            nc.vector.tensor_reduce(out=kw_sq[:], in_=norm_sums[g][:, :, 1:3], axis=AXIS.X, op=ALU.add)
            kw_sums[g] = kw_sq

        sp_squares = {}

        def time_square(g):
            inv_ms = three.tile([P, SUB], F32, tag="inv_ms")
            nc.scalar.activation(out=inv_ms[:], in_=rstd[g][:], func=ACT.Square)
            sp_sq = three.tile([P, SUB], F32, tag="sp_sq")
            nc.gpsimd.tensor_tensor(out=sp_sq[:], in0=kw_sums[g][:], in1=inv_ms[:], op=ALU.mult)
            sp_squares[g] = sp_sq

        def time_root(g):
            tm = three.tile([P, SUB], F32, tag="tm")
            nc.scalar.activation(out=tm[:], in_=sp_squares[g][:], func=ACT.Sqrt, bias=1.0, scale=1.0)
            time_sp[g] = tm

        sp_rows = {}
        sp_codes = {}
        sp_scales = {}
        spread_of = {}

        def spread_rstd(g):
            spread = psum_norm.tile([P, GROUP], F32, tag="norm")
            for n in range(SUB):
                nc.tensor.transpose(
                    spread[:, n * P : (n + 1) * P], rstd[g][:, n : n + 1].to_broadcast([P, P]), ident[:]
                )
            spread_of[g] = spread

        def norm(g, places):
            if places.start == 0:
                rows_new = once.tile([P, GROUP, SUB], BF16, tag="sp_grouped", align_bytes=64)
                sp_rows[g] = rows_new
            cols = slice(places.start * P, places.stop * P)
            quads = (cols.stop - cols.start) // 4
            nc.vector.tensor_tensor(
                out=sp_rows[g][:, cols, :].rearrange("p (c i) t -> p c t i", i=4),
                in0=kv_w[g][:, :, cols].rearrange("p t (c i) -> p c t i", i=4),
                in1=spread_of[g][:, cols]
                .rearrange("p (c i) -> p c i", i=4)
                .unsqueeze(2)
                .to_broadcast([P, quads, SUB, 4]),
                op=ALU.mult,
            )

        def quantise_sp(g, places):
            if places.start == 0:
                codes_new = twice.tile([P, GROUP], U32, tag="sp_codes", align_bytes=64)
                scales_new = twice.tile([P, GROUP], U8, tag="sp_scales", align_bytes=64)
                sp_codes[g] = codes_new
                sp_scales[g] = scales_new
            cols = slice(places.start * P, places.stop * P)
            nc.vector.quantize_mx(
                out=sp_codes[g][:, cols].bitcast(FP8X4),
                scales=sp_scales[g][:, cols],
                in_=sp_rows[g][:, cols, :].rearrange("p c t -> p (c t)"),
            )

        ksl_sb = {}
        vs_sb = {}
        kv2_sb = {}
        kv2_banks = {}

        def second_product(g, pair):
            bank = psum_kv2.tile([P, 2, KV2], F32, tag="kv2")
            for i in range(2):
                n = 2 * pair + i
                nc.tensor.matmul_mx(
                    out=bank[:, i, :],
                    lhsT=sp_codes[g][:, n * P : (n + 1) * P].bitcast(FP8X4),
                    lhsT_scale=sp_scales[g][:, n * P : (n + 1) * P],
                    rhs=wb_codes[:].bitcast(FP8X4),
                    rhs_scale=wb_scales[:],
                    start=True,
                    stop=True,
                )
            kv2_banks[g, pair] = bank

        def add_time_term(g, pair):
            if pair == 0:
                kv2_new = twice.tile([P, SUB, HEADS, NOPE + V_DIM], F32, tag="kv2_rows")
                kv2_sb[g] = kv2_new
            for i in range(2):
                n = 2 * pair + i
                nc.vector.scalar_tensor_tensor(
                    out=kv2_sb[g][:, n, :, :].rearrange("p h c -> p (h c)"),
                    in0=wb0_all,
                    scalar=time_sp[g][:, n : n + 1],
                    in1=kv2_banks[g, pair][:, i, :],
                    op0=ALU.mult,
                    op1=ALU.add,
                )

        def second_bias(places):
            rows = bb_all.rearrange("p (h c) -> p h c", h=HEADS).unsqueeze(1)
            return rows.to_broadcast([P, places.stop - places.start, HEADS, NOPE + V_DIM])

        def bias_k(g, places, engine):
            engine.tensor_tensor(
                out=ksl_sb[g][:, places, :, 1 : 1 + NOPE],
                in0=kv2_sb[g][:, places, :, 0:NOPE],
                in1=second_bias(places)[:, :, :, 0:NOPE],
                op=ALU.add,
            )

        def bias_v(g, places, engine):
            if places.start == 0:
                vs_new = three.tile([P, SUB, HEADS, V_ROW], F32, tag="vs")
                vs_sb[g] = vs_new
            engine.tensor_tensor(
                out=vs_sb[g][:, places, :, 1:V_ROW],
                in0=kv2_sb[g][:, places, :, NOPE : NOPE + V_DIM],
                in1=second_bias(places)[:, :, :, NOPE : NOPE + V_DIM],
                op=ALU.add,
            )

        k_stats = {}
        v_sums = {}
        k_sums = {}

        def lift_k(g, n):
            if n == 0:
                stats_new = twice.tile([P, SUB, 4, 3], F32, tag="stats")
                k_stats[g] = stats_new
            row = ksl_sb[g][:, n, :, :].rearrange("p h f -> p (h f)")
            first = row[:, 1 : 1 + 2 * NOPE].rearrange("p (u c) -> p c u", u=2)
            start = 1 + 2 * NOPE
            second = row[:, start : start + 2 * (NOPE + 1)].rearrange("p (u c) -> p u c", u=2)[:, :, 0:NOPE]
            for k, runs in enumerate((first, second.rearrange("p u c -> p c u"))):
                nc.vector.bn_stats(
                    out=k_stats[g][:, n, 2 * k : 2 * k + 2, :].rearrange("p u s -> p (u s)"), in_=runs
                )

        def sum_squares(out, in_):
            junk = twice.tile([P, K_ROW], BF16, tag="junk")
            nc.scalar.activation(out=junk[:, 0 : in_.shape[1]], in_=in_, func=ACT.Square, accum_out=out)

        def lift_rows(g, n):
            if n == 0:
                sums_new = twice.tile([P, SUB, HEADS], F32, tag="k_sum")
                k_sums[g] = sums_new
            for h in range(HEADS):
                sum_squares(k_sums[g][:, n, h : h + 1], ksl_sb[g][:, n, h, 1:K_ROW])

        def lift_v(g, n):
            if n == 0:
                v_new = twice.tile([P, SUB, HEADS], F32, tag="v_sums")
                v_sums[g] = v_new
            for h in range(HEADS):
                sum_squares(v_sums[g][:, n, h : h + 1], vs_sb[g][:, n, h, 1:V_ROW])

        def lift_combine(g):
            stats = k_stats[g]
            nc.scalar.activation(out=stats[:, :, :, 0], in_=stats[:, :, :, 1], func=ACT.Square, scale=8.0)
            k_sum = twice.tile([P, SUB, HEADS], F32, tag="k_sum")
            for h in range(HEADS):
                nc.vector.tensor_reduce(
                    out=k_sum[:, :, h], in_=stats[:, :, h : h + 3, 0::2], axis=AXIS.XY, op=ALU.add
                )
            k_sums[g] = k_sum

        def finish_k(g):
            nc.scalar.activation(out=ksl_sb[g][:, :, :, 0], in_=k_sums[g][:], func=ACT.Sqrt, bias=1.0, scale=1.0)
            nc.sync.dma_start(out=ksl_groups[g], in_=ksl_sb[g][:].rearrange("p n h f -> p (n h f)"))

        def finish_v(g):
            nc.scalar.activation(out=vs_sb[g][:, :, :, 0], in_=v_sums[g][:], func=ACT.Sqrt, bias=1.0, scale=1.0)
            nc.sync.dma_start(out=vs_groups[g], in_=vs_sb[g][:].rearrange("p n h f -> p (n h f)"))

        ALL = slice(0, SUB)

        def do(stage, g, *args):
            if 0 <= g < GROUPS:
                stage(g, *args)

        with tc.manual_schedule():
            keep_warm(3, psum_kv2, "kv2")
            flip_x(0, 0)
            flip_x(0, 1, nc.vector.tensor_copy)
            quantise_place(0, 0)
            flip_x(0, 2, nc.scalar.copy, psum_rope, "rope")
            flip_x(0, 3, nc.vector.tensor_copy, psum_rope, "rope")
            keep_warm(1, psum_kv2, "kv2")
            flip_wa(0, nc.scalar.copy, psum_y, "y")
            quantise_place(0, 1)
            quantise_place(0, 2)
            quantise_place(0, 3)
            quantise_wa(0)
            feature_constants()
            flip_wa(1, nc.scalar.copy)
            flip_wa_rope()
            kv_product(0, 0)
            kv_square(0, 0)
            quantise_wa(1)
            sum_constants()
            load_x(4)
            align_wkv_b()
            twin_table(0)
            twin_table(1)
            flip_wa(2, nc.scalar.copy)
            flip_wa(3, nc.scalar.copy)
            kv_product(0, 1)
            kv_square(0, 1)
            second_vector_products()
            flip_x(1, 0)
            flip_x(1, 1)
            quantise_wa(2)
            kv_weighted(0, 0, True)
            kv_product(0, 2)
            kv_square(0, 2)
            flip_wkv_b()
            flip_x(1, 2)
            square_rest(0, 0, nc.gpsimd)
            turn_tables(0, psum_rope, "rope")
            quantise_wa(3)
            quantise_wa_rope()
            kv_weighted(0, 1, True)
            kv_product(0, 3)
            kv_square(0, 3)
            square_rest(0, 1, nc.vector)
            square_rest(0, 2, nc.gpsimd)
            kv_weighted(0, 2, True)
            flip_x(1, 3)
            square_rest(0, 3, nc.vector)
            flip_x(2, 0)
            rope_product(0)
            feature_sums(0, 0)
            quantise_x(1)
            flip_x(2, 1)
            feature_sums(0, 1)
            pair_constants()
            kv_product(1, 0)
            kv_weighted(0, 3, True)
            second_vector_copies()
            kv_square(1, 0)
            rope_multiply(0, 0)
            feature_sums(0, 2)
            kv_weighted(1, 0, False)
            feature_sums(0, 3)
            rope_multiply(0, 1)
            kv_product(1, 1)
            norm_root(0)
            square_rest(1, 0, nc.gpsimd)
            time_square(0)
            kv_square(1, 1)
            flip_x(2, 2)
            flip_x(2, 3, nc.vector.tensor_copy)
            spread_rstd(0)
            quantise_wkv_b()
            kv_weighted(1, 1, False)
            kv_product(1, 2)
            rope_turn(0)
            kv_square(1, 2)
            flip_x(3, 0)
            flip_x(3, 1)
            quantise_x(2)
            kv_weighted(1, 2, True)
            kv_product(1, 3)
            rope_product(1)
            square_rest(1, 1, nc.gpsimd)
            square_rest(1, 2, nc.gpsimd)
            norm(0, ALL)
            kv_square(1, 3)
            time_root(0)
            flip_x(3, 2)
            kv_weighted(1, 3, True)
            flip_x(3, 3)
            quantise_sp(0, ALL)
            square_rest(1, 3, nc.gpsimd)
            turn_tables(1, psum_kv2, "kv2")
            for i in range(2, GROUPS):
                do(load_x, i + 3)
                do(rope_multiply, i - 1, 0)
                do(kv_product, i, 0)
                do(bias_v, i - 3, ALL, nc.gpsimd)
                do(rope_rows, i - 2)
                do(lift_k, i - 3, 0)
                do(lift_k, i - 3, 1)
                do(feature_sums, i - 1, 0)
                do(feature_sums, i - 1, 1)
                do(lift_k, i - 3, 2)
                do(kv_product, i, 1)
                do(kv_square, i, 0)
                do(kv_weighted, i, 0, False)
                do(second_product, i - 2, 0)
                do(quantise_x, i + 1)
                do(feature_sums, i - 1, 2)
                do(lift_k, i - 3, 3)
                do(add_time_term, i - 2, 0)
                do(rope_multiply, i - 1, 1)
                do(lift_combine, i - 3)
                do(kv_square, i, 1)
                do(square_rest, i, 0, nc.gpsimd)
                do(feature_sums, i - 1, 3)
                do(norm_root, i - 1)
                do(kv_weighted, i, 1, True)
                do(lift_v, i - 3, 0)
                do(square_rest, i, 1, nc.gpsimd)
                do(kv_product, i, 2)
                do(kv_square, i, 2)
                do(second_product, i - 2, 1)
                do(lift_v, i - 3, 1)
                do(finish_k, i - 3)
                do(square_rest, i, 2, nc.gpsimd)
                do(flip_x, i + 2, 0)
                do(lift_v, i - 3, 2)
                do(spread_rstd, i - 1)
                do(kv_product, i, 3)
                do(kv_square, i, 3)
                do(lift_v, i - 3, 3)
                do(add_time_term, i - 2, 1)
                do(bias_k, i - 2, ALL, nc.gpsimd)
                do(flip_x, i + 2, 1)
                do(kv_weighted, i, 2, False)
                do(norm, i - 1, ALL)
                do(kv_weighted, i, 3, False)
                do(time_square, i - 1)
                do(rope_turn, i - 1)
                do(flip_x, i + 2, 2)
                do(square_rest, i, 3, nc.vector)
                do(quantise_sp, i - 1, ALL)
                do(rope_product, i)
                do(flip_x, i + 2, 3)
                do(finish_v, i - 3)
                do(time_root, i - 1)
            last = GROUPS - 1
            rope_multiply(last, 0)
            bias_v(last - 2, ALL, nc.gpsimd)
            feature_sums(last, 0)
            lift_rows(last - 2, 0)
            feature_sums(last, 1)
            lift_rows(last - 2, 1)
            keep_warm(1, psum_y, "y")
            lift_v(last - 2, 0)
            second_product(last - 1, 0)
            lift_v(last - 2, 1)
            feature_sums(last, 2)
            add_time_term(last - 1, 0)
            rope_multiply(last, 1)
            feature_sums(last, 3)
            norm_root(last)
            second_product(last - 1, 1)
            add_time_term(last - 1, 1)
            lift_rows(last - 2, 2)
            rope_rows(last - 1)
            spread_rstd(last)
            lift_rows(last - 2, 3)
            finish_k(last - 2)
            norm(last, slice(0, 2))
            rope_turn(last)
            bias_k(last - 1, ALL, nc.gpsimd)
            quantise_sp(last, slice(0, 2))
            lift_rows(last - 1, 0)
            lift_rows(last - 1, 1)
            lift_rows(last - 1, 2)
            time_square(last)
            time_root(last)
            second_product(last, 0)
            norm(last, slice(2, 4))
            lift_rows(last - 1, 3)
            finish_k(last - 1)
            lift_v(last - 2, 2)
            lift_v(last - 2, 3)
            finish_v(last - 2)
            add_time_term(last, 0)
            bias_v(last - 1, ALL, nc.gpsimd)
            rope_rows(last)
            lift_v(last - 1, 0)
            lift_v(last - 1, 1)
            lift_v(last - 1, 2)
            quantise_sp(last, slice(2, 4))
            second_product(last, 1)
            bias_k(last, slice(0, 2), nc.vector)
            add_time_term(last, 1)
            bias_k(last, slice(2, 4), nc.vector)
            lift_k(last, 0)
            lift_k(last, 1)
            bias_v(last, slice(0, 2), nc.gpsimd)
            lift_v(last - 1, 3)
            finish_v(last - 1)
            lift_v(last, 0)
            lift_v(last, 1)
            bias_v(last, slice(2, 4), nc.gpsimd)
            lift_v(last, 2)
            lift_v(last, 3)
            finish_v(last)
            lift_k(last, 2)
            lift_k(last, 3)
            lift_combine(last)
            finish_k(last)
